import numpy as np
import ml_dtypes


def mxq(x, axis, fmt="e4m3"):
    dtype, down = {"e4m3": (ml_dtypes.float8_e4m3fn, 7), "e5m2": (ml_dtypes.float8_e5m2, 14)}[fmt]
    v = np.moveaxis(np.asarray(x, np.float32).astype(ml_dtypes.bfloat16).astype(np.float64), axis, -1)
    blocks = v.reshape(v.shape[:-1] + (-1, 32))
    amax = np.abs(blocks).max(-1, keepdims=True)
    byte = np.maximum(np.where(amax > 0, np.frexp(amax)[1] - 1 + 127, 0) - down, 1)
    scale = np.exp2(byte - 127.0)
    codes = (blocks / scale).astype(np.float32).astype(dtype).astype(np.float64)
    return np.moveaxis((codes * scale).reshape(v.shape), -1, axis)


WIDE = False


def mx_kscale(k):
    if not WIDE:
        return np.ones(k)
    levels = np.array([10, -10, 5, -5, 0])
    a = np.random.permutation(np.resize(levels, k // 512 * 4)).reshape(k // 512, 4)
    idx = np.arange(k)
    return np.exp2(a[idx // 512, idx % 128 // 32])


BF16 = ml_dtypes.bfloat16


def bf(x):
    return np.asarray(x, np.float32).astype(BF16)


def f64(x):
    return np.asarray(x).astype(np.float64)


B, T, HID, QH, KVH, D, W = 1, 4096, 1024, 4, 1, 128, 512
R = QH // KVH
NB = T // W


def setup_inputs():
    s = mx_kscale(HID)
    return {"q_rot": bf(np.random.standard_normal((B, T, QH, D)) * 1.5),
            "k_rot": bf(np.random.standard_normal((B, T, KVH, D)) * 1.5),
            "x": bf(np.random.standard_normal((B, T, HID)) * s),
            "wv": bf(np.random.standard_normal((KVH * D, HID)) * 2.0 / np.sqrt(HID) / s)}


def reference(q_rot, k_rot, x, wv):
    v = (mxq(f64(x), 2, "e4m3") @ mxq(f64(wv), 1, "e4m3").T).reshape(B, T, KVH, D)
    vq = mxq(v, 1, "e4m3").transpose(0, 2, 1, 3)
    qg = f64(q_rot).reshape(B, T, KVH, R, D).transpose(0, 2, 3, 1, 4)
    kt = f64(k_rot).transpose(0, 2, 3, 1)
    outs = []
    for i in range(NB):
        lo, t0, t1 = max(i - 1, 0) * W, i * W, (i + 1) * W
        sc = qg[:, :, :, t0:t1].reshape(B, KVH, R * W, D) @ kt[:, :, :, lo:t1] / np.sqrt(D)
        dist = np.arange(t0, t1)[:, None] - np.arange(lo, t1)[None, :]
        allowed = np.tile((dist >= 0) & (dist <= W), (R, 1))
        sc = np.where(allowed, sc, -np.inf)
        e = np.exp(sc - sc.max(-1, keepdims=True))
        o = (mxq(e, 3, "e4m3") @ vq[:, :, lo:t1]) / e.sum(-1, keepdims=True)
        outs.append(o.reshape(B, KVH, R, W, D).transpose(0, 3, 1, 2, 4))
    return np.concatenate(outs, axis=1).reshape(B, T, QH * D)

@@ -1,0 +1,334 @@
+import math
+
+import concourse.mybir as mybir
+from concourse.masks import make_identity
+
+F32 = mybir.dt.float32
+BF16 = mybir.dt.bfloat16
+I32 = mybir.dt.int32
+U32 = mybir.dt.uint32
+U8 = mybir.dt.uint8
+FP8X4 = mybir.dt.float8_e4m3fn_x4
+ALU = mybir.AluOpType
+ACT = mybir.ActivationFunctionType
+AX = mybir.AxisListType
+
+P = 128
+T = 4096
+HID = 1024
+HEADS = 4
+D = 128
+BLOCK = 512
+TILES = BLOCK // P
+N_BLOCKS = T // BLOCK
+HALF = 256
+GROUPED_BUFS = 3
+EARLY_FLIPS = 2
+MASKED = -1.0e30
+
+FLOPS = 2 * T * HID * D + 2 * 2 * HEADS * D * BLOCK * (2 * BLOCK * (N_BLOCKS - 1) + BLOCK)
+
+
+def tile_localgqattention_pb_t_kernel(tc, q_rot, k_rot, x, wv, out):
+    nc = tc.nc
+    scale = 1.0 / math.sqrt(D)
+
+    q_rows = q_rot.rearrange("b t h d -> (b t) (h d)")
+    k_rows = k_rot.rearrange("b t h d -> (b t) (h d)")
+    x_rows = x.flatten_outer_dims()
+    out_rows = out.flatten_outer_dims()
+
+    with (
+        tc.tile_pool(name="keep", bufs=1) as keep,
+        tc.tile_pool(name="queries", bufs=3) as queries,
+        tc.tile_pool(name="e_pack", bufs=8) as e_pack,
+        tc.tile_pool(name="x_pack", bufs=4) as x_pack,
+        tc.tile_pool(name="stats", bufs=4) as stats,
+        tc.tile_pool(name="results", bufs=4) as results,
+        tc.psum_pool(name="scores", bufs=5) as scores,
+        tc.psum_pool(name="work", bufs=3) as work,
+    ):
+        k_in, q_in, x_in = [], [], []
+        wv_in = keep.tile([P, HID], BF16, name="wv_in")
+        for b in range(N_BLOCKS):
+            rows = slice(b * BLOCK, (b + 1) * BLOCK)
+            k_in.append(keep.tile([P, TILES, D], BF16, name="k_in%d" % b))
+            q_in.append(keep.tile([P, TILES, HEADS * D], BF16, name="q_in%d" % b))
+            x_in.append(keep.tile([P, 4, HID], BF16, name="x_in%d" % b))
+            nc.sync.dma_start(out=k_in[b][:], in_=k_rows[rows, :].rearrange("(c p) d -> p c d", p=P))
+            nc.sync.dma_start(out=q_in[b][:], in_=q_rows[rows, :].rearrange("(c p) f -> p c f", p=P))
+            if b == 0:
+                nc.sync.dma_start(out=wv_in[:], in_=wv)
+            nc.sync.dma_start(
+                out=x_in[b][:].rearrange("p (u e) f -> p u e f", u=2),
+                in_=x_rows[rows, :].rearrange("(u p e) f -> p u e f", u=2, e=2),
+            )
+
+        ident_f32 = keep.tile([P, P], F32, name="ident_f32")
+        make_identity(nc, ident_f32[:])
+        ident_bf = keep.tile([P, P], BF16, name="ident_bf")
+        make_identity(nc, ident_bf[:])
+
+        own_f32 = keep.tile([P, P], F32, name="own_f32")
+        nc.gpsimd.memset(own_f32[:], 0.0)
+        nc.gpsimd.affine_select(
+            out=own_f32[:], in_=own_f32[:], compare_op=ALU.is_ge, fill=MASKED,
+            base=0, pattern=[[-1, P]], channel_multiplier=1,
+        )
+        far_f32 = keep.tile([P, P], F32, name="far_f32")
+        nc.gpsimd.memset(far_f32[:], 0.0)
+        nc.gpsimd.affine_select(
+            out=far_f32[:], in_=far_f32[:], compare_op=ALU.is_ge, fill=MASKED,
+            base=0, pattern=[[1, P]], channel_multiplier=-1,
+        )
+        own_mask = keep.tile([P, HEADS, P], BF16, name="own_mask")
+        for h in range(HEADS):
+            nc.vector.tensor_copy(out=own_mask[:, h, :], in_=own_f32[:])
+        far_mask = keep.tile([P, P], BF16, name="far_mask")
+        nc.vector.tensor_copy(out=far_mask[:], in_=far_f32[:])
+
+        e_rows = []
+        for c in range(TILES):
+            e_rows.append([])
+            for h in range(HEADS):
+                e_tile = keep.tile([P, 2 * BLOCK], BF16, name="e_rows%d_%d" % (c, h))
+                nc.vector.memset(e_tile[:].bitcast(I32), 0)
+                e_rows[c].append(e_tile)
+
+        keys_t = keep.tile([P, T], BF16, name="keys_t")
+        v_codes = keep.tile([P, N_BLOCKS, D], U32, name="v_codes", align_bytes=64)
+        v_scales = keep.tile([P, N_BLOCKS, D], U8, name="v_scales", align_bytes=64)
+
+        def flip_rows(rows_bf16, n_pass):
+            words = rows_bf16.bitcast(F32)
+            flipped = work.tile([P, 2 * n_pass, P], F32, name="flipped", tag="work")
+            for j in range(2 * n_pass):
+                nc.tensor.transpose(flipped[:, j, :], words[:, j * P : (j + 1) * P], ident_f32[:])
+            return flipped
+
+        def group_words(flipped, n_pass, pool):
+            grouped = pool.tile([P, n_pass * BLOCK], BF16, name="grouped", tag="grouped", bufs=GROUPED_BUFS,
+                                align_bytes=64)
+            nc.scalar.copy(
+                out=grouped[:].bitcast(F32).rearrange("p (g r u) -> p g r u", g=n_pass, u=2),
+                in_=flipped[:].rearrange("p (g u) r -> p g r u", u=2),
+            )
+            return grouped
+
+        def quantise(grouped, n_pass, pool):
+            codes = pool.tile([P, n_pass * P], U32, name="codes", tag="codes", align_bytes=64)
+            planes = pool.tile([P, n_pass * P], U8, name="planes", tag="planes", align_bytes=64)
+            nc.vector.quantize_mx(out=codes[:].bitcast(FP8X4), scales=planes[:], in_=grouped[:])
+            return codes, planes
+
+        hid_passes = HID // BLOCK
+        queries_t = {}
+        x_packed = {}
+
+        def prepare_keys(b):
+            k_flip = work.tile([P, TILES, P], BF16, name="k_flip", tag="work")
+            for c in range(TILES):
+                nc.tensor.transpose(k_flip[:, c, :], k_in[b][:, c, :], ident_bf[:])
+            nc.vector.tensor_copy(
+                out=keys_t[:, b * BLOCK : (b + 1) * BLOCK], in_=k_flip[:].rearrange("p c r -> p (c r)")
+            )
+
+        def prepare_queries(b):
+            q_t = queries.tile([P, HEADS, BLOCK], BF16, name="q_t", tag="q_t")
+            for pair in range(HEADS // 2):
+                q_flip = work.tile([P, 2, TILES, P], BF16, name="q_flip", tag="work")
+                for hh in range(2):
+                    h = 2 * pair + hh
+                    for c in range(TILES):
+                        nc.tensor.transpose(q_flip[:, hh, c, :], q_in[b][:, c, h * D : (h + 1) * D], ident_bf[:])
+                nc.vector.tensor_copy(
+                    out=q_t[:, 2 * pair : 2 * pair + 2, :].rearrange("p h r -> p (h r)"),
+                    in_=q_flip[:].rearrange("p h c r -> p (h c r)"),
+                )
+            queries_t[b] = q_t
+
+        def pack_x(b, slot):
+            flipped = flip_rows(x_in[b][:, slot, :], hid_passes)
+            grouped = group_words(flipped, hid_passes, x_pack)
+            x_packed[(b, slot)] = quantise(grouped, hid_passes, x_pack)
+
+        def project_values(b):
+            v_acc = work.tile([P, 4, D], F32, name="v_acc", tag="work")
+            for slot in range(4):
+                x_codes, x_scales = x_packed[(b, slot)]
+                for g in range(hid_passes):
+                    cols = slice(g * P, (g + 1) * P)
+                    nc.tensor.matmul_mx(
+                        out=v_acc[:, slot, :],
+                        lhsT=x_codes[:, cols].bitcast(FP8X4), lhsT_scale=x_scales[:, cols],
+                        rhs=wv_codes[:, cols].bitcast(FP8X4), rhs_scale=wv_scales[:, cols],
+                        start=(g == 0), stop=(g == hid_passes - 1),
+                    )
+            v_grouped = x_pack.tile([P, D, 4], BF16, name="v_grouped", tag="v_grouped", bufs=2, align_bytes=64)
+            nc.vector.tensor_copy(out=v_grouped[:], in_=v_acc[:].rearrange("p s d -> p d s"))
+            nc.vector.quantize_mx(
+                out=v_codes[:, b, :].bitcast(FP8X4), scales=v_scales[:, b, :],
+                in_=v_grouped[:].rearrange("p d s -> p (d s)"),
+            )
+
+        live = {}
+
+        def n_old(tau):
+            return min(tau, TILES)
+
+        def scores_own(tau):
+            b, c = divmod(tau, TILES)
+            live[tau] = {"s_old": [], "flipped": [], "packed": []}
+            s_own = scores.tile([P, HEADS, P], F32, name="s_own", tag="scores")
+            nc.tensor.matmul(
+                s_own[:].rearrange("p h r -> p (h r)"), lhsT=ident_bf[:],
+                rhs=own_mask[:].rearrange("p h r -> p (h r)"), start=True, stop=False,
+            )
+            for h in range(HEADS):
+                nc.tensor.matmul(
+                    s_own[:, h, :], lhsT=queries_t[b][:, h, c * P : (c + 1) * P],
+                    rhs=keys_t[:, tau * P : (tau + 1) * P], start=False, stop=(h == HEADS - 1),
+                )
+            top_own = stats.tile([P, HEADS], F32, name="top_own", tag="top_own")
+            nc.vector.reduce_max(out=top_own[:], in_=s_own[:], axis=AX.X)
+            live[tau]["s_own"] = s_own
+            live[tau]["top_own"] = top_own
+            if n_old(tau):
+                live[tau]["top_old"] = stats.tile([P, HEADS], F32, name="top_old", tag="top_old")
+
+        def scores_old(tau, h):
+            b, c = divmod(tau, TILES)
+            cols = n_old(tau) * P
+            s_h = scores.tile([P, BLOCK], F32, name="s_old", tag="scores")
+            nc.tensor.matmul(
+                s_h[:, :cols], lhsT=queries_t[b][:, h, c * P : (c + 1) * P],
+                rhs=keys_t[:, tau * P - cols : tau * P], start=True, stop=(tau < TILES),
+            )
+            if tau >= TILES:
+                nc.tensor.matmul(s_h[:, :P], lhsT=ident_bf[:], rhs=far_mask[:], start=False, stop=True)
+            nc.vector.reduce_max(out=live[tau]["top_old"][:, h : h + 1], in_=s_h[:, :cols], axis=AX.X)
+            live[tau]["s_old"].append(s_h)
+
+        def make_bias(tau):
+            top = live[tau]["top_own"]
+            if n_old(tau):
+                top = stats.tile([P, HEADS], F32, name="top", tag="top")
+                nc.vector.tensor_max(out=top[:], in0=live[tau]["top_own"][:], in1=live[tau]["top_old"][:])
+            bias = stats.tile([P, HEADS], F32, name="bias", tag="bias")
+            nc.vector.tensor_scalar_mul(out=bias[:], in0=top[:], scalar1=-scale)
+            live[tau]["bias"] = bias
+
+        def exp_own(tau):
+            c = tau % TILES
+            own_col = BLOCK + c * P
+            sum_own = stats.tile([P, HEADS], F32, name="sum_own", tag="sum_own")
+            for h in range(HEADS):
+                nc.scalar.activation(
+                    out=e_rows[c][h][:, own_col : own_col + P], in_=live[tau]["s_own"][:, h, :], func=ACT.Exp,
+                    bias=live[tau]["bias"][:, h : h + 1], scale=scale, accum_out=sum_own[:, h : h + 1],
+                )
+            live[tau]["sum_own"] = sum_own
+            if n_old(tau):
+                live[tau]["sum_old"] = stats.tile([P, HEADS], F32, name="sum_old", tag="sum_old")
+
+        def exp_old(tau, h):
+            c = tau % TILES
+            own_col = BLOCK + c * P
+            cols = n_old(tau) * P
+            nc.scalar.activation(
+                out=e_rows[c][h][:, own_col - cols : own_col], in_=live[tau]["s_old"][h][:, :cols], func=ACT.Exp,
+                bias=live[tau]["bias"][:, h : h + 1], scale=scale, accum_out=live[tau]["sum_old"][:, h : h + 1],
+            )
+
+        def value_blocks(tau):
+            b = tau // TILES
+            return [b - 1, b] if b > 0 else [b]
+
+        def flip_e(tau, h):
+            n_pass = len(value_blocks(tau))
+            live[tau]["flipped"].append(flip_rows(e_rows[tau % TILES][h][:, (2 - n_pass) * BLOCK :], n_pass))
+
+        def pack_e(tau, h):
+            n_pass = len(value_blocks(tau))
+            grouped = group_words(live[tau]["flipped"][h], n_pass, e_pack)
+            live[tau]["packed"].append(quantise(grouped, n_pass, e_pack))
+
+        def multiply_values(tau):
+            blocks = value_blocks(tau)
+            o_acc = work.tile([P, HEADS, D], F32, name="o_acc", tag="work")
+            for h in range(HEADS):
+                e_codes, e_scales = live[tau]["packed"][h]
+                for g, vb in enumerate(blocks):
+                    cols = slice(g * P, (g + 1) * P)
+                    nc.tensor.matmul_mx(
+                        out=o_acc[:, h, :],
+                        lhsT=e_codes[:, cols].bitcast(FP8X4), lhsT_scale=e_scales[:, cols],
+                        rhs=v_codes[:, vb, :].bitcast(FP8X4), rhs_scale=v_scales[:, vb, :],
+                        start=(g == 0), stop=(g == len(blocks) - 1),
+                    )
+            live[tau]["o_acc"] = o_acc
+
+        def divide_and_store(tau):
+            total = live[tau]["sum_own"]
+            if n_old(tau):
+                total = stats.tile([P, HEADS], F32, name="total", tag="total")
+                nc.vector.tensor_add(out=total[:], in0=live[tau]["sum_own"][:], in1=live[tau]["sum_old"][:])
+            inverse = stats.tile([P, HEADS], F32, name="inverse", tag="inverse")
+            nc.vector.reciprocal(out=inverse[:], in_=total[:])
+            result = results.tile([P, HEADS, D], F32, name="result", tag="result")
+            nc.vector.tensor_tensor(
+                out=result[:], in0=live[tau]["o_acc"][:],
+                in1=inverse[:].unsqueeze(2).to_broadcast([P, HEADS, D]), op=ALU.mult,
+            )
+            nc.sync.dma_start(
+                out=out_rows[tau * P : (tau + 1) * P, :], in_=result[:].rearrange("p h d -> p (h d)")
+            )
+
+        def prepare_quarter(b, c):
+            if c < 2:
+                pack_x(b, 2 * c)
+                pack_x(b, 2 * c + 1)
+            elif c == 2:
+                prepare_keys(b)
+                prepare_queries(b)
+            else:
+                project_values(b)
+
+        n_tiles = T // P
+        with tc.manual_schedule():
+            prepare_keys(0)
+            prepare_queries(0)
+            scores_own(0)
+            make_bias(0)
+            wv_grouped = group_words(flip_rows(wv_in[:], hid_passes), hid_passes, keep)
+            wv_codes, wv_scales = quantise(wv_grouped, hid_passes, keep)
+            for slot in range(4):
+                pack_x(0, slot)
+            project_values(0)
+
+            for tau in range(n_tiles):
+                b, c = divmod(tau, TILES)
+                following = tau + 1 < n_tiles
+                exp_own(tau)
+                if following:
+                    scores_own(tau + 1)
+                if tau > 0:
+                    multiply_values(tau - 1)
+                    divide_and_store(tau - 1)
+                for h in range(HEADS):
+                    if n_old(tau):
+                        exp_old(tau, h)
+                    if following:
+                        scores_old(tau + 1, h)
+                    if h < EARLY_FLIPS:
+                        flip_e(tau, h)
+                if following:
+                    make_bias(tau + 1)
+                for h in range(HEADS):
+                    if h + EARLY_FLIPS < HEADS:
+                        flip_e(tau, h + EARLY_FLIPS)
+                    pack_e(tau, h)
+                if b + 1 < N_BLOCKS:
+                    prepare_quarter(b + 1, c)
+            multiply_values(n_tiles - 1)
+            divide_and_store(n_tiles - 1)

@@ -23,7 +23,7 @@ TILES = BLOCK // P
 N_BLOCKS = T // BLOCK
 HALF = 256
 GROUPED_BUFS = 3
-EARLY_FLIPS = 2
+AHEAD = 2
 MASKED = -1.0e30
 
 FLOPS = 2 * T * HID * D + 2 * 2 * HEADS * D * BLOCK * (2 * BLOCK * (N_BLOCKS - 1) + BLOCK)
@@ -45,8 +45,10 @@ def tile_localgqattention_pb_t_kernel(tc, q_rot, k_rot, x, wv, out):
         tc.tile_pool(name="x_pack", bufs=4) as x_pack,
         tc.tile_pool(name="stats", bufs=4) as stats,
         tc.tile_pool(name="results", bufs=4) as results,
-        tc.psum_pool(name="scores", bufs=5) as scores,
-        tc.psum_pool(name="work", bufs=3) as work,
+        tc.psum_pool(name="mids", bufs=3) as mids,
+        tc.psum_pool(name="edges", bufs=2) as edges,
+        tc.psum_pool(name="work", bufs=2) as work,
+        tc.psum_pool(name="sums", bufs=1) as sums,
     ):
         k_in, q_in, x_in = [], [], []
         wv_in = keep.tile([P, HID], BF16, name="wv_in")
@@ -81,11 +83,10 @@ def tile_localgqattention_pb_t_kernel(tc, q_rot, k_rot, x, wv, out):
             out=far_f32[:], in_=far_f32[:], compare_op=ALU.is_ge, fill=MASKED,
             base=0, pattern=[[1, P]], channel_multiplier=-1,
         )
-        own_mask = keep.tile([P, HEADS, P], BF16, name="own_mask")
-        for h in range(HEADS):
-            nc.vector.tensor_copy(out=own_mask[:, h, :], in_=own_f32[:])
-        far_mask = keep.tile([P, P], BF16, name="far_mask")
-        nc.vector.tensor_copy(out=far_mask[:], in_=far_f32[:])
+        edge_mask = keep.tile([P, 2, 2, P], BF16, name="edge_mask")
+        for hh in range(2):
+            nc.vector.tensor_copy(out=edge_mask[:, hh, 0, :], in_=far_f32[:])
+            nc.vector.tensor_copy(out=edge_mask[:, hh, 1, :], in_=own_f32[:])
 
         e_rows = []
         for c in range(TILES):
@@ -133,19 +134,18 @@ def tile_localgqattention_pb_t_kernel(tc, q_rot, k_rot, x, wv, out):
                 out=keys_t[:, b * BLOCK : (b + 1) * BLOCK], in_=k_flip[:].rearrange("p c r -> p (c r)")
             )
 
-        def prepare_queries(b):
-            q_t = queries.tile([P, HEADS, BLOCK], BF16, name="q_t", tag="q_t")
-            for pair in range(HEADS // 2):
-                q_flip = work.tile([P, 2, TILES, P], BF16, name="q_flip", tag="work")
-                for hh in range(2):
-                    h = 2 * pair + hh
-                    for c in range(TILES):
-                        nc.tensor.transpose(q_flip[:, hh, c, :], q_in[b][:, c, h * D : (h + 1) * D], ident_bf[:])
-                nc.vector.tensor_copy(
-                    out=q_t[:, 2 * pair : 2 * pair + 2, :].rearrange("p h r -> p (h r)"),
-                    in_=q_flip[:].rearrange("p h c r -> p (h c r)"),
-                )
-            queries_t[b] = q_t
+        def prepare_queries(b, pair):
+            if pair == 0:
+                queries_t[b] = queries.tile([P, HEADS, BLOCK], BF16, name="q_t", tag="q_t")
+            q_flip = work.tile([P, 2, TILES, P], BF16, name="q_flip", tag="work")
+            for hh in range(2):
+                h = 2 * pair + hh
+                for c in range(TILES):
+                    nc.tensor.transpose(q_flip[:, hh, c, :], q_in[b][:, c, h * D : (h + 1) * D], ident_bf[:])
+            nc.vector.tensor_copy(
+                out=queries_t[b][:, 2 * pair : 2 * pair + 2, :].rearrange("p h r -> p (h r)"),
+                in_=q_flip[:].rearrange("p h c r -> p (h c r)"),
+            )
 
         def pack_x(b, slot):
             flipped = flip_rows(x_in[b][:, slot, :], hid_passes)
@@ -171,73 +171,102 @@ def tile_localgqattention_pb_t_kernel(tc, q_rot, k_rot, x, wv, out):
                 in_=v_grouped[:].rearrange("p d s -> p (d s)"),
             )
 
-        live = {}
+        def prepare_eighth(b, j):
+            if j < 4:
+                pack_x(b, j)
+            elif j == 4:
+                prepare_keys(b)
+            elif j < 7:
+                prepare_queries(b, j - 5)
+            else:
+                project_values(b)
 
-        def n_old(tau):
-            return min(tau, TILES)
+        per_tile = {}
+        per_unit = {}
 
-        def scores_own(tau):
+        def n_mid(tau):
+            return min(tau, TILES - 1)
+
+        def has_far(tau):
+            return tau >= TILES
+
+        def query_cols(tau, h):
             b, c = divmod(tau, TILES)
-            live[tau] = {"s_old": [], "flipped": [], "packed": []}
-            s_own = scores.tile([P, HEADS, P], F32, name="s_own", tag="scores")
+            return queries_t[b][:, h, c * P : (c + 1) * P]
+
+        def edge_scores(tau, pair):
+            if pair == 0:
+                per_tile[tau] = {
+                    "sum_edge": stats.tile([P, HEADS], F32, name="sum_edge", tag="sum_edge"),
+                    "sum_mid": stats.tile([P, HEADS], F32, name="sum_mid", tag="sum_mid") if n_mid(tau) else None,
+                }
+            edge = edges.tile([P, 2, 2, P], F32, name="edge", tag="edge")
             nc.tensor.matmul(
-                s_own[:].rearrange("p h r -> p (h r)"), lhsT=ident_bf[:],
-                rhs=own_mask[:].rearrange("p h r -> p (h r)"), start=True, stop=False,
+                edge[:].rearrange("p h s r -> p (h s r)"), lhsT=ident_bf[:],
+                rhs=edge_mask[:].rearrange("p h s r -> p (h s r)"), start=True, stop=False,
             )
-            for h in range(HEADS):
-                nc.tensor.matmul(
-                    s_own[:, h, :], lhsT=queries_t[b][:, h, c * P : (c + 1) * P],
-                    rhs=keys_t[:, tau * P : (tau + 1) * P], start=False, stop=(h == HEADS - 1),
+            key_tiles = keys_t[:].rearrange("p (t r) -> p t r", r=P)
+            for hh in range(2):
+                if has_far(tau):
+                    nc.tensor.matmul(
+                        edge[:, hh, :, :], lhsT=query_cols(tau, 2 * pair + hh),
+                        rhs=key_tiles[:, tau - TILES : tau + 1 : TILES, :], start=False, stop=(hh == 1),
+                    )
+                else:
+                    nc.tensor.matmul(
+                        edge[:, hh, 1, :], lhsT=query_cols(tau, 2 * pair + hh),
+                        rhs=key_tiles[:, tau, :], start=False, stop=(hh == 1),
+                    )
+            top_edge = stats.tile([P, 2], F32, name="top_edge", tag="top_edge")
+            seen = edge[:].rearrange("p h s r -> p h (s r)") if has_far(tau) else edge[:, :, 1, :]
+            nc.vector.reduce_max(out=top_edge[:], in_=seen, axis=AX.X)
+            for hh in range(2):
+                per_unit[(tau, 2 * pair + hh)] = {"edge": edge[:, hh, :, :], "top_edge": top_edge[:, hh : hh + 1]}
+
+        def mid_scores(tau, h):
+            cols = n_mid(tau) * P
+            mid = mids.tile([P, (TILES - 1) * P], F32, name="mid", tag="mid")
+            nc.tensor.matmul(
+                mid[:, :cols], lhsT=query_cols(tau, h), rhs=keys_t[:, tau * P - cols : tau * P],
+                start=True, stop=True,
+            )
+            top_mid = stats.tile([P, 1], F32, name="top_mid", tag="top_mid")
+            nc.vector.reduce_max(out=top_mid[:], in_=mid[:, :cols], axis=AX.X)
+            per_unit[(tau, h)]["mid"] = mid
+            per_unit[(tau, h)]["top_mid"] = top_mid
+
+        def make_bias(tau, h):
+            unit = per_unit[(tau, h)]
+            bias = stats.tile([P, 1], F32, name="bias", tag="bias")
+            if n_mid(tau):
+                nc.vector.tensor_scalar(
+                    out=bias[:], in0=unit["top_mid"][:], scalar1=unit["top_edge"], scalar2=-scale,
+                    op0=ALU.max, op1=ALU.mult,
                 )
-            top_own = stats.tile([P, HEADS], F32, name="top_own", tag="top_own")
-            nc.vector.reduce_max(out=top_own[:], in_=s_own[:], axis=AX.X)
-            live[tau]["s_own"] = s_own
-            live[tau]["top_own"] = top_own
-            if n_old(tau):
-                live[tau]["top_old"] = stats.tile([P, HEADS], F32, name="top_old", tag="top_old")
+            else:
+                nc.vector.tensor_scalar_mul(out=bias[:], in0=unit["top_edge"], scalar1=-scale)
+            unit["bias"] = bias
 
-        def scores_old(tau, h):
-            b, c = divmod(tau, TILES)
-            cols = n_old(tau) * P
-            s_h = scores.tile([P, BLOCK], F32, name="s_old", tag="scores")
-            nc.tensor.matmul(
-                s_h[:, :cols], lhsT=queries_t[b][:, h, c * P : (c + 1) * P],
-                rhs=keys_t[:, tau * P - cols : tau * P], start=True, stop=(tau < TILES),
-            )
-            if tau >= TILES:
-                nc.tensor.matmul(s_h[:, :P], lhsT=ident_bf[:], rhs=far_mask[:], start=False, stop=True)
-            nc.vector.reduce_max(out=live[tau]["top_old"][:, h : h + 1], in_=s_h[:, :cols], axis=AX.X)
-            live[tau]["s_old"].append(s_h)
-
-        def make_bias(tau):
-            top = live[tau]["top_own"]
-            if n_old(tau):
-                top = stats.tile([P, HEADS], F32, name="top", tag="top")
-                nc.vector.tensor_max(out=top[:], in0=live[tau]["top_own"][:], in1=live[tau]["top_old"][:])
-            bias = stats.tile([P, HEADS], F32, name="bias", tag="bias")
-            nc.vector.tensor_scalar_mul(out=bias[:], in0=top[:], scalar1=-scale)
-            live[tau]["bias"] = bias
-
-        def exp_own(tau):
+        def exponentials(tau, h):
             c = tau % TILES
+            unit = per_unit[(tau, h)]
+            e_tile = e_rows[c][h]
             own_col = BLOCK + c * P
-            sum_own = stats.tile([P, HEADS], F32, name="sum_own", tag="sum_own")
-            for h in range(HEADS):
+            if n_mid(tau):
+                cols = n_mid(tau) * P
                 nc.scalar.activation(
-                    out=e_rows[c][h][:, own_col : own_col + P], in_=live[tau]["s_own"][:, h, :], func=ACT.Exp,
-                    bias=live[tau]["bias"][:, h : h + 1], scale=scale, accum_out=sum_own[:, h : h + 1],
+                    out=e_tile[:, own_col - cols : own_col], in_=unit["mid"][:, :cols], func=ACT.Exp,
+                    bias=unit["bias"][:], scale=scale, accum_out=per_tile[tau]["sum_mid"][:, h : h + 1],
                 )
-            live[tau]["sum_own"] = sum_own
-            if n_old(tau):
-                live[tau]["sum_old"] = stats.tile([P, HEADS], F32, name="sum_old", tag="sum_old")
-
-        def exp_old(tau, h):
-            c = tau % TILES
-            own_col = BLOCK + c * P
-            cols = n_old(tau) * P
+            if has_far(tau):
+                e_edge = e_tile[:].rearrange("p (g k) -> p g k", g=2)[:, :, c * P : (c + 1) * P]
+                s_edge = unit["edge"]
+            else:
+                e_edge = e_tile[:, own_col : own_col + P]
+                s_edge = unit["edge"][:, 1, :]
             nc.scalar.activation(
-                out=e_rows[c][h][:, own_col - cols : own_col], in_=live[tau]["s_old"][h][:, :cols], func=ACT.Exp,
-                bias=live[tau]["bias"][:, h : h + 1], scale=scale, accum_out=live[tau]["sum_old"][:, h : h + 1],
+                out=e_edge, in_=s_edge, func=ACT.Exp,
+                bias=unit["bias"][:], scale=scale, accum_out=per_tile[tau]["sum_edge"][:, h : h + 1],
             )
 
         def value_blocks(tau):
@@ -246,18 +275,21 @@ def tile_localgqattention_pb_t_kernel(tc, q_rot, k_rot, x, wv, out):
 
         def flip_e(tau, h):
             n_pass = len(value_blocks(tau))
-            live[tau]["flipped"].append(flip_rows(e_rows[tau % TILES][h][:, (2 - n_pass) * BLOCK :], n_pass))
+            per_unit[(tau, h)]["flipped"] = flip_rows(e_rows[tau % TILES][h][:, (2 - n_pass) * BLOCK :], n_pass)
 
-        def pack_e(tau, h):
-            n_pass = len(value_blocks(tau))
-            grouped = group_words(live[tau]["flipped"][h], n_pass, e_pack)
-            live[tau]["packed"].append(quantise(grouped, n_pass, e_pack))
+        def group_e(tau, h):
+            unit = per_unit[(tau, h)]
+            unit["grouped"] = group_words(unit["flipped"], len(value_blocks(tau)), e_pack)
+
+        def quantise_e(tau, h):
+            unit = per_unit[(tau, h)]
+            unit["packed"] = quantise(unit["grouped"], len(value_blocks(tau)), e_pack)
 
         def multiply_values(tau):
             blocks = value_blocks(tau)
-            o_acc = work.tile([P, HEADS, D], F32, name="o_acc", tag="work")
+            o_acc = sums.tile([P, HEADS, D], F32, name="o_acc", tag="o_acc")
             for h in range(HEADS):
-                e_codes, e_scales = live[tau]["packed"][h]
+                e_codes, e_scales = per_unit[(tau, h)]["packed"]
                 for g, vb in enumerate(blocks):
                     cols = slice(g * P, (g + 1) * P)
                     nc.tensor.matmul_mx(
@@ -266,69 +298,65 @@ def tile_localgqattention_pb_t_kernel(tc, q_rot, k_rot, x, wv, out):
                         rhs=v_codes[:, vb, :].bitcast(FP8X4), rhs_scale=v_scales[:, vb, :],
                         start=(g == 0), stop=(g == len(blocks) - 1),
                     )
-            live[tau]["o_acc"] = o_acc
+            per_tile[tau]["o_acc"] = o_acc
 
         def divide_and_store(tau):
-            total = live[tau]["sum_own"]
-            if n_old(tau):
+            total = per_tile[tau]["sum_edge"]
+            if n_mid(tau):
                 total = stats.tile([P, HEADS], F32, name="total", tag="total")
-                nc.vector.tensor_add(out=total[:], in0=live[tau]["sum_own"][:], in1=live[tau]["sum_old"][:])
+                nc.vector.tensor_add(out=total[:], in0=per_tile[tau]["sum_edge"][:], in1=per_tile[tau]["sum_mid"][:])
             inverse = stats.tile([P, HEADS], F32, name="inverse", tag="inverse")
             nc.vector.reciprocal(out=inverse[:], in_=total[:])
             result = results.tile([P, HEADS, D], F32, name="result", tag="result")
             nc.vector.tensor_tensor(
-                out=result[:], in0=live[tau]["o_acc"][:],
+                out=result[:], in0=per_tile[tau]["o_acc"][:],
                 in1=inverse[:].unsqueeze(2).to_broadcast([P, HEADS, D]), op=ALU.mult,
             )
             nc.sync.dma_start(
                 out=out_rows[tau * P : (tau + 1) * P, :], in_=result[:].rearrange("p h d -> p (h d)")
             )
 
-        def prepare_quarter(b, c):
-            if c < 2:
-                pack_x(b, 2 * c)
-                pack_x(b, 2 * c + 1)
-            elif c == 2:
-                prepare_keys(b)
-                prepare_queries(b)
-            else:
-                project_values(b)
+        n_units = (T // P) * HEADS
 
-        n_tiles = T // P
+        def scores_and_maxima(u):
+            tau, h = divmod(u, HEADS)
+            if h % 2 == 0:
+                edge_scores(tau, h // 2)
+            if n_mid(tau):
+                mid_scores(tau, h)
+
         with tc.manual_schedule():
             prepare_keys(0)
-            prepare_queries(0)
-            scores_own(0)
-            make_bias(0)
+            prepare_queries(0, 0)
+            prepare_queries(0, 1)
+            for u in range(AHEAD):
+                scores_and_maxima(u)
+                make_bias(*divmod(u, HEADS))
             wv_grouped = group_words(flip_rows(wv_in[:], hid_passes), hid_passes, keep)
             wv_codes, wv_scales = quantise(wv_grouped, hid_passes, keep)
             for slot in range(4):
                 pack_x(0, slot)
             project_values(0)
 
-            for tau in range(n_tiles):
+            for u in range(n_units + HEADS + 1):
+                if u < n_units:
+                    exponentials(*divmod(u, HEADS))
+                if 0 <= u - 2 < n_units:
+                    group_e(*divmod(u - 2, HEADS))
+                if 0 <= u - 1 < n_units:
+                    flip_e(*divmod(u - 1, HEADS))
+                if u + AHEAD < n_units:
+                    scores_and_maxima(u + AHEAD)
+                if 0 <= u - 3 < n_units:
+                    quantise_e(*divmod(u - 3, HEADS))
+                tau_done, place = divmod(u - 2 * HEADS, HEADS)
+                if place == 0 and 0 <= tau_done < T // P:
+                    divide_and_store(tau_done)
+                if u + AHEAD < n_units:
+                    make_bias(*divmod(u + AHEAD, HEADS))
+                if place == HEADS - 1 and 0 <= tau_done + 1 < T // P:
+                    multiply_values(tau_done + 1)
+                tau, h = divmod(u, HEADS)
                 b, c = divmod(tau, TILES)
-                following = tau + 1 < n_tiles
-                exp_own(tau)
-                if following:
-                    scores_own(tau + 1)
-                if tau > 0:
-                    multiply_values(tau - 1)
-                    divide_and_store(tau - 1)
-                for h in range(HEADS):
-                    if n_old(tau):
-                        exp_old(tau, h)
-                    if following:
-                        scores_old(tau + 1, h)
-                    if h < EARLY_FLIPS:
-                        flip_e(tau, h)
-                if following:
-                    make_bias(tau + 1)
-                for h in range(HEADS):
-                    if h + EARLY_FLIPS < HEADS:
-                        flip_e(tau, h + EARLY_FLIPS)
-                    pack_e(tau, h)
-                if b + 1 < N_BLOCKS:
-                    prepare_quarter(b + 1, c)
-            multiply_values(n_tiles - 1)
-            divide_and_store(n_tiles - 1)
+                if h % 2 == 1 and b + 1 < N_BLOCKS:
+                    prepare_eighth(b + 1, 2 * c + h // 2)

@@ -42,29 +42,33 @@ def tile_localgqattention_pb_t_kernel(tc, q_rot, k_rot, x, wv, out):
         tc.tile_pool(name="keep", bufs=1) as keep,
         tc.tile_pool(name="queries", bufs=3) as queries,
         tc.tile_pool(name="e_pack", bufs=8) as e_pack,
-        tc.tile_pool(name="x_pack", bufs=4) as x_pack,
+        tc.tile_pool(name="x_pack", bufs=6) as x_pack,
         tc.tile_pool(name="stats", bufs=4) as stats,
         tc.tile_pool(name="results", bufs=4) as results,
         tc.psum_pool(name="mids", bufs=3) as mids,
         tc.psum_pool(name="edges", bufs=2) as edges,
         tc.psum_pool(name="work", bufs=2) as work,
-        tc.psum_pool(name="sums", bufs=1) as sums,
+        tc.psum_pool(name="aux", bufs=1) as aux,
     ):
-        k_in, q_in, x_in = [], [], []
+        k_in = [keep.tile([P, TILES, D], BF16, name="k_in%d" % b) for b in range(N_BLOCKS)]
+        q_in = [keep.tile([P, TILES, HEADS * D], BF16, name="q_in%d" % b) for b in range(N_BLOCKS)]
+        x_in = [keep.tile([P, 4, HID], BF16, name="x_in%d" % b) for b in range(N_BLOCKS)]
         wv_in = keep.tile([P, HID], BF16, name="wv_in")
-        for b in range(N_BLOCKS):
+
+        def load_keys_and_queries(b):
             rows = slice(b * BLOCK, (b + 1) * BLOCK)
-            k_in.append(keep.tile([P, TILES, D], BF16, name="k_in%d" % b))
-            q_in.append(keep.tile([P, TILES, HEADS * D], BF16, name="q_in%d" % b))
-            x_in.append(keep.tile([P, 4, HID], BF16, name="x_in%d" % b))
             nc.sync.dma_start(out=k_in[b][:], in_=k_rows[rows, :].rearrange("(c p) d -> p c d", p=P))
             nc.sync.dma_start(out=q_in[b][:], in_=q_rows[rows, :].rearrange("(c p) f -> p c f", p=P))
-            if b == 0:
-                nc.sync.dma_start(out=wv_in[:], in_=wv)
+
+        load_keys_and_queries(0)
+        nc.sync.dma_start(out=wv_in[:], in_=wv)
+        for b in range(N_BLOCKS):
             nc.sync.dma_start(
                 out=x_in[b][:].rearrange("p (u e) f -> p u e f", u=2),
-                in_=x_rows[rows, :].rearrange("(u p e) f -> p u e f", u=2, e=2),
+                in_=x_rows[b * BLOCK : (b + 1) * BLOCK, :].rearrange("(u p e) f -> p u e f", u=2, e=2),
             )
+        for b in range(1, N_BLOCKS):
+            load_keys_and_queries(b)
 
         ident_f32 = keep.tile([P, P], F32, name="ident_f32")
         make_identity(nc, ident_f32[:])
@@ -100,9 +104,9 @@ def tile_localgqattention_pb_t_kernel(tc, q_rot, k_rot, x, wv, out):
         v_codes = keep.tile([P, N_BLOCKS, D], U32, name="v_codes", align_bytes=64)
         v_scales = keep.tile([P, N_BLOCKS, D], U8, name="v_scales", align_bytes=64)
 
-        def flip_rows(rows_bf16, n_pass):
+        def flip_rows(rows_bf16, n_pass, pool, tag):
             words = rows_bf16.bitcast(F32)
-            flipped = work.tile([P, 2 * n_pass, P], F32, name="flipped", tag="work")
+            flipped = pool.tile([P, 2 * n_pass, P], F32, name="flipped", tag=tag)
             for j in range(2 * n_pass):
                 nc.tensor.transpose(flipped[:, j, :], words[:, j * P : (j + 1) * P], ident_f32[:])
             return flipped
@@ -127,7 +131,7 @@ def tile_localgqattention_pb_t_kernel(tc, q_rot, k_rot, x, wv, out):
         x_packed = {}
 
         def prepare_keys(b):
-            k_flip = work.tile([P, TILES, P], BF16, name="k_flip", tag="work")
+            k_flip = aux.tile([P, TILES, P], BF16, name="k_flip", tag="aux")
             for c in range(TILES):
                 nc.tensor.transpose(k_flip[:, c, :], k_in[b][:, c, :], ident_bf[:])
             nc.vector.tensor_copy(
@@ -137,7 +141,7 @@ def tile_localgqattention_pb_t_kernel(tc, q_rot, k_rot, x, wv, out):
         def prepare_queries(b, pair):
             if pair == 0:
                 queries_t[b] = queries.tile([P, HEADS, BLOCK], BF16, name="q_t", tag="q_t")
-            q_flip = work.tile([P, 2, TILES, P], BF16, name="q_flip", tag="work")
+            q_flip = aux.tile([P, 2, TILES, P], BF16, name="q_flip", tag="aux")
             for hh in range(2):
                 h = 2 * pair + hh
                 for c in range(TILES):
@@ -147,13 +151,19 @@ def tile_localgqattention_pb_t_kernel(tc, q_rot, k_rot, x, wv, out):
                 in_=q_flip[:].rearrange("p h c r -> p (h c r)"),
             )
 
-        def pack_x(b, slot):
-            flipped = flip_rows(x_in[b][:, slot, :], hid_passes)
-            grouped = group_words(flipped, hid_passes, x_pack)
-            x_packed[(b, slot)] = quantise(grouped, hid_passes, x_pack)
+        x_stage = {}
+
+        def flip_x(b, slot):
+            x_stage[(b, slot)] = flip_rows(x_in[b][:, slot, :], hid_passes, mids, "mid")
+
+        def group_x(b, slot):
+            x_stage[(b, slot)] = group_words(x_stage[(b, slot)], hid_passes, x_pack)
+
+        def quantise_x(b, slot):
+            x_packed[(b, slot)] = quantise(x_stage[(b, slot)], hid_passes, x_pack)
 
         def project_values(b):
-            v_acc = work.tile([P, 4, D], F32, name="v_acc", tag="work")
+            v_acc = aux.tile([P, 4, D], F32, name="v_acc", tag="aux")
             for slot in range(4):
                 x_codes, x_scales = x_packed[(b, slot)]
                 for g in range(hid_passes):
@@ -170,16 +180,6 @@ def tile_localgqattention_pb_t_kernel(tc, q_rot, k_rot, x, wv, out):
                 out=v_codes[:, b, :].bitcast(FP8X4), scales=v_scales[:, b, :],
                 in_=v_grouped[:].rearrange("p d s -> p (d s)"),
             )
-
-        def prepare_eighth(b, j):
-            if j < 4:
-                pack_x(b, j)
-            elif j == 4:
-                prepare_keys(b)
-            elif j < 7:
-                prepare_queries(b, j - 5)
-            else:
-                project_values(b)
 
         per_tile = {}
         per_unit = {}
@@ -275,7 +275,9 @@ def tile_localgqattention_pb_t_kernel(tc, q_rot, k_rot, x, wv, out):
 
         def flip_e(tau, h):
             n_pass = len(value_blocks(tau))
-            per_unit[(tau, h)]["flipped"] = flip_rows(e_rows[tau % TILES][h][:, (2 - n_pass) * BLOCK :], n_pass)
+            per_unit[(tau, h)]["flipped"] = flip_rows(
+                e_rows[tau % TILES][h][:, (2 - n_pass) * BLOCK :], n_pass, work, "work"
+            )
 
         def group_e(tau, h):
             unit = per_unit[(tau, h)]
@@ -287,7 +289,7 @@ def tile_localgqattention_pb_t_kernel(tc, q_rot, k_rot, x, wv, out):
 
         def multiply_values(tau):
             blocks = value_blocks(tau)
-            o_acc = sums.tile([P, HEADS, D], F32, name="o_acc", tag="o_acc")
+            o_acc = aux.tile([P, HEADS, D], F32, name="o_acc", tag="aux")
             for h in range(HEADS):
                 e_codes, e_scales = per_unit[(tau, h)]["packed"]
                 for g, vb in enumerate(blocks):
@@ -300,17 +302,23 @@ def tile_localgqattention_pb_t_kernel(tc, q_rot, k_rot, x, wv, out):
                     )
             per_tile[tau]["o_acc"] = o_acc
 
-        def divide_and_store(tau):
+        def add_sums(tau):
             total = per_tile[tau]["sum_edge"]
             if n_mid(tau):
                 total = stats.tile([P, HEADS], F32, name="total", tag="total")
                 nc.vector.tensor_add(out=total[:], in0=per_tile[tau]["sum_edge"][:], in1=per_tile[tau]["sum_mid"][:])
+            per_tile[tau]["total"] = total
+
+        def invert_sums(tau):
             inverse = stats.tile([P, HEADS], F32, name="inverse", tag="inverse")
-            nc.vector.reciprocal(out=inverse[:], in_=total[:])
+            nc.vector.reciprocal(out=inverse[:], in_=per_tile[tau]["total"][:])
+            per_tile[tau]["inverse"] = inverse
+
+        def divide_and_store(tau):
             result = results.tile([P, HEADS, D], F32, name="result", tag="result")
             nc.vector.tensor_tensor(
                 out=result[:], in0=per_tile[tau]["o_acc"][:],
-                in1=inverse[:].unsqueeze(2).to_broadcast([P, HEADS, D]), op=ALU.mult,
+                in1=per_tile[tau]["inverse"][:].unsqueeze(2).to_broadcast([P, HEADS, D]), op=ALU.mult,
             )
             nc.sync.dma_start(
                 out=out_rows[tau * P : (tau + 1) * P, :], in_=result[:].rearrange("p h d -> p (h d)")
@@ -325,6 +333,10 @@ def tile_localgqattention_pb_t_kernel(tc, q_rot, k_rot, x, wv, out):
             if n_mid(tau):
                 mid_scores(tau, h)
 
+        def tile_whose_last_unit_was(u):
+            tau, h = divmod(u, HEADS)
+            return tau if h == HEADS - 1 and 0 <= tau < T // P else None
+
         with tc.manual_schedule():
             prepare_keys(0)
             prepare_queries(0, 0)
@@ -332,31 +344,48 @@ def tile_localgqattention_pb_t_kernel(tc, q_rot, k_rot, x, wv, out):
             for u in range(AHEAD):
                 scores_and_maxima(u)
                 make_bias(*divmod(u, HEADS))
-            wv_grouped = group_words(flip_rows(wv_in[:], hid_passes), hid_passes, keep)
-            wv_codes, wv_scales = quantise(wv_grouped, hid_passes, keep)
-            for slot in range(4):
-                pack_x(0, slot)
-            project_values(0)
 
-            for u in range(n_units + HEADS + 1):
+            wv_grouped = group_words(flip_rows(wv_in[:], hid_passes, mids, "mid"), hid_passes, keep)
+            wv_codes, wv_scales = quantise(wv_grouped, hid_passes, keep)
+            n_slots = 4 * N_BLOCKS
+            for j in range(n_slots + 3):
+                if j < n_slots:
+                    flip_x(*divmod(j, 4))
+                if 0 <= j - 1 < n_slots:
+                    group_x(*divmod(j - 1, 4))
+                if 0 <= j - 2 < n_slots:
+                    quantise_x(*divmod(j - 2, 4))
+                if j >= 3 and (j - 3) % 4 == 3:
+                    project_values((j - 3) // 4)
+
+            for u in range(n_units + 7):
                 if u < n_units:
                     exponentials(*divmod(u, HEADS))
+                if u + AHEAD < n_units:
+                    scores_and_maxima(u + AHEAD)
+                summed = tile_whose_last_unit_was(u - 2)
+                if summed is not None:
+                    add_sums(summed)
+                if 0 <= u - 3 < n_units:
+                    quantise_e(*divmod(u - 3, HEADS))
+                if u + AHEAD < n_units:
+                    make_bias(*divmod(u + AHEAD, HEADS))
+                if summed is not None:
+                    invert_sums(summed)
                 if 0 <= u - 2 < n_units:
                     group_e(*divmod(u - 2, HEADS))
                 if 0 <= u - 1 < n_units:
                     flip_e(*divmod(u - 1, HEADS))
-                if u + AHEAD < n_units:
-                    scores_and_maxima(u + AHEAD)
-                if 0 <= u - 3 < n_units:
-                    quantise_e(*divmod(u - 3, HEADS))
-                tau_done, place = divmod(u - 2 * HEADS, HEADS)
-                if place == 0 and 0 <= tau_done < T // P:
-                    divide_and_store(tau_done)
-                if u + AHEAD < n_units:
-                    make_bias(*divmod(u + AHEAD, HEADS))
-                if place == HEADS - 1 and 0 <= tau_done + 1 < T // P:
-                    multiply_values(tau_done + 1)
+                multiplied = tile_whose_last_unit_was(u - 6)
+                if multiplied is not None:
+                    divide_and_store(multiplied)
                 tau, h = divmod(u, HEADS)
                 b, c = divmod(tau, TILES)
-                if h % 2 == 1 and b + 1 < N_BLOCKS:
-                    prepare_eighth(b + 1, 2 * c + h // 2)
+                if h == 2 and b + 1 < N_BLOCKS:
+                    if c == 0:
+                        prepare_keys(b + 1)
+                    elif c <= 2:
+                        prepare_queries(b + 1, c - 1)
+                packed = tile_whose_last_unit_was(u - 5)
+                if packed is not None:
+                    multiply_values(packed)

@@ -21,8 +21,10 @@ D = 128
 BLOCK = 512
 TILES = BLOCK // P
 N_BLOCKS = T // BLOCK
-HALF = 256
-GROUPED_BUFS = 3
+N_TILES = T // P
+N_UNITS = N_TILES * HEADS
+HID_PASSES = HID // BLOCK
+PLACES = (0, 2, 1, 3)
 AHEAD = 2
 MASKED = -1.0e30
 
@@ -44,9 +46,10 @@ def tile_localgqattention_pb_t_kernel(tc, q_rot, k_rot, x, wv, out):
         tc.tile_pool(name="e_pack", bufs=8) as e_pack,
         tc.tile_pool(name="x_pack", bufs=6) as x_pack,
         tc.tile_pool(name="stats", bufs=4) as stats,
+        tc.tile_pool(name="tile_stats", bufs=6) as tile_stats,
         tc.tile_pool(name="results", bufs=4) as results,
-        tc.psum_pool(name="mids", bufs=3) as mids,
-        tc.psum_pool(name="edges", bufs=2) as edges,
+        tc.psum_pool(name="bigs", bufs=3) as bigs,
+        tc.psum_pool(name="smalls", bufs=2) as smalls,
         tc.psum_pool(name="work", bufs=2) as work,
         tc.psum_pool(name="aux", bufs=1) as aux,
     ):
@@ -60,12 +63,12 @@ def tile_localgqattention_pb_t_kernel(tc, q_rot, k_rot, x, wv, out):
             nc.sync.dma_start(out=k_in[b][:], in_=k_rows[rows, :].rearrange("(c p) d -> p c d", p=P))
             nc.sync.dma_start(out=q_in[b][:], in_=q_rows[rows, :].rearrange("(c p) f -> p c f", p=P))
 
-        load_keys_and_queries(0)
         nc.sync.dma_start(out=wv_in[:], in_=wv)
         for b in range(N_BLOCKS):
+            if b == 2:
+                load_keys_and_queries(0)
             nc.sync.dma_start(
-                out=x_in[b][:].rearrange("p (u e) f -> p u e f", u=2),
-                in_=x_rows[b * BLOCK : (b + 1) * BLOCK, :].rearrange("(u p e) f -> p u e f", u=2, e=2),
+                out=x_in[b][:], in_=x_rows[b * BLOCK : (b + 1) * BLOCK, :].rearrange("(p j) f -> p j f", j=4)
             )
         for b in range(1, N_BLOCKS):
             load_keys_and_queries(b)
@@ -87,32 +90,37 @@ def tile_localgqattention_pb_t_kernel(tc, q_rot, k_rot, x, wv, out):
             out=far_f32[:], in_=far_f32[:], compare_op=ALU.is_ge, fill=MASKED,
             base=0, pattern=[[1, P]], channel_multiplier=-1,
         )
-        edge_mask = keep.tile([P, 2, 2, P], BF16, name="edge_mask")
-        for hh in range(2):
-            nc.vector.tensor_copy(out=edge_mask[:, hh, 0, :], in_=far_f32[:])
-            nc.vector.tensor_copy(out=edge_mask[:, hh, 1, :], in_=own_f32[:])
+        own_mask = keep.tile([P, P], BF16, name="own_mask")
+        nc.vector.tensor_copy(out=own_mask[:], in_=own_f32[:])
+        far_mask = keep.tile([P, P], BF16, name="far_mask")
+        nc.vector.tensor_copy(out=far_mask[:], in_=far_f32[:])
 
-        e_rows = []
-        for c in range(TILES):
-            e_rows.append([])
+        e_early = [[keep.tile([P, BLOCK], BF16, name="e_early%d_%d" % (r, h)) for h in range(HEADS)] for r in range(2)]
+        e_late = [[keep.tile([P, 2 * BLOCK], BF16, name="e_late%d_%d" % (r, h)) for h in range(HEADS)] for r in range(2)]
+        for r in range(2):
             for h in range(HEADS):
-                e_tile = keep.tile([P, 2 * BLOCK], BF16, name="e_rows%d_%d" % (c, h))
-                nc.vector.memset(e_tile[:].bitcast(I32), 0)
-                e_rows[c].append(e_tile)
+                nc.vector.memset(e_early[r][h][:].bitcast(I32), 0)
+                nc.vector.memset(e_late[r][h][:].bitcast(I32), 0)
 
         keys_t = keep.tile([P, T], BF16, name="keys_t")
         v_codes = keep.tile([P, N_BLOCKS, D], U32, name="v_codes", align_bytes=64)
         v_scales = keep.tile([P, N_BLOCKS, D], U8, name="v_scales", align_bytes=64)
+        half_codes = keep.tile([P, 2, N_BLOCKS, D], U32, name="half_codes", align_bytes=64)
+        half_scales = keep.tile([P, 2, N_BLOCKS, D], U8, name="half_scales", align_bytes=64)
+        nc.vector.memset(half_codes[:].bitcast(I32), 0)
+        nc.vector.memset(half_scales[:].bitcast(I32), 0)
 
-        def flip_rows(rows_bf16, n_pass, pool, tag):
-            words = rows_bf16.bitcast(F32)
-            flipped = pool.tile([P, 2 * n_pass, P], F32, name="flipped", tag=tag)
-            for j in range(2 * n_pass):
-                nc.tensor.transpose(flipped[:, j, :], words[:, j * P : (j + 1) * P], ident_f32[:])
+        def flip_rows(passes, woven, pool, tag):
+            flipped = pool.tile([P, 2 * len(passes), P], F32, name="flipped", tag=tag)
+            for g, rows_bf16 in enumerate(passes):
+                words = rows_bf16.bitcast(F32)
+                for u in range(2):
+                    taken = words[:, u : 2 * P : 2] if woven else words[:, u * P : (u + 1) * P]
+                    nc.tensor.transpose(flipped[:, 2 * g + u, :], taken, ident_f32[:])
             return flipped
 
         def group_words(flipped, n_pass, pool):
-            grouped = pool.tile([P, n_pass * BLOCK], BF16, name="grouped", tag="grouped", bufs=GROUPED_BUFS,
+            grouped = pool.tile([P, n_pass * BLOCK], BF16, name="grouped", tag="grouped%d" % n_pass, bufs=3,
                                 align_bytes=64)
             nc.scalar.copy(
                 out=grouped[:].bitcast(F32).rearrange("p (g r u) -> p g r u", g=n_pass, u=2),
@@ -121,14 +129,21 @@ def tile_localgqattention_pb_t_kernel(tc, q_rot, k_rot, x, wv, out):
             return grouped
 
         def quantise(grouped, n_pass, pool):
-            codes = pool.tile([P, n_pass * P], U32, name="codes", tag="codes", align_bytes=64)
-            planes = pool.tile([P, n_pass * P], U8, name="planes", tag="planes", align_bytes=64)
+            codes = pool.tile([P, n_pass * P], U32, name="codes", tag="codes%d" % n_pass, align_bytes=64)
+            planes = pool.tile([P, n_pass * P], U8, name="planes", tag="planes%d" % n_pass, align_bytes=64)
             nc.vector.quantize_mx(out=codes[:].bitcast(FP8X4), scales=planes[:], in_=grouped[:])
             return codes, planes
 
-        hid_passes = HID // BLOCK
+        def multiply(acc, products):
+            for g, (l_codes, l_scales, r_codes, r_scales) in enumerate(products):
+                nc.tensor.matmul_mx(
+                    out=acc, lhsT=l_codes.bitcast(FP8X4), lhsT_scale=l_scales,
+                    rhs=r_codes.bitcast(FP8X4), rhs_scale=r_scales,
+                    start=(g == 0), stop=(g == len(products) - 1),
+                )
+
         queries_t = {}
-        x_packed = {}
+        x_stage = {}
 
         def prepare_keys(b):
             k_flip = aux.tile([P, TILES, P], BF16, name="k_flip", tag="aux")
@@ -151,29 +166,27 @@ def tile_localgqattention_pb_t_kernel(tc, q_rot, k_rot, x, wv, out):
                 in_=q_flip[:].rearrange("p h c r -> p (h c r)"),
             )
 
-        x_stage = {}
+        def hidden_passes(rows_bf16):
+            return [rows_bf16[:, g * BLOCK : (g + 1) * BLOCK] for g in range(HID_PASSES)]
 
         def flip_x(b, slot):
-            x_stage[(b, slot)] = flip_rows(x_in[b][:, slot, :], hid_passes, mids, "mid")
+            x_stage[(b, slot)] = flip_rows(hidden_passes(x_in[b][:, slot, :]), False, bigs, "big")
 
         def group_x(b, slot):
-            x_stage[(b, slot)] = group_words(x_stage[(b, slot)], hid_passes, x_pack)
+            x_stage[(b, slot)] = group_words(x_stage[(b, slot)], HID_PASSES, x_pack)
 
         def quantise_x(b, slot):
-            x_packed[(b, slot)] = quantise(x_stage[(b, slot)], hid_passes, x_pack)
+            x_stage[(b, slot)] = quantise(x_stage[(b, slot)], HID_PASSES, x_pack)
 
         def project_values(b):
             v_acc = aux.tile([P, 4, D], F32, name="v_acc", tag="aux")
             for slot in range(4):
-                x_codes, x_scales = x_packed[(b, slot)]
-                for g in range(hid_passes):
-                    cols = slice(g * P, (g + 1) * P)
-                    nc.tensor.matmul_mx(
-                        out=v_acc[:, slot, :],
-                        lhsT=x_codes[:, cols].bitcast(FP8X4), lhsT_scale=x_scales[:, cols],
-                        rhs=wv_codes[:, cols].bitcast(FP8X4), rhs_scale=wv_scales[:, cols],
-                        start=(g == 0), stop=(g == hid_passes - 1),
-                    )
+                x_codes, x_scales = x_stage[(b, slot)]
+                multiply(v_acc[:, slot, :], [
+                    (x_codes[:, g * P : (g + 1) * P], x_scales[:, g * P : (g + 1) * P],
+                     wv_codes[:, g * P : (g + 1) * P], wv_scales[:, g * P : (g + 1) * P])
+                    for g in range(HID_PASSES)
+                ])
             v_grouped = x_pack.tile([P, D, 4], BF16, name="v_grouped", tag="v_grouped", bufs=2, align_bytes=64)
             nc.vector.tensor_copy(out=v_grouped[:], in_=v_acc[:].rearrange("p s d -> p d s"))
             nc.vector.quantize_mx(
@@ -181,136 +194,169 @@ def tile_localgqattention_pb_t_kernel(tc, q_rot, k_rot, x, wv, out):
                 in_=v_grouped[:].rearrange("p d s -> p (d s)"),
             )
 
+        def copy_value_halves():
+            for half in range(2):
+                rows = slice(half * (P // 2), (half + 1) * (P // 2))
+                nc.vector.tensor_copy(out=half_codes[rows, half].bitcast(I32), in_=v_codes[rows].bitcast(I32))
+                nc.vector.tensor_copy(out=half_scales[rows, half].bitcast(I32), in_=v_scales[rows].bitcast(I32))
+
         per_tile = {}
         per_unit = {}
 
-        def n_mid(tau):
-            return min(tau, TILES - 1)
+        def unit_at(n):
+            s, h = divmod(n, HEADS)
+            b, i = divmod(s, TILES)
+            return b * TILES + PLACES[i], h
 
-        def has_far(tau):
-            return tau >= TILES
+        def is_early(tau):
+            return tau % TILES < TILES // 2
 
-        def query_cols(tau, h):
+        def part_tiles(tau, part):
             b, c = divmod(tau, TILES)
-            return queries_t[b][:, h, c * P : (c + 1) * P]
+            if part == "own":
+                return c + 1
+            return TILES - c if b > 0 else 0
 
-        def edge_scores(tau, pair):
-            if pair == 0:
-                per_tile[tau] = {
-                    "sum_edge": stats.tile([P, HEADS], F32, name="sum_edge", tag="sum_edge"),
-                    "sum_mid": stats.tile([P, HEADS], F32, name="sum_mid", tag="sum_mid") if n_mid(tau) else None,
-                }
-            edge = edges.tile([P, 2, 2, P], F32, name="edge", tag="edge")
+        def big_part(tau):
+            return "previous" if is_early(tau) else "own"
+
+        def small_part(tau):
+            return "own" if is_early(tau) else "previous"
+
+        def part_scores(dest, tau, h, part):
+            b, c = divmod(tau, TILES)
+            n = part_tiles(tau, part)
+            first = b * TILES if part == "own" else tau - TILES
             nc.tensor.matmul(
-                edge[:].rearrange("p h s r -> p (h s r)"), lhsT=ident_bf[:],
-                rhs=edge_mask[:].rearrange("p h s r -> p (h s r)"), start=True, stop=False,
+                dest[:, : n * P], lhsT=queries_t[b][:, h, c * P : (c + 1) * P],
+                rhs=keys_t[:, first * P : (first + n) * P], start=True, stop=False,
             )
-            key_tiles = keys_t[:].rearrange("p (t r) -> p t r", r=P)
-            for hh in range(2):
-                if has_far(tau):
-                    nc.tensor.matmul(
-                        edge[:, hh, :, :], lhsT=query_cols(tau, 2 * pair + hh),
-                        rhs=key_tiles[:, tau - TILES : tau + 1 : TILES, :], start=False, stop=(hh == 1),
-                    )
-                else:
-                    nc.tensor.matmul(
-                        edge[:, hh, 1, :], lhsT=query_cols(tau, 2 * pair + hh),
-                        rhs=key_tiles[:, tau, :], start=False, stop=(hh == 1),
-                    )
-            top_edge = stats.tile([P, 2], F32, name="top_edge", tag="top_edge")
-            seen = edge[:].rearrange("p h s r -> p h (s r)") if has_far(tau) else edge[:, :, 1, :]
-            nc.vector.reduce_max(out=top_edge[:], in_=seen, axis=AX.X)
-            for hh in range(2):
-                per_unit[(tau, 2 * pair + hh)] = {"edge": edge[:, hh, :, :], "top_edge": top_edge[:, hh : hh + 1]}
+            if part == "own":
+                nc.tensor.matmul(dest[:, (n - 1) * P : n * P], lhsT=ident_bf[:], rhs=own_mask[:], start=False, stop=True)
+            else:
+                nc.tensor.matmul(dest[:, :P], lhsT=ident_bf[:], rhs=far_mask[:], start=False, stop=True)
 
-        def mid_scores(tau, h):
-            cols = n_mid(tau) * P
-            mid = mids.tile([P, (TILES - 1) * P], F32, name="mid", tag="mid")
-            nc.tensor.matmul(
-                mid[:, :cols], lhsT=query_cols(tau, h), rhs=keys_t[:, tau * P - cols : tau * P],
-                start=True, stop=True,
-            )
-            top_mid = stats.tile([P, 1], F32, name="top_mid", tag="top_mid")
-            nc.vector.reduce_max(out=top_mid[:], in_=mid[:, :cols], axis=AX.X)
-            per_unit[(tau, h)]["mid"] = mid
-            per_unit[(tau, h)]["top_mid"] = top_mid
+        def e_columns(tau, h, part):
+            c = tau % TILES
+            r = c % 2
+            n = part_tiles(tau, part)
+            if is_early(tau):
+                if part == "previous":
+                    return e_early[r][h][:, c * P : BLOCK]
+                return e_late[r][h][:, BLOCK : BLOCK + n * P]
+            if part == "own":
+                return e_late[r][h][:, : n * P]
+            return e_late[r][h][:, BLOCK + c * P :]
 
-        def make_bias(tau, h):
-            unit = per_unit[(tau, h)]
+        def small_scores(tau, pair):
+            n = part_tiles(tau, small_part(tau))
+            small = smalls.tile([P, 2, 2 * P], F32, name="small", tag="small")
+            for hh in range(2):
+                part_scores(small[:, hh, :], tau, 2 * pair + hh, small_part(tau))
+            top_small = stats.tile([P, 2], F32, name="top_small", tag="top_small")
+            nc.vector.reduce_max(out=top_small[:], in_=small[:, :, : n * P], axis=AX.X)
+            for hh in range(2):
+                per_unit[(tau, 2 * pair + hh)]["small"] = small[:, hh, : n * P]
+                per_unit[(tau, 2 * pair + hh)]["top_small"] = top_small[:, hh : hh + 1]
+
+        def big_scores(tau, h):
+            n = part_tiles(tau, big_part(tau))
+            big = bigs.tile([P, BLOCK], F32, name="big", tag="big")
+            part_scores(big, tau, h, big_part(tau))
+            top_big = stats.tile([P, 1], F32, name="top_big", tag="top_big")
+            nc.vector.reduce_max(out=top_big[:], in_=big[:, : n * P], axis=AX.X)
+            per_unit[(tau, h)]["big"] = big[:, : n * P]
+            per_unit[(tau, h)]["top_big"] = top_big[:]
+
+        def scores_and_maxima(n):
+            tau, h = unit_at(n)
+            if h == 0:
+                per_tile[tau] = {}
+            if h % 2 == 0:
+                per_unit[(tau, h)] = {}
+                per_unit[(tau, h + 1)] = {}
+                if part_tiles(tau, small_part(tau)):
+                    small_scores(tau, h // 2)
+            if part_tiles(tau, big_part(tau)):
+                big_scores(tau, h)
+
+        def make_bias(n):
+            unit = per_unit[unit_at(n)]
             bias = stats.tile([P, 1], F32, name="bias", tag="bias")
-            if n_mid(tau):
+            if "big" in unit and "small" in unit:
                 nc.vector.tensor_scalar(
-                    out=bias[:], in0=unit["top_mid"][:], scalar1=unit["top_edge"], scalar2=-scale,
+                    out=bias[:], in0=unit["top_big"], scalar1=unit["top_small"], scalar2=-scale,
                     op0=ALU.max, op1=ALU.mult,
                 )
             else:
-                nc.vector.tensor_scalar_mul(out=bias[:], in0=unit["top_edge"], scalar1=-scale)
+                top = unit["top_big"] if "big" in unit else unit["top_small"]
+                nc.vector.tensor_scalar_mul(out=bias[:], in0=top, scalar1=-scale)
             unit["bias"] = bias
 
-        def exponentials(tau, h):
-            c = tau % TILES
+        def exponentials(n):
+            tau, h = unit_at(n)
             unit = per_unit[(tau, h)]
-            e_tile = e_rows[c][h]
-            own_col = BLOCK + c * P
-            if n_mid(tau):
-                cols = n_mid(tau) * P
-                nc.scalar.activation(
-                    out=e_tile[:, own_col - cols : own_col], in_=unit["mid"][:, :cols], func=ACT.Exp,
-                    bias=unit["bias"][:], scale=scale, accum_out=per_tile[tau]["sum_mid"][:, h : h + 1],
-                )
-            if has_far(tau):
-                e_edge = e_tile[:].rearrange("p (g k) -> p g k", g=2)[:, :, c * P : (c + 1) * P]
-                s_edge = unit["edge"]
-            else:
-                e_edge = e_tile[:, own_col : own_col + P]
-                s_edge = unit["edge"][:, 1, :]
-            nc.scalar.activation(
-                out=e_edge, in_=s_edge, func=ACT.Exp,
-                bias=unit["bias"][:], scale=scale, accum_out=per_tile[tau]["sum_edge"][:, h : h + 1],
-            )
+            for size, part in (("big", big_part(tau)), ("small", small_part(tau))):
+                if size in unit:
+                    if h == 0:
+                        per_tile[tau]["sum_" + size] = tile_stats.tile([P, HEADS], F32, name="sum_" + size, tag="sum_" + size)
+                    nc.scalar.activation(
+                        out=e_columns(tau, h, part), in_=unit[size], func=ACT.Exp,
+                        bias=unit["bias"][:], scale=scale, accum_out=per_tile[tau]["sum_" + size][:, h : h + 1],
+                    )
 
-        def value_blocks(tau):
-            b = tau // TILES
-            return [b - 1, b] if b > 0 else [b]
+        def e_passes(tau, h):
+            r = tau % 2
+            if is_early(tau):
+                return [e_early[r][h][:]] if tau >= TILES else []
+            return [e_late[r][h][:, :BLOCK], e_late[r][h][:, BLOCK:]]
 
-        def flip_e(tau, h):
-            n_pass = len(value_blocks(tau))
-            per_unit[(tau, h)]["flipped"] = flip_rows(
-                e_rows[tau % TILES][h][:, (2 - n_pass) * BLOCK :], n_pass, work, "work"
-            )
+        def flip_e(n):
+            tau, h = unit_at(n)
+            if e_passes(tau, h):
+                per_unit[(tau, h)]["stage"] = flip_rows(e_passes(tau, h), True, work, "work")
 
-        def group_e(tau, h):
-            unit = per_unit[(tau, h)]
-            unit["grouped"] = group_words(unit["flipped"], len(value_blocks(tau)), e_pack)
+        def group_e(n):
+            tau, h = unit_at(n)
+            if e_passes(tau, h):
+                per_unit[(tau, h)]["stage"] = group_words(per_unit[(tau, h)]["stage"], len(e_passes(tau, h)), e_pack)
 
-        def quantise_e(tau, h):
-            unit = per_unit[(tau, h)]
-            unit["packed"] = quantise(unit["grouped"], len(value_blocks(tau)), e_pack)
+        def quantise_e(n):
+            tau, h = unit_at(n)
+            if e_passes(tau, h):
+                per_unit[(tau, h)]["stage"] = quantise(per_unit[(tau, h)]["stage"], len(e_passes(tau, h)), e_pack)
 
         def multiply_values(tau):
-            blocks = value_blocks(tau)
+            b = tau // TILES
+            late = tau + 2 if is_early(tau) else tau
             o_acc = aux.tile([P, HEADS, D], F32, name="o_acc", tag="aux")
             for h in range(HEADS):
-                e_codes, e_scales = per_unit[(tau, h)]["packed"]
-                for g, vb in enumerate(blocks):
-                    cols = slice(g * P, (g + 1) * P)
-                    nc.tensor.matmul_mx(
-                        out=o_acc[:, h, :],
-                        lhsT=e_codes[:, cols].bitcast(FP8X4), lhsT_scale=e_scales[:, cols],
-                        rhs=v_codes[:, vb, :].bitcast(FP8X4), rhs_scale=v_scales[:, vb, :],
-                        start=(g == 0), stop=(g == len(blocks) - 1),
-                    )
+                late_codes, late_scales = per_unit[(late, h)]["stage"]
+                shared = (late_codes[:, P:], late_scales[:, P:])
+                products = []
+                if is_early(tau):
+                    if b > 0:
+                        early_codes, early_scales = per_unit[(tau, h)]["stage"]
+                        products.append((early_codes[:], early_scales[:], v_codes[:, b - 1, :], v_scales[:, b - 1, :]))
+                    products.append(shared + (half_codes[:, 0, b, :], half_scales[:, 0, b, :]))
+                else:
+                    products.append((late_codes[:, :P], late_scales[:, :P], v_codes[:, b, :], v_scales[:, b, :]))
+                    if b > 0:
+                        products.append(shared + (half_codes[:, 1, b - 1, :], half_scales[:, 1, b - 1, :]))
+                multiply(o_acc[:, h, :], products)
             per_tile[tau]["o_acc"] = o_acc
 
         def add_sums(tau):
-            total = per_tile[tau]["sum_edge"]
-            if n_mid(tau):
-                total = stats.tile([P, HEADS], F32, name="total", tag="total")
-                nc.vector.tensor_add(out=total[:], in0=per_tile[tau]["sum_edge"][:], in1=per_tile[tau]["sum_mid"][:])
-            per_tile[tau]["total"] = total
+            sums = per_tile[tau]
+            if "sum_big" in sums and "sum_small" in sums:
+                total = tile_stats.tile([P, HEADS], F32, name="total", tag="total")
+                nc.vector.tensor_add(out=total[:], in0=sums["sum_big"][:], in1=sums["sum_small"][:])
+            else:
+                total = sums["sum_big"] if "sum_big" in sums else sums["sum_small"]
+            sums["total"] = total
 
         def invert_sums(tau):
-            inverse = stats.tile([P, HEADS], F32, name="inverse", tag="inverse")
+            inverse = tile_stats.tile([P, HEADS], F32, name="inverse", tag="inverse")
             nc.vector.reciprocal(out=inverse[:], in_=per_tile[tau]["total"][:])
             per_tile[tau]["inverse"] = inverse
 
@@ -324,29 +370,18 @@ def tile_localgqattention_pb_t_kernel(tc, q_rot, k_rot, x, wv, out):
                 out=out_rows[tau * P : (tau + 1) * P, :], in_=result[:].rearrange("p h d -> p (h d)")
             )
 
-        n_units = (T // P) * HEADS
+        def tile_ending_at(n):
+            if 0 <= n < N_UNITS and n % HEADS == HEADS - 1:
+                return unit_at(n)[0]
+            return None
 
-        def scores_and_maxima(u):
-            tau, h = divmod(u, HEADS)
-            if h % 2 == 0:
-                edge_scores(tau, h // 2)
-            if n_mid(tau):
-                mid_scores(tau, h)
-
-        def tile_whose_last_unit_was(u):
-            tau, h = divmod(u, HEADS)
-            return tau if h == HEADS - 1 and 0 <= tau < T // P else None
+        def late_tile_ending_at(n):
+            tau = tile_ending_at(n)
+            return tau if tau is not None and not is_early(tau) else None
 
         with tc.manual_schedule():
-            prepare_keys(0)
-            prepare_queries(0, 0)
-            prepare_queries(0, 1)
-            for u in range(AHEAD):
-                scores_and_maxima(u)
-                make_bias(*divmod(u, HEADS))
-
-            wv_grouped = group_words(flip_rows(wv_in[:], hid_passes, mids, "mid"), hid_passes, keep)
-            wv_codes, wv_scales = quantise(wv_grouped, hid_passes, keep)
+            wv_grouped = group_words(flip_rows(hidden_passes(wv_in[:]), False, bigs, "big"), HID_PASSES, keep)
+            wv_codes, wv_scales = quantise(wv_grouped, HID_PASSES, keep)
             n_slots = 4 * N_BLOCKS
             for j in range(n_slots + 3):
                 if j < n_slots:
@@ -357,35 +392,45 @@ def tile_localgqattention_pb_t_kernel(tc, q_rot, k_rot, x, wv, out):
                     quantise_x(*divmod(j - 2, 4))
                 if j >= 3 and (j - 3) % 4 == 3:
                     project_values((j - 3) // 4)
+                if j == n_slots // 2:
+                    prepare_keys(0)
+                    prepare_queries(0, 0)
+                    prepare_queries(0, 1)
+                    for n in range(AHEAD):
+                        scores_and_maxima(n)
+                        make_bias(n)
+            copy_value_halves()
 
-            for u in range(n_units + 7):
-                if u < n_units:
-                    exponentials(*divmod(u, HEADS))
-                if u + AHEAD < n_units:
-                    scores_and_maxima(u + AHEAD)
-                summed = tile_whose_last_unit_was(u - 2)
+            for n in range(N_UNITS + 9):
+                if n < N_UNITS:
+                    exponentials(n)
+                if late_tile_ending_at(n - 6) is not None:
+                    divide_and_store(late_tile_ending_at(n - 6) - 2)
+                if late_tile_ending_at(n - 8) is not None:
+                    divide_and_store(late_tile_ending_at(n - 8))
+                if n + AHEAD < N_UNITS:
+                    scores_and_maxima(n + AHEAD)
+                summed = tile_ending_at(n - 2)
                 if summed is not None:
                     add_sums(summed)
-                if 0 <= u - 3 < n_units:
-                    quantise_e(*divmod(u - 3, HEADS))
-                if u + AHEAD < n_units:
-                    make_bias(*divmod(u + AHEAD, HEADS))
+                if 0 <= n - 3 < N_UNITS:
+                    quantise_e(n - 3)
+                if n + AHEAD < N_UNITS:
+                    make_bias(n + AHEAD)
                 if summed is not None:
                     invert_sums(summed)
-                if 0 <= u - 2 < n_units:
-                    group_e(*divmod(u - 2, HEADS))
-                if 0 <= u - 1 < n_units:
-                    flip_e(*divmod(u - 1, HEADS))
-                multiplied = tile_whose_last_unit_was(u - 6)
-                if multiplied is not None:
-                    divide_and_store(multiplied)
-                tau, h = divmod(u, HEADS)
-                b, c = divmod(tau, TILES)
-                if h == 2 and b + 1 < N_BLOCKS:
-                    if c == 0:
+                if 0 <= n - 2 < N_UNITS:
+                    group_e(n - 2)
+                if 0 <= n - 1 < N_UNITS:
+                    flip_e(n - 1)
+                if late_tile_ending_at(n - 5) is not None:
+                    multiply_values(late_tile_ending_at(n - 5) - 2)
+                if late_tile_ending_at(n - 7) is not None:
+                    multiply_values(late_tile_ending_at(n - 7))
+                b, step = divmod(n, TILES * HEADS)
+                if b + 1 < N_BLOCKS and step % 8 in (1, 3):
+                    part = 2 * (step // 8) + (step % 8) // 2
+                    if part == 0:
                         prepare_keys(b + 1)
-                    elif c <= 2:
-                        prepare_queries(b + 1, c - 1)
-                packed = tile_whose_last_unit_was(u - 5)
-                if packed is not None:
-                    multiply_values(packed)
+                    elif part <= 2:
+                        prepare_queries(b + 1, part - 1)

@@ -284,13 +284,13 @@ def tile_localgqattention_pb_t_kernel(tc, q_rot, k_rot, x, wv, out):
             unit = per_unit[unit_at(n)]
             bias = stats.tile([P, 1], F32, name="bias", tag="bias")
             if "big" in unit and "small" in unit:
-                nc.vector.tensor_scalar(
+                nc.gpsimd.tensor_scalar(
                     out=bias[:], in0=unit["top_big"], scalar1=unit["top_small"], scalar2=-scale,
                     op0=ALU.max, op1=ALU.mult,
                 )
             else:
                 top = unit["top_big"] if "big" in unit else unit["top_small"]
-                nc.vector.tensor_scalar_mul(out=bias[:], in0=top, scalar1=-scale)
+                nc.gpsimd.tensor_scalar_mul(out=bias[:], in0=top, scalar1=-scale)
             unit["bias"] = bias
 
         def exponentials(n):
@@ -350,7 +350,7 @@ def tile_localgqattention_pb_t_kernel(tc, q_rot, k_rot, x, wv, out):
             sums = per_tile[tau]
             if "sum_big" in sums and "sum_small" in sums:
                 total = tile_stats.tile([P, HEADS], F32, name="total", tag="total")
-                nc.vector.tensor_add(out=total[:], in0=sums["sum_big"][:], in1=sums["sum_small"][:])
+                nc.gpsimd.tensor_tensor(out=total[:], in0=sums["sum_big"][:], in1=sums["sum_small"][:], op=ALU.add)
             else:
                 total = sums["sum_big"] if "sum_big" in sums else sums["sum_small"]
             sums["total"] = total
@@ -410,15 +410,13 @@ def tile_localgqattention_pb_t_kernel(tc, q_rot, k_rot, x, wv, out):
                     divide_and_store(late_tile_ending_at(n - 8))
                 if n + AHEAD < N_UNITS:
                     scores_and_maxima(n + AHEAD)
-                summed = tile_ending_at(n - 2)
-                if summed is not None:
-                    add_sums(summed)
+                    make_bias(n + AHEAD)
+                if tile_ending_at(n - 2) is not None:
+                    add_sums(tile_ending_at(n - 2))
                 if 0 <= n - 3 < N_UNITS:
                     quantise_e(n - 3)
-                if n + AHEAD < N_UNITS:
-                    make_bias(n + AHEAD)
-                if summed is not None:
-                    invert_sums(summed)
+                if tile_ending_at(n - 3) is not None:
+                    invert_sums(tile_ending_at(n - 3))
                 if 0 <= n - 2 < N_UNITS:
                     group_e(n - 2)
                 if 0 <= n - 1 < N_UNITS:

@@ -21,11 +21,13 @@ D = 128
 BLOCK = 512
 TILES = BLOCK // P
 N_BLOCKS = T // BLOCK
-N_TILES = T // P
-N_UNITS = N_TILES * HEADS
+GROUP = 32
+SLOTS = BLOCK // GROUP
+N_UNITS = T // GROUP
+QUAD = 4
 HID_PASSES = HID // BLOCK
-PLACES = (0, 2, 1, 3)
 AHEAD = 2
+RING = 6
 MASKED = -1.0e30
 
 FLOPS = 2 * T * HID * D + 2 * 2 * HEADS * D * BLOCK * (2 * BLOCK * (N_BLOCKS - 1) + BLOCK)
@@ -38,15 +40,14 @@ def tile_localgqattention_pb_t_kernel(tc, q_rot, k_rot, x, wv, out):
     q_rows = q_rot.rearrange("b t h d -> (b t) (h d)")
     k_rows = k_rot.rearrange("b t h d -> (b t) (h d)")
     x_rows = x.flatten_outer_dims()
-    out_rows = out.flatten_outer_dims()
+    out_rows = out.flatten_outer_dims().rearrange("t (h d) -> (t h) d", h=HEADS)
 
     with (
         tc.tile_pool(name="keep", bufs=1) as keep,
         tc.tile_pool(name="queries", bufs=3) as queries,
-        tc.tile_pool(name="e_pack", bufs=8) as e_pack,
-        tc.tile_pool(name="x_pack", bufs=6) as x_pack,
-        tc.tile_pool(name="stats", bufs=4) as stats,
-        tc.tile_pool(name="tile_stats", bufs=6) as tile_stats,
+        tc.tile_pool(name="packs", bufs=3) as packs,
+        tc.tile_pool(name="stats", bufs=6) as stats,
+        tc.tile_pool(name="quad_stats", bufs=12) as quad_stats,
         tc.tile_pool(name="results", bufs=4) as results,
         tc.psum_pool(name="bigs", bufs=3) as bigs,
         tc.psum_pool(name="smalls", bufs=2) as smalls,
@@ -58,79 +59,92 @@ def tile_localgqattention_pb_t_kernel(tc, q_rot, k_rot, x, wv, out):
         x_in = [keep.tile([P, 4, HID], BF16, name="x_in%d" % b) for b in range(N_BLOCKS)]
         wv_in = keep.tile([P, HID], BF16, name="wv_in")
 
-        def load_keys_and_queries(b):
+        def load_keys(b):
             rows = slice(b * BLOCK, (b + 1) * BLOCK)
             nc.sync.dma_start(out=k_in[b][:], in_=k_rows[rows, :].rearrange("(c p) d -> p c d", p=P))
-            nc.sync.dma_start(out=q_in[b][:], in_=q_rows[rows, :].rearrange("(c p) f -> p c f", p=P))
 
-        nc.sync.dma_start(out=wv_in[:], in_=wv)
-        for b in range(N_BLOCKS):
-            if b == 2:
-                load_keys_and_queries(0)
+        def load_queries(b, half):
+            first = b * BLOCK + half * 2 * P
+            nc.sync.dma_start(
+                out=q_in[b][:, 2 * half : 2 * half + 2, :],
+                in_=q_rows[first : first + 2 * P, :].rearrange("(c p) f -> p c f", p=P),
+            )
+
+        def load_hidden(b):
             nc.sync.dma_start(
                 out=x_in[b][:], in_=x_rows[b * BLOCK : (b + 1) * BLOCK, :].rearrange("(p j) f -> p j f", j=4)
             )
-        for b in range(1, N_BLOCKS):
-            load_keys_and_queries(b)
 
-        ident_f32 = keep.tile([P, P], F32, name="ident_f32")
-        make_identity(nc, ident_f32[:])
+        load_keys(0)
+        load_queries(0, 0)
+        nc.sync.dma_start(out=wv_in[:], in_=wv)
+        load_queries(0, 1)
+        load_hidden(0)
+        load_keys(1)
+        load_hidden(1)
+        load_queries(1, 0)
+        load_queries(1, 1)
+        for b in range(2, N_BLOCKS):
+            load_hidden(b)
+            load_keys(b)
+            load_queries(b, 0)
+            load_queries(b, 1)
+
         ident_bf = keep.tile([P, P], BF16, name="ident_bf")
         make_identity(nc, ident_bf[:])
 
-        own_f32 = keep.tile([P, P], F32, name="own_f32")
+        own_f32 = keep.tile([P, GROUP], F32, name="own_f32")
         nc.gpsimd.memset(own_f32[:], 0.0)
         nc.gpsimd.affine_select(
             out=own_f32[:], in_=own_f32[:], compare_op=ALU.is_ge, fill=MASKED,
-            base=0, pattern=[[-1, P]], channel_multiplier=1,
+            base=0, pattern=[[-HEADS, GROUP]], channel_multiplier=1,
         )
-        far_f32 = keep.tile([P, P], F32, name="far_f32")
+        far_f32 = keep.tile([P, GROUP], F32, name="far_f32")
         nc.gpsimd.memset(far_f32[:], 0.0)
         nc.gpsimd.affine_select(
             out=far_f32[:], in_=far_f32[:], compare_op=ALU.is_ge, fill=MASKED,
-            base=0, pattern=[[1, P]], channel_multiplier=-1,
+            base=HEADS - 1, pattern=[[HEADS, GROUP]], channel_multiplier=-1,
         )
-        own_mask = keep.tile([P, P], BF16, name="own_mask")
-        nc.vector.tensor_copy(out=own_mask[:], in_=own_f32[:])
-        far_mask = keep.tile([P, P], BF16, name="far_mask")
+        ident_f32 = keep.tile([P, P], F32, name="ident_f32")
+        make_identity(nc, ident_f32[:])
+        own_masks = keep.tile([P, QUAD, GROUP], BF16, name="own_masks")
+        for u in range(QUAD):
+            nc.vector.tensor_copy(out=own_masks[:, u, :], in_=own_f32[:])
+        far_mask = keep.tile([P, GROUP], BF16, name="far_mask")
         nc.vector.tensor_copy(out=far_mask[:], in_=far_f32[:])
 
-        e_early = [[keep.tile([P, BLOCK], BF16, name="e_early%d_%d" % (r, h)) for h in range(HEADS)] for r in range(2)]
-        e_late = [[keep.tile([P, 2 * BLOCK], BF16, name="e_late%d_%d" % (r, h)) for h in range(HEADS)] for r in range(2)]
-        for r in range(2):
-            for h in range(HEADS):
-                nc.vector.memset(e_early[r][h][:].bitcast(I32), 0)
-                nc.vector.memset(e_late[r][h][:].bitcast(I32), 0)
+        e_main = [keep.tile([P, BLOCK], BF16, name="e_main%d" % i) for i in range(RING)]
+        e_shared = [keep.tile([P, BLOCK], BF16, name="e_shared%d" % i) for i in range(2)]
+        for e_tile in e_main + e_shared:
+            nc.vector.memset(e_tile[:].bitcast(I32), 0)
 
         keys_t = keep.tile([P, T], BF16, name="keys_t")
         v_codes = keep.tile([P, N_BLOCKS, D], U32, name="v_codes", align_bytes=64)
         v_scales = keep.tile([P, N_BLOCKS, D], U8, name="v_scales", align_bytes=64)
-        half_codes = keep.tile([P, 2, N_BLOCKS, D], U32, name="half_codes", align_bytes=64)
-        half_scales = keep.tile([P, 2, N_BLOCKS, D], U8, name="half_scales", align_bytes=64)
-        nc.vector.memset(half_codes[:].bitcast(I32), 0)
-        nc.vector.memset(half_scales[:].bitcast(I32), 0)
+        nc.gpsimd.memset(v_scales[:].bitcast(I32), 0)
+        v_planes = [keep.tile([P, SLOTS, 3, D // 4], I32, name="v_planes%d" % i, align_bytes=64) for i in range(3)]
+        for planes in v_planes:
+            nc.gpsimd.memset(planes[:].rearrange("p s k w -> p (s k w)"), 0)
 
-        def flip_rows(passes, woven, pool, tag):
-            flipped = pool.tile([P, 2 * len(passes), P], F32, name="flipped", tag=tag)
+        def flip_rows(passes):
+            flipped = work.tile([P, 4, P], F32, name="flipped", tag="work")
             for g, rows_bf16 in enumerate(passes):
                 words = rows_bf16.bitcast(F32)
                 for u in range(2):
-                    taken = words[:, u : 2 * P : 2] if woven else words[:, u * P : (u + 1) * P]
-                    nc.tensor.transpose(flipped[:, 2 * g + u, :], taken, ident_f32[:])
+                    nc.tensor.transpose(flipped[:, 2 * g + u, :], words[:, u * P : (u + 1) * P], ident_f32[:])
             return flipped
 
-        def group_words(flipped, n_pass, pool):
-            grouped = pool.tile([P, n_pass * BLOCK], BF16, name="grouped", tag="grouped%d" % n_pass, bufs=3,
-                                align_bytes=64)
+        def group_words(flipped, n_pass):
+            grouped = packs.tile([P, n_pass * BLOCK], BF16, name="grouped", tag="grouped%d" % n_pass, align_bytes=64)
             nc.scalar.copy(
                 out=grouped[:].bitcast(F32).rearrange("p (g r u) -> p g r u", g=n_pass, u=2),
-                in_=flipped[:].rearrange("p (g u) r -> p g r u", u=2),
+                in_=flipped[:, : 2 * n_pass, :].rearrange("p (g u) r -> p g r u", u=2),
             )
             return grouped
 
-        def quantise(grouped, n_pass, pool):
-            codes = pool.tile([P, n_pass * P], U32, name="codes", tag="codes%d" % n_pass, align_bytes=64)
-            planes = pool.tile([P, n_pass * P], U8, name="planes", tag="planes%d" % n_pass, align_bytes=64)
+        def quantise(grouped, n_pass, kind, bufs):
+            codes = packs.tile([P, n_pass * P], U32, name="codes", tag=kind + "_codes", bufs=bufs, align_bytes=64)
+            planes = packs.tile([P, n_pass * P], U8, name="planes", tag=kind + "_scales", bufs=bufs, align_bytes=64)
             nc.vector.quantize_mx(out=codes[:].bitcast(FP8X4), scales=planes[:], in_=grouped[:])
             return codes, planes
 
@@ -143,7 +157,7 @@ def tile_localgqattention_pb_t_kernel(tc, q_rot, k_rot, x, wv, out):
                 )
 
         queries_t = {}
-        x_stage = {}
+        packed = {}
 
         def prepare_keys(b):
             k_flip = aux.tile([P, TILES, P], BF16, name="k_flip", tag="aux")
@@ -153,282 +167,276 @@ def tile_localgqattention_pb_t_kernel(tc, q_rot, k_rot, x, wv, out):
                 out=keys_t[:, b * BLOCK : (b + 1) * BLOCK], in_=k_flip[:].rearrange("p c r -> p (c r)")
             )
 
-        def prepare_queries(b, pair):
-            if pair == 0:
-                queries_t[b] = queries.tile([P, HEADS, BLOCK], BF16, name="q_t", tag="q_t")
-            q_flip = aux.tile([P, 2, TILES, P], BF16, name="q_flip", tag="aux")
-            for hh in range(2):
-                h = 2 * pair + hh
-                for c in range(TILES):
-                    nc.tensor.transpose(q_flip[:, hh, c, :], q_in[b][:, c, h * D : (h + 1) * D], ident_bf[:])
+        def prepare_queries(b, half):
+            if half == 0:
+                queries_t[b] = queries.tile([P, BLOCK * HEADS], BF16, name="q_t", tag="q_t")
+            q_flip = aux.tile([P, 2, HEADS, P], BF16, name="q_flip", tag="aux")
+            for cc in range(2):
+                for h in range(HEADS):
+                    nc.tensor.transpose(q_flip[:, cc, h, :], q_in[b][:, 2 * half + cc, h * D : (h + 1) * D], ident_bf[:])
+            n = 2 * P * HEADS
             nc.vector.tensor_copy(
-                out=queries_t[b][:, 2 * pair : 2 * pair + 2, :].rearrange("p h r -> p (h r)"),
-                in_=q_flip[:].rearrange("p h c r -> p (h c r)"),
+                out=queries_t[b][:, half * n : (half + 1) * n].rearrange("p (c r h) -> p c r h", c=2, h=HEADS),
+                in_=q_flip[:].rearrange("p c h r -> p c r h"),
             )
 
         def hidden_passes(rows_bf16):
             return [rows_bf16[:, g * BLOCK : (g + 1) * BLOCK] for g in range(HID_PASSES)]
 
-        def flip_x(b, slot):
-            x_stage[(b, slot)] = flip_rows(hidden_passes(x_in[b][:, slot, :]), False, bigs, "big")
-
-        def group_x(b, slot):
-            x_stage[(b, slot)] = group_words(x_stage[(b, slot)], HID_PASSES, x_pack)
-
-        def quantise_x(b, slot):
-            x_stage[(b, slot)] = quantise(x_stage[(b, slot)], HID_PASSES, x_pack)
+        v_stage = {}
 
         def project_values(b):
             v_acc = aux.tile([P, 4, D], F32, name="v_acc", tag="aux")
+            wv_codes, wv_scales = packed[("wv",)]
             for slot in range(4):
-                x_codes, x_scales = x_stage[(b, slot)]
+                x_codes, x_scales = packed.pop(("x", b, slot))
                 multiply(v_acc[:, slot, :], [
                     (x_codes[:, g * P : (g + 1) * P], x_scales[:, g * P : (g + 1) * P],
                      wv_codes[:, g * P : (g + 1) * P], wv_scales[:, g * P : (g + 1) * P])
                     for g in range(HID_PASSES)
                 ])
-            v_grouped = x_pack.tile([P, D, 4], BF16, name="v_grouped", tag="v_grouped", bufs=2, align_bytes=64)
+            v_grouped = packs.tile([P, D, 4], BF16, name="v_grouped", tag="v_grouped", bufs=2, align_bytes=64)
             nc.vector.tensor_copy(out=v_grouped[:], in_=v_acc[:].rearrange("p s d -> p d s"))
+            v_stage[b] = v_grouped
+
+        def quantise_values(b):
             nc.vector.quantize_mx(
                 out=v_codes[:, b, :].bitcast(FP8X4), scales=v_scales[:, b, :],
-                in_=v_grouped[:].rearrange("p d s -> p (d s)"),
+                in_=v_stage.pop(b)[:].rearrange("p d s -> p (d s)"),
             )
 
-        def copy_value_halves():
-            for half in range(2):
-                rows = slice(half * (P // 2), (half + 1) * (P // 2))
-                nc.vector.tensor_copy(out=half_codes[rows, half].bitcast(I32), in_=v_codes[rows].bitcast(I32))
-                nc.vector.tensor_copy(out=half_scales[rows, half].bitcast(I32), in_=v_scales[rows].bitcast(I32))
+        def plane_moves(b):
+            moves = []
+            source = v_scales[:, b, :].bitcast(I32)
+            planes = v_planes[b % 3]
 
-        per_tile = {}
+            def copy(lo, hi, dest):
+                moves.append(lambda: nc.gpsimd.tensor_copy(
+                    out=dest, in_=source[lo:hi].unsqueeze(1).to_broadcast([hi - lo, dest.shape[1], D // 4])
+                ))
+
+            def clear(dest):
+                moves.append(lambda: nc.gpsimd.memset(dest, 0))
+
+            for a in range(TILES):
+                rows = slice(32 * a, 32 * a + 4)
+                copy(32 * a, 32 * a + 4, planes[rows, : 4 * a + 4, 2, :])
+                if a + 1 < TILES:
+                    copy(32 * a, 32 * a + 4, planes[rows, 4 * a + 4 :, 0, :])
+            for s in range(SLOTS):
+                a, r = divmod(s, 4)
+                copy(32 * a, 32 * a + r + 1, planes[32 * a : 32 * a + r + 1, s, 0:2, :])
+                if r:
+                    clear(planes[32 * a : 32 * a + r, s, 1:3, :])
+            return moves
+
+        per_quad = {}
         per_unit = {}
 
-        def unit_at(n):
-            s, h = divmod(n, HEADS)
-            b, i = divmod(s, TILES)
-            return b * TILES + PLACES[i], h
+        def run_of_columns(tile_ap, first, n_slots):
+            halves = tile_ap.rearrange("q (u w) -> q u w", u=2)
+            return halves[:, :, first * GROUP // 2 : (first + n_slots) * GROUP // 2].rearrange("q u (p e) -> q u p e", e=2)
 
-        def is_early(tau):
-            return tau % TILES < TILES // 2
-
-        def part_tiles(tau, part):
-            b, c = divmod(tau, TILES)
-            if part == "own":
-                return c + 1
-            return TILES - c if b > 0 else 0
-
-        def big_part(tau):
-            return "previous" if is_early(tau) else "own"
-
-        def small_part(tau):
-            return "own" if is_early(tau) else "previous"
-
-        def part_scores(dest, tau, h, part):
-            b, c = divmod(tau, TILES)
-            n = part_tiles(tau, part)
-            first = b * TILES if part == "own" else tau - TILES
+        def small_scores(quad):
+            b = quad * QUAD // SLOTS
+            small = smalls.tile([P, QUAD, GROUP], F32, name="small", tag="small")
             nc.tensor.matmul(
-                dest[:, : n * P], lhsT=queries_t[b][:, h, c * P : (c + 1) * P],
-                rhs=keys_t[:, first * P : (first + n) * P], start=True, stop=False,
+                small[:].rearrange("p u k -> p (u k)"), lhsT=ident_bf[:],
+                rhs=own_masks[:].rearrange("p u k -> p (u k)"), start=True, stop=False,
             )
-            if part == "own":
-                nc.tensor.matmul(dest[:, (n - 1) * P : n * P], lhsT=ident_bf[:], rhs=own_mask[:], start=False, stop=True)
-            else:
-                nc.tensor.matmul(dest[:, :P], lhsT=ident_bf[:], rhs=far_mask[:], start=False, stop=True)
+            for u in range(QUAD):
+                n = quad * QUAD + u
+                s = n % SLOTS
+                nc.tensor.matmul(
+                    small[:, u, :], lhsT=queries_t[b][:, s * P : (s + 1) * P],
+                    rhs=keys_t[:, n * GROUP : (n + 1) * GROUP], start=False, stop=(u == QUAD - 1),
+                )
+            top_small = stats.tile([P, QUAD], F32, name="top_small", tag="top_small")
+            nc.vector.reduce_max(out=top_small[:], in_=small[:], axis=AX.X)
+            per_quad[quad] = {"small": small, "top_small": top_small}
 
-        def e_columns(tau, h, part):
-            c = tau % TILES
-            r = c % 2
-            n = part_tiles(tau, part)
-            if is_early(tau):
-                if part == "previous":
-                    return e_early[r][h][:, c * P : BLOCK]
-                return e_late[r][h][:, BLOCK : BLOCK + n * P]
-            if part == "own":
-                return e_late[r][h][:, : n * P]
-            return e_late[r][h][:, BLOCK + c * P :]
-
-        def small_scores(tau, pair):
-            n = part_tiles(tau, small_part(tau))
-            small = smalls.tile([P, 2, 2 * P], F32, name="small", tag="small")
-            for hh in range(2):
-                part_scores(small[:, hh, :], tau, 2 * pair + hh, small_part(tau))
-            top_small = stats.tile([P, 2], F32, name="top_small", tag="top_small")
-            nc.vector.reduce_max(out=top_small[:], in_=small[:, :, : n * P], axis=AX.X)
-            for hh in range(2):
-                per_unit[(tau, 2 * pair + hh)]["small"] = small[:, hh, : n * P]
-                per_unit[(tau, 2 * pair + hh)]["top_small"] = top_small[:, hh : hh + 1]
-
-        def big_scores(tau, h):
-            n = part_tiles(tau, big_part(tau))
+        def big_scores(n):
+            b, s = divmod(n, SLOTS)
+            unit = {}
+            per_unit[n] = unit
+            cols = BLOCK if b > 0 else s * GROUP
+            if cols == 0:
+                return
             big = bigs.tile([P, BLOCK], F32, name="big", tag="big")
-            part_scores(big, tau, h, big_part(tau))
+            q_ap = queries_t[b][:, s * P : (s + 1) * P]
+            if s > 0:
+                nc.tensor.matmul(
+                    big[:, : s * GROUP], lhsT=q_ap, rhs=keys_t[:, b * BLOCK : b * BLOCK + s * GROUP],
+                    start=True, stop=True,
+                )
+            if b > 0:
+                nc.tensor.matmul(
+                    big[:, s * GROUP :], lhsT=q_ap, rhs=keys_t[:, (n - SLOTS) * GROUP : b * BLOCK],
+                    start=True, stop=False,
+                )
+                nc.tensor.matmul(
+                    big[:, s * GROUP : (s + 1) * GROUP], lhsT=ident_bf[:], rhs=far_mask[:], start=False, stop=True,
+                )
             top_big = stats.tile([P, 1], F32, name="top_big", tag="top_big")
-            nc.vector.reduce_max(out=top_big[:], in_=big[:, : n * P], axis=AX.X)
-            per_unit[(tau, h)]["big"] = big[:, : n * P]
-            per_unit[(tau, h)]["top_big"] = top_big[:]
+            nc.vector.reduce_max(out=top_big[:], in_=big[:, :cols], axis=AX.X)
+            unit["big"] = big
+            unit["top_big"] = top_big
 
         def scores_and_maxima(n):
-            tau, h = unit_at(n)
-            if h == 0:
-                per_tile[tau] = {}
-            if h % 2 == 0:
-                per_unit[(tau, h)] = {}
-                per_unit[(tau, h + 1)] = {}
-                if part_tiles(tau, small_part(tau)):
-                    small_scores(tau, h // 2)
-            if part_tiles(tau, big_part(tau)):
-                big_scores(tau, h)
+            if n % QUAD == 0:
+                small_scores(n // QUAD)
+            big_scores(n)
 
         def make_bias(n):
-            unit = per_unit[unit_at(n)]
+            unit = per_unit[n]
+            top_small = per_quad[n // QUAD]["top_small"][:, n % QUAD : n % QUAD + 1]
             bias = stats.tile([P, 1], F32, name="bias", tag="bias")
-            if "big" in unit and "small" in unit:
+            if "big" in unit:
                 nc.gpsimd.tensor_scalar(
-                    out=bias[:], in0=unit["top_big"], scalar1=unit["top_small"], scalar2=-scale,
+                    out=bias[:], in0=unit["top_big"][:], scalar1=top_small, scalar2=-scale,
                     op0=ALU.max, op1=ALU.mult,
                 )
             else:
-                top = unit["top_big"] if "big" in unit else unit["top_small"]
-                nc.gpsimd.tensor_scalar_mul(out=bias[:], in0=top, scalar1=-scale)
+                nc.gpsimd.tensor_scalar_mul(out=bias[:], in0=top_small, scalar1=-scale)
             unit["bias"] = bias
 
         def exponentials(n):
-            tau, h = unit_at(n)
-            unit = per_unit[(tau, h)]
-            for size, part in (("big", big_part(tau)), ("small", small_part(tau))):
-                if size in unit:
-                    if h == 0:
-                        per_tile[tau]["sum_" + size] = tile_stats.tile([P, HEADS], F32, name="sum_" + size, tag="sum_" + size)
-                    nc.scalar.activation(
-                        out=e_columns(tau, h, part), in_=unit[size], func=ACT.Exp,
-                        bias=unit["bias"][:], scale=scale, accum_out=per_tile[tau]["sum_" + size][:, h : h + 1],
-                    )
+            b, s = divmod(n, SLOTS)
+            unit = per_unit.pop(n)
+            quad = per_quad[n // QUAD]
+            k = n % QUAD
+            if k == 0:
+                quad["sum_big"] = quad_stats.tile([P, QUAD], F32, name="sum_big", tag="sum_big")
+                quad["sum_small"] = quad_stats.tile([P, QUAD], F32, name="sum_small", tag="sum_small")
+                if n == 0:
+                    nc.vector.memset(quad["sum_big"][:], 0.0)
+            if "big" in unit:
+                n_slots = SLOTS if b > 0 else s
+                nc.scalar.activation(
+                    out=run_of_columns(e_main[n % RING][:], 0, n_slots),
+                    in_=unit["big"][:, : n_slots * GROUP].rearrange("q (p u e) -> q u p e", u=2, e=2),
+                    func=ACT.Exp, bias=unit["bias"][:], scale=scale, accum_out=quad["sum_big"][:, k : k + 1],
+                )
+            nc.scalar.activation(
+                out=run_of_columns(e_shared[b % 2][:], s, 1),
+                in_=quad["small"][:, k, :].rearrange("q (p u e) -> q u p e", u=2, e=2),
+                func=ACT.Exp, bias=unit["bias"][:], scale=scale, accum_out=quad["sum_small"][:, k : k + 1],
+            )
 
-        def e_passes(tau, h):
-            r = tau % 2
-            if is_early(tau):
-                return [e_early[r][h][:]] if tau >= TILES else []
-            return [e_late[r][h][:, :BLOCK], e_late[r][h][:, BLOCK:]]
+        def add_sums(quad):
+            total = quad_stats.tile([P, QUAD], F32, name="total", tag="total")
+            nc.gpsimd.tensor_tensor(
+                out=total[:], in0=per_quad[quad]["sum_big"][:], in1=per_quad[quad]["sum_small"][:], op=ALU.add
+            )
+            per_quad[quad]["total"] = total
 
-        def flip_e(n):
-            tau, h = unit_at(n)
-            if e_passes(tau, h):
-                per_unit[(tau, h)]["stage"] = flip_rows(e_passes(tau, h), True, work, "work")
+        def invert_sums(quad):
+            inverse = quad_stats.tile([P, QUAD], F32, name="inverse", tag="inverse")
+            nc.vector.reciprocal(out=inverse[:], in_=per_quad[quad]["total"][:])
+            per_quad[quad]["inverse"] = inverse
 
-        def group_e(n):
-            tau, h = unit_at(n)
-            if e_passes(tau, h):
-                per_unit[(tau, h)]["stage"] = group_words(per_unit[(tau, h)]["stage"], len(e_passes(tau, h)), e_pack)
-
-        def quantise_e(n):
-            tau, h = unit_at(n)
-            if e_passes(tau, h):
-                per_unit[(tau, h)]["stage"] = quantise(per_unit[(tau, h)]["stage"], len(e_passes(tau, h)), e_pack)
-
-        def multiply_values(tau):
-            b = tau // TILES
-            late = tau + 2 if is_early(tau) else tau
-            o_acc = aux.tile([P, HEADS, D], F32, name="o_acc", tag="aux")
-            for h in range(HEADS):
-                late_codes, late_scales = per_unit[(late, h)]["stage"]
-                shared = (late_codes[:, P:], late_scales[:, P:])
+        def multiply_values(quad):
+            o_acc = aux.tile([P, QUAD, D], F32, name="o_acc", tag="aux")
+            for u in range(QUAD):
+                n = quad * QUAD + u
+                b, s = divmod(n, SLOTS)
                 products = []
-                if is_early(tau):
+                if n > 0:
+                    codes, planes = packed[("main", n // 2)]
+                    g = n % 2 if n > 1 else 0
+                    main = (codes[:, g * P : (g + 1) * P], planes[:, g * P : (g + 1) * P])
+                    if s > 0:
+                        products.append(main + (v_codes[:, b, :], v_planes[b % 3][:, s - 1, 0, :].bitcast(U8)))
                     if b > 0:
-                        early_codes, early_scales = per_unit[(tau, h)]["stage"]
-                        products.append((early_codes[:], early_scales[:], v_codes[:, b - 1, :], v_scales[:, b - 1, :]))
-                    products.append(shared + (half_codes[:, 0, b, :], half_scales[:, 0, b, :]))
-                else:
-                    products.append((late_codes[:, :P], late_scales[:, :P], v_codes[:, b, :], v_scales[:, b, :]))
-                    if b > 0:
-                        products.append(shared + (half_codes[:, 1, b - 1, :], half_scales[:, 1, b - 1, :]))
-                multiply(o_acc[:, h, :], products)
-            per_tile[tau]["o_acc"] = o_acc
+                        products.append(main + (v_codes[:, b - 1, :], v_planes[(b - 1) % 3][:, s, 2, :].bitcast(U8)))
+                codes, planes = packed[("shared", flush_of(n))]
+                products.append((codes[:], planes[:], v_codes[:, b, :], v_planes[b % 3][:, s, 1, :].bitcast(U8)))
+                multiply(o_acc[:, u, :], products)
+            per_quad[quad]["o_acc"] = o_acc
 
-        def add_sums(tau):
-            sums = per_tile[tau]
-            if "sum_big" in sums and "sum_small" in sums:
-                total = tile_stats.tile([P, HEADS], F32, name="total", tag="total")
-                nc.gpsimd.tensor_tensor(out=total[:], in0=sums["sum_big"][:], in1=sums["sum_small"][:], op=ALU.add)
-            else:
-                total = sums["sum_big"] if "sum_big" in sums else sums["sum_small"]
-            sums["total"] = total
-
-        def invert_sums(tau):
-            inverse = tile_stats.tile([P, HEADS], F32, name="inverse", tag="inverse")
-            nc.vector.reciprocal(out=inverse[:], in_=per_tile[tau]["total"][:])
-            per_tile[tau]["inverse"] = inverse
-
-        def divide_and_store(tau):
-            result = results.tile([P, HEADS, D], F32, name="result", tag="result")
+        def divide_and_store(quad):
+            result = results.tile([P, QUAD, D], F32, name="result", tag="result")
+            stats_of = per_quad.pop(quad)
             nc.vector.tensor_tensor(
-                out=result[:], in0=per_tile[tau]["o_acc"][:],
-                in1=per_tile[tau]["inverse"][:].unsqueeze(2).to_broadcast([P, HEADS, D]), op=ALU.mult,
+                out=result[:], in0=stats_of["o_acc"][:],
+                in1=stats_of["inverse"][:].unsqueeze(2).to_broadcast([P, QUAD, D]), op=ALU.mult,
             )
+            rows = QUAD * P
             nc.sync.dma_start(
-                out=out_rows[tau * P : (tau + 1) * P, :], in_=result[:].rearrange("p h d -> p (h d)")
+                out=out_rows[quad * rows : (quad + 1) * rows, :].rearrange("(u p) d -> p u d", p=P), in_=result[:]
             )
 
-        def tile_ending_at(n):
-            if 0 <= n < N_UNITS and n % HEADS == HEADS - 1:
-                return unit_at(n)[0]
-            return None
+        def flush_of(n):
+            b, s = divmod(n, SLOTS)
+            last = SLOTS - 1 if b + 1 < N_BLOCKS else max(s // QUAD * QUAD + QUAD - 1, SLOTS // 2 - 1)
+            return b * SLOTS + last
 
-        def late_tile_ending_at(n):
-            tau = tile_ending_at(n)
-            return tau if tau is not None and not is_early(tau) else None
+        flips = {}
+        flips[0] = (("wv",), hidden_passes(wv_in[:]), "wv", 1)
+        for pair in range(N_UNITS // 2):
+            units = [n for n in (2 * pair, 2 * pair + 1) if n > 0]
+            flips[2 * pair + 2] = (("main", pair), [e_main[n % RING][:] for n in units], "main%d" % len(units), 16)
+        for b in range(N_BLOCKS):
+            for slot in range(4):
+                step = 2 * (4 * b + slot) + 1 if b < 2 else (b - 1) * SLOTS + 4 * slot + 3
+                flips[step] = (("x", b, slot), hidden_passes(x_in[b][:, slot, :]), "x", 8)
+        for n in sorted(set([flush_of(n) for n in range(N_UNITS)])):
+            flips[n + 2] = (("shared", n), [e_shared[n // SLOTS % 2][:]], "shared", 3)
+
+        product_quads = {}
+        step = 0
+        for quad in range(N_UNITS // QUAD):
+            apart = QUAD if quad * QUAD < N_UNITS - 2 * SLOTS else 2
+            step = max(flush_of(quad * QUAD) + 5, step + apart)
+            product_quads[step] = quad
+        last_step = step + 1
+
+        prepares = {10: [(project_values, 0)]}
+        for b in range(N_BLOCKS):
+            if b > 0:
+                prepares.setdefault(b * SLOTS + 2, []).append((project_values, b))
+            if b + 1 < N_BLOCKS:
+                prepares.setdefault(b * SLOTS + 6, []).append((prepare_keys, b + 1))
+                prepares.setdefault(b * SLOTS + (10 if b > 0 else 12), []).append((prepare_queries, b + 1, 0))
+                prepares.setdefault(b * SLOTS + 14, []).append((prepare_queries, b + 1, 1))
 
         with tc.manual_schedule():
-            wv_grouped = group_words(flip_rows(hidden_passes(wv_in[:]), False, bigs, "big"), HID_PASSES, keep)
-            wv_codes, wv_scales = quantise(wv_grouped, HID_PASSES, keep)
-            n_slots = 4 * N_BLOCKS
-            for j in range(n_slots + 3):
-                if j < n_slots:
-                    flip_x(*divmod(j, 4))
-                if 0 <= j - 1 < n_slots:
-                    group_x(*divmod(j - 1, 4))
-                if 0 <= j - 2 < n_slots:
-                    quantise_x(*divmod(j - 2, 4))
-                if j >= 3 and (j - 3) % 4 == 3:
-                    project_values((j - 3) // 4)
-                if j == n_slots // 2:
-                    prepare_keys(0)
-                    prepare_queries(0, 0)
-                    prepare_queries(0, 1)
-                    for n in range(AHEAD):
-                        scores_and_maxima(n)
-                        make_bias(n)
-            copy_value_halves()
-
-            for n in range(N_UNITS + 9):
+            prepare_keys(0)
+            prepare_queries(0, 0)
+            for n in range(AHEAD):
+                scores_and_maxima(n)
+                make_bias(n)
+            prepare_queries(0, 1)
+            moves = []
+            flipped = {}
+            grouped = {}
+            for n in range(last_step + 1):
                 if n < N_UNITS:
                     exponentials(n)
-                if late_tile_ending_at(n - 6) is not None:
-                    divide_and_store(late_tile_ending_at(n - 6) - 2)
-                if late_tile_ending_at(n - 8) is not None:
-                    divide_and_store(late_tile_ending_at(n - 8))
+                if n - 1 in product_quads:
+                    divide_and_store(product_quads[n - 1])
                 if n + AHEAD < N_UNITS:
                     scores_and_maxima(n + AHEAD)
                     make_bias(n + AHEAD)
-                if tile_ending_at(n - 2) is not None:
-                    add_sums(tile_ending_at(n - 2))
-                if 0 <= n - 3 < N_UNITS:
-                    quantise_e(n - 3)
-                if tile_ending_at(n - 3) is not None:
-                    invert_sums(tile_ending_at(n - 3))
-                if 0 <= n - 2 < N_UNITS:
-                    group_e(n - 2)
-                if 0 <= n - 1 < N_UNITS:
-                    flip_e(n - 1)
-                if late_tile_ending_at(n - 5) is not None:
-                    multiply_values(late_tile_ending_at(n - 5) - 2)
-                if late_tile_ending_at(n - 7) is not None:
-                    multiply_values(late_tile_ending_at(n - 7))
-                b, step = divmod(n, TILES * HEADS)
-                if b + 1 < N_BLOCKS and step % 8 in (1, 3):
-                    part = 2 * (step // 8) + (step % 8) // 2
-                    if part == 0:
-                        prepare_keys(b + 1)
-                    elif part <= 2:
-                        prepare_queries(b + 1, part - 1)
+                if n % QUAD == 1 and 0 <= n - 5 < N_UNITS:
+                    add_sums((n - 5) // QUAD)
+                if n - 2 in flips:
+                    key, passes, kind, bufs = flips[n - 2]
+                    packed[key] = quantise(grouped.pop(n - 2), len(passes), kind, bufs)
+                if n % QUAD == 2 and 0 <= n - 6 < N_UNITS:
+                    invert_sums((n - 6) // QUAD)
+                if n - 1 in flips:
+                    grouped[n - 1] = group_words(flipped.pop(n - 1), len(flips[n - 1][1]))
+                if n in flips:
+                    flipped[n] = flip_rows(flips[n][1])
+                if n in product_quads:
+                    multiply_values(product_quads[n])
+                for call in prepares.get(n - 1, []):
+                    if call[0] is project_values:
+                        quantise_values(call[1])
+                        moves.extend(plane_moves(call[1]))
+                for call in prepares.get(n, []):
+                    call[0](*call[1:])
+                for move in moves[:3]:
+                    move()
+                moves = moves[3:]

@@ -122,9 +122,10 @@ def tile_localgqattention_pb_t_kernel(tc, q_rot, k_rot, x, wv, out):
         v_codes = keep.tile([P, N_BLOCKS, D], U32, name="v_codes", align_bytes=64)
         v_scales = keep.tile([P, N_BLOCKS, D], U8, name="v_scales", align_bytes=64)
         nc.gpsimd.memset(v_scales[:].bitcast(I32), 0)
-        v_planes = [keep.tile([P, SLOTS, 3, D // 4], I32, name="v_planes%d" % i, align_bytes=64) for i in range(3)]
-        for planes in v_planes:
-            nc.gpsimd.memset(planes[:].rearrange("p s k w -> p (s k w)"), 0)
+        part_planes = [keep.tile([P, 2 * SLOTS, D // 4], I32, name="part_planes%d" % i, align_bytes=64) for i in range(3)]
+        diag_planes = [keep.tile([P, SLOTS, D // 4], I32, name="diag_planes%d" % i, align_bytes=64) for i in range(3)]
+        for planes in part_planes + diag_planes:
+            nc.gpsimd.memset(planes[:].rearrange("p s w -> p (s w)"), 0)
 
         def flip_rows(passes):
             flipped = work.tile([P, 4, P], F32, name="flipped", tag="work")
@@ -205,30 +206,15 @@ def tile_localgqattention_pb_t_kernel(tc, q_rot, k_rot, x, wv, out):
                 in_=v_stage.pop(b)[:].rearrange("p d s -> p (d s)"),
             )
 
-        def plane_moves(b):
-            moves = []
+        def spread_scales(b):
             source = v_scales[:, b, :].bitcast(I32)
-            planes = v_planes[b % 3]
-
-            def copy(lo, hi, dest):
-                moves.append(lambda: nc.gpsimd.tensor_copy(
-                    out=dest, in_=source[lo:hi].unsqueeze(1).to_broadcast([hi - lo, dest.shape[1], D // 4])
-                ))
-
-            def clear(dest):
-                moves.append(lambda: nc.gpsimd.memset(dest, 0))
-
-            for a in range(TILES):
-                rows = slice(32 * a, 32 * a + 4)
-                copy(32 * a, 32 * a + 4, planes[rows, : 4 * a + 4, 2, :])
-                if a + 1 < TILES:
-                    copy(32 * a, 32 * a + 4, planes[rows, 4 * a + 4 :, 0, :])
             for s in range(SLOTS):
-                a, r = divmod(s, 4)
-                copy(32 * a, 32 * a + r + 1, planes[32 * a : 32 * a + r + 1, s, 0:2, :])
-                if r:
-                    clear(planes[32 * a : 32 * a + r, s, 1:3, :])
-            return moves
+                row = 32 * (s // 4) + s % 4
+                nc.sync.dma_start(
+                    out=part_planes[b % 3][row : row + 1, s + 1 : s + 1 + SLOTS, :],
+                    in_=source[row : row + 1].unsqueeze(1).to_broadcast([1, SLOTS, D // 4]),
+                )
+                nc.sync.dma_start(out=diag_planes[b % 3][row : row + 1, s, :], in_=source[row : row + 1])
 
         per_quad = {}
         per_unit = {}
@@ -346,11 +332,11 @@ def tile_localgqattention_pb_t_kernel(tc, q_rot, k_rot, x, wv, out):
                     g = n % 2 if n > 1 else 0
                     main = (codes[:, g * P : (g + 1) * P], planes[:, g * P : (g + 1) * P])
                     if s > 0:
-                        products.append(main + (v_codes[:, b, :], v_planes[b % 3][:, s - 1, 0, :].bitcast(U8)))
+                        products.append(main + (v_codes[:, b, :], part_planes[b % 3][:, s, :].bitcast(U8)))
                     if b > 0:
-                        products.append(main + (v_codes[:, b - 1, :], v_planes[(b - 1) % 3][:, s, 2, :].bitcast(U8)))
+                        products.append(main + (v_codes[:, b - 1, :], part_planes[(b - 1) % 3][:, SLOTS + s, :].bitcast(U8)))
                 codes, planes = packed[("shared", flush_of(n))]
-                products.append((codes[:], planes[:], v_codes[:, b, :], v_planes[b % 3][:, s, 1, :].bitcast(U8)))
+                products.append((codes[:], planes[:], v_codes[:, b, :], diag_planes[b % 3][:, s, :].bitcast(U8)))
                 multiply(o_acc[:, u, :], products)
             per_quad[quad]["o_acc"] = o_acc
 
@@ -407,7 +393,6 @@ def tile_localgqattention_pb_t_kernel(tc, q_rot, k_rot, x, wv, out):
                 scores_and_maxima(n)
                 make_bias(n)
             prepare_queries(0, 1)
-            moves = []
             flipped = {}
             grouped = {}
             for n in range(last_step + 1):
@@ -434,9 +419,6 @@ def tile_localgqattention_pb_t_kernel(tc, q_rot, k_rot, x, wv, out):
                 for call in prepares.get(n - 1, []):
                     if call[0] is project_values:
                         quantise_values(call[1])
-                        moves.extend(plane_moves(call[1]))
+                        spread_scales(call[1])
                 for call in prepares.get(n, []):
                     call[0](*call[1:])
-                for move in moves[:3]:
-                    move()
-                moves = moves[3:]

@@ -47,7 +47,7 @@ def tile_localgqattention_pb_t_kernel(tc, q_rot, k_rot, x, wv, out):
         tc.tile_pool(name="queries", bufs=3) as queries,
         tc.tile_pool(name="packs", bufs=3) as packs,
         tc.tile_pool(name="stats", bufs=6) as stats,
-        tc.tile_pool(name="quad_stats", bufs=12) as quad_stats,
+        tc.tile_pool(name="quad_stats", bufs=3) as quad_stats,
         tc.tile_pool(name="results", bufs=4) as results,
         tc.psum_pool(name="bigs", bufs=3) as bigs,
         tc.psum_pool(name="smalls", bufs=2) as smalls,
@@ -70,25 +70,20 @@ def tile_localgqattention_pb_t_kernel(tc, q_rot, k_rot, x, wv, out):
                 in_=q_rows[first : first + 2 * P, :].rearrange("(c p) f -> p c f", p=P),
             )
 
-        def load_hidden(b):
-            nc.sync.dma_start(
-                out=x_in[b][:], in_=x_rows[b * BLOCK : (b + 1) * BLOCK, :].rearrange("(p j) f -> p j f", j=4)
-            )
+        def load_hidden(b, first, last):
+            rows = x_rows[b * BLOCK : (b + 1) * BLOCK, :].rearrange("(p j) f -> p j f", j=4)
+            nc.sync.dma_start(out=x_in[b][:, first:last, :], in_=rows[:, first:last, :])
 
         load_keys(0)
         load_queries(0, 0)
         nc.sync.dma_start(out=wv_in[:], in_=wv)
         load_queries(0, 1)
-        load_hidden(0)
+        load_hidden(0, 0, 2)
+        load_hidden(0, 2, 4)
         load_keys(1)
-        load_hidden(1)
+        load_hidden(1, 0, 4)
         load_queries(1, 0)
         load_queries(1, 1)
-        for b in range(2, N_BLOCKS):
-            load_hidden(b)
-            load_keys(b)
-            load_queries(b, 0)
-            load_queries(b, 1)
 
         ident_bf = keep.tile([P, P], BF16, name="ident_bf")
         make_identity(nc, ident_bf[:])
@@ -124,8 +119,12 @@ def tile_localgqattention_pb_t_kernel(tc, q_rot, k_rot, x, wv, out):
         nc.gpsimd.memset(v_scales[:].bitcast(I32), 0)
         part_planes = [keep.tile([P, 2 * SLOTS, D // 4], I32, name="part_planes%d" % i, align_bytes=64) for i in range(3)]
         diag_planes = [keep.tile([P, SLOTS, D // 4], I32, name="diag_planes%d" % i, align_bytes=64) for i in range(3)]
-        for planes in part_planes + diag_planes:
-            nc.gpsimd.memset(planes[:].rearrange("p s w -> p (s w)"), 0)
+
+        def clear_planes(engine, i):
+            for planes in (part_planes[i], diag_planes[i]):
+                engine.memset(planes[:].rearrange("p s w -> p (s w)"), 0)
+
+        clear_planes(nc.gpsimd, 0)
 
         def flip_rows(passes):
             flipped = work.tile([P, 4, P], F32, name="flipped", tag="work")
@@ -164,7 +163,7 @@ def tile_localgqattention_pb_t_kernel(tc, q_rot, k_rot, x, wv, out):
             k_flip = aux.tile([P, TILES, P], BF16, name="k_flip", tag="aux")
             for c in range(TILES):
                 nc.tensor.transpose(k_flip[:, c, :], k_in[b][:, c, :], ident_bf[:])
-            nc.vector.tensor_copy(
+            return lambda: nc.vector.tensor_copy(
                 out=keys_t[:, b * BLOCK : (b + 1) * BLOCK], in_=k_flip[:].rearrange("p c r -> p (c r)")
             )
 
@@ -176,7 +175,7 @@ def tile_localgqattention_pb_t_kernel(tc, q_rot, k_rot, x, wv, out):
                 for h in range(HEADS):
                     nc.tensor.transpose(q_flip[:, cc, h, :], q_in[b][:, 2 * half + cc, h * D : (h + 1) * D], ident_bf[:])
             n = 2 * P * HEADS
-            nc.vector.tensor_copy(
+            return lambda: nc.vector.tensor_copy(
                 out=queries_t[b][:, half * n : (half + 1) * n].rearrange("p (c r h) -> p c r h", c=2, h=HEADS),
                 in_=q_flip[:].rearrange("p c h r -> p c r h"),
             )
@@ -184,7 +183,7 @@ def tile_localgqattention_pb_t_kernel(tc, q_rot, k_rot, x, wv, out):
         def hidden_passes(rows_bf16):
             return [rows_bf16[:, g * BLOCK : (g + 1) * BLOCK] for g in range(HID_PASSES)]
 
-        v_stage = {}
+        stage = {}
 
         def project_values(b):
             v_acc = aux.tile([P, 4, D], F32, name="v_acc", tag="aux")
@@ -196,14 +195,18 @@ def tile_localgqattention_pb_t_kernel(tc, q_rot, k_rot, x, wv, out):
                      wv_codes[:, g * P : (g + 1) * P], wv_scales[:, g * P : (g + 1) * P])
                     for g in range(HID_PASSES)
                 ])
-            v_grouped = packs.tile([P, D, 4], BF16, name="v_grouped", tag="v_grouped", bufs=2, align_bytes=64)
-            nc.vector.tensor_copy(out=v_grouped[:], in_=v_acc[:].rearrange("p s d -> p d s"))
-            v_stage[b] = v_grouped
+
+            def copy_values():
+                v_grouped = packs.tile([P, D, 4], BF16, name="v_grouped", tag="v_grouped", bufs=2, align_bytes=64)
+                nc.vector.tensor_copy(out=v_grouped[:], in_=v_acc[:].rearrange("p s d -> p d s"))
+                stage[b] = v_grouped
+
+            return copy_values
 
         def quantise_values(b):
             nc.vector.quantize_mx(
                 out=v_codes[:, b, :].bitcast(FP8X4), scales=v_scales[:, b, :],
-                in_=v_stage.pop(b)[:].rearrange("p d s -> p (d s)"),
+                in_=stage.pop(b)[:].rearrange("p d s -> p (d s)"),
             )
 
         def spread_scales(b):
@@ -218,6 +221,7 @@ def tile_localgqattention_pb_t_kernel(tc, q_rot, k_rot, x, wv, out):
 
         per_quad = {}
         per_unit = {}
+        sums = {}
 
         def run_of_columns(tile_ap, first, n_slots):
             halves = tile_ap.rearrange("q (u w) -> q u w", u=2)
@@ -225,9 +229,9 @@ def tile_localgqattention_pb_t_kernel(tc, q_rot, k_rot, x, wv, out):
 
         def small_scores(quad):
             b = quad * QUAD // SLOTS
-            small = smalls.tile([P, QUAD, GROUP], F32, name="small", tag="small")
+            small = smalls.tile([P, QUAD, GROUP], F32, name="small", tag="small")[:]
             nc.tensor.matmul(
-                small[:].rearrange("p u k -> p (u k)"), lhsT=ident_bf[:],
+                small.rearrange("p u k -> p (u k)"), lhsT=ident_bf[:],
                 rhs=own_masks[:].rearrange("p u k -> p (u k)"), start=True, stop=False,
             )
             for u in range(QUAD):
@@ -237,9 +241,7 @@ def tile_localgqattention_pb_t_kernel(tc, q_rot, k_rot, x, wv, out):
                     small[:, u, :], lhsT=queries_t[b][:, s * P : (s + 1) * P],
                     rhs=keys_t[:, n * GROUP : (n + 1) * GROUP], start=False, stop=(u == QUAD - 1),
                 )
-            top_small = stats.tile([P, QUAD], F32, name="top_small", tag="top_small")
-            nc.vector.reduce_max(out=top_small[:], in_=small[:], axis=AX.X)
-            per_quad[quad] = {"small": small, "top_small": top_small}
+            per_quad[quad] = {"small": small}
 
         def big_scores(n):
             b, s = divmod(n, SLOTS)
@@ -263,15 +265,23 @@ def tile_localgqattention_pb_t_kernel(tc, q_rot, k_rot, x, wv, out):
                 nc.tensor.matmul(
                     big[:, s * GROUP : (s + 1) * GROUP], lhsT=ident_bf[:], rhs=far_mask[:], start=False, stop=True,
                 )
-            top_big = stats.tile([P, 1], F32, name="top_big", tag="top_big")
-            nc.vector.reduce_max(out=top_big[:], in_=big[:, :cols], axis=AX.X)
             unit["big"] = big
-            unit["top_big"] = top_big
+            unit["cols"] = cols
 
-        def scores_and_maxima(n):
+        def scores(n):
             if n % QUAD == 0:
                 small_scores(n // QUAD)
             big_scores(n)
+
+        def maxima(n):
+            if n % QUAD == 0:
+                quad = per_quad[n // QUAD]
+                quad["top_small"] = stats.tile([P, QUAD], F32, name="top_small", tag="top_small")
+                nc.vector.reduce_max(out=quad["top_small"][:], in_=quad["small"], axis=AX.X)
+            unit = per_unit[n]
+            if "big" in unit:
+                unit["top_big"] = stats.tile([P, 1], F32, name="top_big", tag="top_big")
+                nc.vector.reduce_max(out=unit["top_big"][:], in_=unit["big"][:, : unit["cols"]], axis=AX.X)
 
         def make_bias(n):
             unit = per_unit[n]
@@ -291,35 +301,30 @@ def tile_localgqattention_pb_t_kernel(tc, q_rot, k_rot, x, wv, out):
             unit = per_unit.pop(n)
             quad = per_quad[n // QUAD]
             k = n % QUAD
-            if k == 0:
-                quad["sum_big"] = quad_stats.tile([P, QUAD], F32, name="sum_big", tag="sum_big")
-                quad["sum_small"] = quad_stats.tile([P, QUAD], F32, name="sum_small", tag="sum_small")
-                if n == 0:
-                    nc.vector.memset(quad["sum_big"][:], 0.0)
+            if s == 0:
+                sums[b] = [quad_stats.tile([P, SLOTS], F32, name="sum", tag="sum%d" % i) for i in range(4)]
+                if b == 0:
+                    nc.vector.memset(sums[b][0][:], 0.0)
             if "big" in unit:
                 n_slots = SLOTS if b > 0 else s
                 nc.scalar.activation(
                     out=run_of_columns(e_main[n % RING][:], 0, n_slots),
                     in_=unit["big"][:, : n_slots * GROUP].rearrange("q (p u e) -> q u p e", u=2, e=2),
-                    func=ACT.Exp, bias=unit["bias"][:], scale=scale, accum_out=quad["sum_big"][:, k : k + 1],
+                    func=ACT.Exp, bias=unit["bias"][:], scale=scale, accum_out=sums[b][0][:, s : s + 1],
                 )
             nc.scalar.activation(
                 out=run_of_columns(e_shared[b % 2][:], s, 1),
                 in_=quad["small"][:, k, :].rearrange("q (p u e) -> q u p e", u=2, e=2),
-                func=ACT.Exp, bias=unit["bias"][:], scale=scale, accum_out=quad["sum_small"][:, k : k + 1],
+                func=ACT.Exp, bias=unit["bias"][:], scale=scale, accum_out=sums[b][1][:, s : s + 1],
             )
 
-        def add_sums(quad):
-            total = quad_stats.tile([P, QUAD], F32, name="total", tag="total")
-            nc.gpsimd.tensor_tensor(
-                out=total[:], in0=per_quad[quad]["sum_big"][:], in1=per_quad[quad]["sum_small"][:], op=ALU.add
-            )
-            per_quad[quad]["total"] = total
+        def add_sums(b, units):
+            sum_big, sum_small, total, inverse = [s[:, units] for s in sums[b]]
+            nc.gpsimd.tensor_tensor(out=total, in0=sum_big, in1=sum_small, op=ALU.add)
 
-        def invert_sums(quad):
-            inverse = quad_stats.tile([P, QUAD], F32, name="inverse", tag="inverse")
-            nc.vector.reciprocal(out=inverse[:], in_=per_quad[quad]["total"][:])
-            per_quad[quad]["inverse"] = inverse
+        def invert_sums(b, units):
+            sum_big, sum_small, total, inverse = [s[:, units] for s in sums[b]]
+            nc.vector.reciprocal(out=inverse, in_=total)
 
         def multiply_values(quad):
             o_acc = aux.tile([P, QUAD, D], F32, name="o_acc", tag="aux")
@@ -342,10 +347,11 @@ def tile_localgqattention_pb_t_kernel(tc, q_rot, k_rot, x, wv, out):
 
         def divide_and_store(quad):
             result = results.tile([P, QUAD, D], F32, name="result", tag="result")
-            stats_of = per_quad.pop(quad)
+            o_acc = per_quad.pop(quad)["o_acc"]
+            b, s = divmod(quad * QUAD, SLOTS)
             nc.vector.tensor_tensor(
-                out=result[:], in0=stats_of["o_acc"][:],
-                in1=stats_of["inverse"][:].unsqueeze(2).to_broadcast([P, QUAD, D]), op=ALU.mult,
+                out=result[:], in0=o_acc[:],
+                in1=sums[b][3][:, s : s + QUAD].unsqueeze(2).to_broadcast([P, QUAD, D]), op=ALU.mult,
             )
             rows = QUAD * P
             nc.sync.dma_start(
@@ -375,7 +381,7 @@ def tile_localgqattention_pb_t_kernel(tc, q_rot, k_rot, x, wv, out):
             apart = QUAD if quad * QUAD < N_UNITS - 2 * SLOTS else 2
             step = max(flush_of(quad * QUAD) + 5, step + apart)
             product_quads[step] = quad
-        last_step = step + 1
+        last_step = step + 2
 
         prepares = {10: [(project_values, 0)]}
         for b in range(N_BLOCKS):
@@ -383,42 +389,62 @@ def tile_localgqattention_pb_t_kernel(tc, q_rot, k_rot, x, wv, out):
                 prepares.setdefault(b * SLOTS + 2, []).append((project_values, b))
             if b + 1 < N_BLOCKS:
                 prepares.setdefault(b * SLOTS + 6, []).append((prepare_keys, b + 1))
-                prepares.setdefault(b * SLOTS + (10 if b > 0 else 12), []).append((prepare_queries, b + 1, 0))
+                prepares.setdefault(b * SLOTS + (10 if b > 0 else 8), []).append((prepare_queries, b + 1, 0))
                 prepares.setdefault(b * SLOTS + 14, []).append((prepare_queries, b + 1, 1))
 
+        sum_spans = {}
+        for n in range(N_UNITS):
+            b, s = divmod(n, SLOTS)
+            span = SLOTS if b + 1 < N_BLOCKS else QUAD
+            if (s + 1) % span == 0:
+                sum_spans[n + 1] = (b, slice(s + 1 - span, s + 1))
+
         with tc.manual_schedule():
-            prepare_keys(0)
-            prepare_queries(0, 0)
+            prepare_keys(0)()
+            prepare_queries(0, 0)()
             for n in range(AHEAD):
-                scores_and_maxima(n)
-                make_bias(n)
-            prepare_queries(0, 1)
+                scores(n)
+            maxima(0)
+            make_bias(0)
+            prepare_queries(0, 1)()
             flipped = {}
             grouped = {}
+            copies = []
             for n in range(last_step + 1):
                 if n < N_UNITS:
                     exponentials(n)
-                if n - 1 in product_quads:
-                    divide_and_store(product_quads[n - 1])
+                if n in (2, 4):
+                    clear_planes(nc.vector, n // 2)
+                if n + 1 < N_UNITS:
+                    maxima(n + 1)
+                    make_bias(n + 1)
+                if n - 2 in product_quads:
+                    divide_and_store(product_quads[n - 2])
+                for copy in copies:
+                    copy()
                 if n + AHEAD < N_UNITS:
-                    scores_and_maxima(n + AHEAD)
-                    make_bias(n + AHEAD)
-                if n % QUAD == 1 and 0 <= n - 5 < N_UNITS:
-                    add_sums((n - 5) // QUAD)
+                    scores(n + AHEAD)
+                if n in sum_spans:
+                    add_sums(*sum_spans[n])
                 if n - 2 in flips:
                     key, passes, kind, bufs = flips[n - 2]
                     packed[key] = quantise(grouped.pop(n - 2), len(passes), kind, bufs)
-                if n % QUAD == 2 and 0 <= n - 6 < N_UNITS:
-                    invert_sums((n - 6) // QUAD)
+                if n - 1 in sum_spans:
+                    invert_sums(*sum_spans[n - 1])
                 if n - 1 in flips:
                     grouped[n - 1] = group_words(flipped.pop(n - 1), len(flips[n - 1][1]))
                 if n in flips:
                     flipped[n] = flip_rows(flips[n][1])
                 if n in product_quads:
                     multiply_values(product_quads[n])
-                for call in prepares.get(n - 1, []):
+                for call in prepares.get(n - 2, []):
                     if call[0] is project_values:
                         quantise_values(call[1])
                         spread_scales(call[1])
-                for call in prepares.get(n, []):
-                    call[0](*call[1:])
+                copies = [call[0](*call[1:]) for call in prepares.get(n, [])]
+                b, s = divmod(n, SLOTS)
+                if b + 2 < N_BLOCKS and s == 0:
+                    load_hidden(b + 2, 0, 4)
+                    load_keys(b + 2)
+                    load_queries(b + 2, 0)
+                    load_queries(b + 2, 1)

@@ -23,10 +23,11 @@ TILES = BLOCK // P
 N_BLOCKS = T // BLOCK
 GROUP = 32
 SLOTS = BLOCK // GROUP
+HALF = SLOTS // 2
 N_UNITS = T // GROUP
 QUAD = 4
 HID_PASSES = HID // BLOCK
-AHEAD = 2
+AHEAD = 3
 RING = 6
 MASKED = -1.0e30
 
@@ -37,7 +38,7 @@ def tile_localgqattention_pb_t_kernel(tc, q_rot, k_rot, x, wv, out):
     nc = tc.nc
     scale = 1.0 / math.sqrt(D)
 
-    q_rows = q_rot.rearrange("b t h d -> (b t) (h d)")
+    q_rows = q_rot.rearrange("b t h d -> (b t h) d")
     k_rows = k_rot.rearrange("b t h d -> (b t) (h d)")
     x_rows = x.flatten_outer_dims()
     out_rows = out.flatten_outer_dims().rearrange("t (h d) -> (t h) d", h=HEADS)
@@ -48,14 +49,13 @@ def tile_localgqattention_pb_t_kernel(tc, q_rot, k_rot, x, wv, out):
         tc.tile_pool(name="packs", bufs=3) as packs,
         tc.tile_pool(name="stats", bufs=6) as stats,
         tc.tile_pool(name="quad_stats", bufs=3) as quad_stats,
-        tc.tile_pool(name="results", bufs=4) as results,
+        tc.tile_pool(name="results", bufs=8) as results,
         tc.psum_pool(name="bigs", bufs=3) as bigs,
         tc.psum_pool(name="smalls", bufs=2) as smalls,
-        tc.psum_pool(name="work", bufs=2) as work,
-        tc.psum_pool(name="aux", bufs=1) as aux,
+        tc.psum_pool(name="work", bufs=3) as work,
     ):
         k_in = [keep.tile([P, TILES, D], BF16, name="k_in%d" % b) for b in range(N_BLOCKS)]
-        q_in = [keep.tile([P, TILES, HEADS * D], BF16, name="q_in%d" % b) for b in range(N_BLOCKS)]
+        q_in = [keep.tile([P, SLOTS, D], BF16, name="q_in%d" % b) for b in range(N_BLOCKS)]
         x_in = [keep.tile([P, 4, HID], BF16, name="x_in%d" % b) for b in range(N_BLOCKS)]
         wv_in = keep.tile([P, HID], BF16, name="wv_in")
 
@@ -64,10 +64,10 @@ def tile_localgqattention_pb_t_kernel(tc, q_rot, k_rot, x, wv, out):
             nc.sync.dma_start(out=k_in[b][:], in_=k_rows[rows, :].rearrange("(c p) d -> p c d", p=P))
 
         def load_queries(b, half):
-            first = b * BLOCK + half * 2 * P
+            first = (b * SLOTS + half * HALF) * P
             nc.sync.dma_start(
-                out=q_in[b][:, 2 * half : 2 * half + 2, :],
-                in_=q_rows[first : first + 2 * P, :].rearrange("(c p) f -> p c f", p=P),
+                out=q_in[b][:, half * HALF : (half + 1) * HALF, :],
+                in_=q_rows[first : first + HALF * P, :].rearrange("(u p) d -> p u d", p=P),
             )
 
         def load_hidden(b, first, last):
@@ -160,7 +160,7 @@ def tile_localgqattention_pb_t_kernel(tc, q_rot, k_rot, x, wv, out):
         packed = {}
 
         def prepare_keys(b):
-            k_flip = aux.tile([P, TILES, P], BF16, name="k_flip", tag="aux")
+            k_flip = work.tile([P, TILES, P], BF16, name="k_flip", tag="work")
             for c in range(TILES):
                 nc.tensor.transpose(k_flip[:, c, :], k_in[b][:, c, :], ident_bf[:])
             return lambda: nc.vector.tensor_copy(
@@ -170,14 +170,12 @@ def tile_localgqattention_pb_t_kernel(tc, q_rot, k_rot, x, wv, out):
         def prepare_queries(b, half):
             if half == 0:
                 queries_t[b] = queries.tile([P, BLOCK * HEADS], BF16, name="q_t", tag="q_t")
-            q_flip = aux.tile([P, 2, HEADS, P], BF16, name="q_flip", tag="aux")
-            for cc in range(2):
-                for h in range(HEADS):
-                    nc.tensor.transpose(q_flip[:, cc, h, :], q_in[b][:, 2 * half + cc, h * D : (h + 1) * D], ident_bf[:])
-            n = 2 * P * HEADS
+            q_flip = work.tile([P, HALF, P], BF16, name="q_flip", tag="work")
+            for u in range(HALF):
+                nc.tensor.transpose(q_flip[:, u, :], q_in[b][:, half * HALF + u, :], ident_bf[:])
             return lambda: nc.vector.tensor_copy(
-                out=queries_t[b][:, half * n : (half + 1) * n].rearrange("p (c r h) -> p c r h", c=2, h=HEADS),
-                in_=q_flip[:].rearrange("p c h r -> p c r h"),
+                out=queries_t[b][:, half * HALF * P : (half + 1) * HALF * P],
+                in_=q_flip[:].rearrange("p u r -> p (u r)"),
             )
 
         def hidden_passes(rows_bf16):
@@ -186,7 +184,7 @@ def tile_localgqattention_pb_t_kernel(tc, q_rot, k_rot, x, wv, out):
         stage = {}
 
         def project_values(b):
-            v_acc = aux.tile([P, 4, D], F32, name="v_acc", tag="aux")
+            v_acc = work.tile([P, 4, D], F32, name="v_acc", tag="work")
             wv_codes, wv_scales = packed[("wv",)]
             for slot in range(4):
                 x_codes, x_scales = packed.pop(("x", b, slot))
@@ -327,7 +325,7 @@ def tile_localgqattention_pb_t_kernel(tc, q_rot, k_rot, x, wv, out):
             nc.vector.reciprocal(out=inverse, in_=total)
 
         def multiply_values(quad):
-            o_acc = aux.tile([P, QUAD, D], F32, name="o_acc", tag="aux")
+            o_acc = work.tile([P, QUAD, D], F32, name="o_acc", tag="work")
             for u in range(QUAD):
                 n = quad * QUAD + u
                 b, s = divmod(n, SLOTS)
@@ -370,7 +368,7 @@ def tile_localgqattention_pb_t_kernel(tc, q_rot, k_rot, x, wv, out):
             flips[2 * pair + 2] = (("main", pair), [e_main[n % RING][:] for n in units], "main%d" % len(units), 16)
         for b in range(N_BLOCKS):
             for slot in range(4):
-                step = 2 * (4 * b + slot) + 1 if b < 2 else (b - 1) * SLOTS + 4 * slot + 3
+                step = 2 * (4 * b + slot) + 1 if b < 2 else (b - 1) * SLOTS + (3, 5, 7, 11)[slot]
                 flips[step] = (("x", b, slot), hidden_passes(x_in[b][:, slot, :]), "x", 8)
         for n in sorted(set([flush_of(n) for n in range(N_UNITS)])):
             flips[n + 2] = (("shared", n), [e_shared[n // SLOTS % 2][:]], "shared", 3)
@@ -383,14 +381,16 @@ def tile_localgqattention_pb_t_kernel(tc, q_rot, k_rot, x, wv, out):
             product_quads[step] = quad
         last_step = step + 2
 
-        prepares = {10: [(project_values, 0)]}
-        for b in range(N_BLOCKS):
-            if b > 0:
-                prepares.setdefault(b * SLOTS + 2, []).append((project_values, b))
-            if b + 1 < N_BLOCKS:
-                prepares.setdefault(b * SLOTS + 6, []).append((prepare_keys, b + 1))
-                prepares.setdefault(b * SLOTS + (10 if b > 0 else 8), []).append((prepare_queries, b + 1, 0))
-                prepares.setdefault(b * SLOTS + 14, []).append((prepare_queries, b + 1, 1))
+        prepares = {10: [(project_values, 0)], SLOTS + 2: [(project_values, 1)]}
+        for b in range(1, N_BLOCKS):
+            before = (b - 1) * SLOTS
+            prepares[before + 6] = [(prepare_keys, b)]
+            prepares[before + (8 if b == 1 else 10)] = [(prepare_queries, b, 0)]
+            if b == 1:
+                prepares[before + 14] = [(prepare_queries, b, 1)]
+            else:
+                prepares[before + 14] = [(project_values, b)]
+                prepares[before + SLOTS + 2] = [(prepare_queries, b, 1)]
 
         sum_spans = {}
         for n in range(N_UNITS):
@@ -404,8 +404,9 @@ def tile_localgqattention_pb_t_kernel(tc, q_rot, k_rot, x, wv, out):
             prepare_queries(0, 0)()
             for n in range(AHEAD):
                 scores(n)
-            maxima(0)
-            make_bias(0)
+            for n in range(2):
+                maxima(n)
+                make_bias(n)
             prepare_queries(0, 1)()
             flipped = {}
             grouped = {}
@@ -415,15 +416,13 @@ def tile_localgqattention_pb_t_kernel(tc, q_rot, k_rot, x, wv, out):
                     exponentials(n)
                 if n in (2, 4):
                     clear_planes(nc.vector, n // 2)
-                if n + 1 < N_UNITS:
-                    maxima(n + 1)
-                    make_bias(n + 1)
+                if n + 2 < N_UNITS:
+                    maxima(n + 2)
+                    make_bias(n + 2)
                 if n - 2 in product_quads:
                     divide_and_store(product_quads[n - 2])
                 for copy in copies:
                     copy()
-                if n + AHEAD < N_UNITS:
-                    scores(n + AHEAD)
                 if n in sum_spans:
                     add_sums(*sum_spans[n])
                 if n - 2 in flips:
@@ -435,6 +434,8 @@ def tile_localgqattention_pb_t_kernel(tc, q_rot, k_rot, x, wv, out):
                     grouped[n - 1] = group_words(flipped.pop(n - 1), len(flips[n - 1][1]))
                 if n in flips:
                     flipped[n] = flip_rows(flips[n][1])
+                if n + AHEAD < N_UNITS:
+                    scores(n + AHEAD)
                 if n in product_quads:
                     multiply_values(product_quads[n])
                 for call in prepares.get(n - 2, []):

@@ -27,7 +27,7 @@ HALF = SLOTS // 2
 N_UNITS = T // GROUP
 QUAD = 4
 HID_PASSES = HID // BLOCK
-AHEAD = 3
+AHEAD = 4
 RING = 6
 MASKED = -1.0e30
 
@@ -50,8 +50,8 @@ def tile_localgqattention_pb_t_kernel(tc, q_rot, k_rot, x, wv, out):
         tc.tile_pool(name="stats", bufs=6) as stats,
         tc.tile_pool(name="quad_stats", bufs=3) as quad_stats,
         tc.tile_pool(name="results", bufs=8) as results,
-        tc.psum_pool(name="bigs", bufs=3) as bigs,
-        tc.psum_pool(name="smalls", bufs=2) as smalls,
+        tc.psum_pool(name="bigs", bufs=4) as bigs,
+        tc.psum_pool(name="smalls", bufs=1) as smalls,
         tc.psum_pool(name="work", bufs=3) as work,
     ):
         k_in = [keep.tile([P, TILES, D], BF16, name="k_in%d" % b) for b in range(N_BLOCKS)]
@@ -211,11 +211,15 @@ def tile_localgqattention_pb_t_kernel(tc, q_rot, k_rot, x, wv, out):
             source = v_scales[:, b, :].bitcast(I32)
             for s in range(SLOTS):
                 row = 32 * (s // 4) + s % 4
-                nc.sync.dma_start(
-                    out=part_planes[b % 3][row : row + 1, s + 1 : s + 1 + SLOTS, :],
-                    in_=source[row : row + 1].unsqueeze(1).to_broadcast([1, SLOTS, D // 4]),
-                )
-                nc.sync.dma_start(out=diag_planes[b % 3][row : row + 1, s, :], in_=source[row : row + 1])
+                first = s + 1 if b > 0 else SLOTS
+                last = s + 1 + SLOTS if b + 1 < N_BLOCKS else SLOTS
+                if first < last:
+                    nc.sync.dma_start(
+                        out=part_planes[b % 3][row : row + 1, first:last, :],
+                        in_=source[row : row + 1].unsqueeze(1).to_broadcast([1, last - first, D // 4]),
+                    )
+                if b > 0:
+                    nc.sync.dma_start(out=diag_planes[b % 3][row : row + 1, s, :], in_=source[row : row + 1])
 
         per_quad = {}
         per_unit = {}
@@ -239,82 +243,76 @@ def tile_localgqattention_pb_t_kernel(tc, q_rot, k_rot, x, wv, out):
                     small[:, u, :], lhsT=queries_t[b][:, s * P : (s + 1) * P],
                     rhs=keys_t[:, n * GROUP : (n + 1) * GROUP], start=False, stop=(u == QUAD - 1),
                 )
-            per_quad[quad] = {"small": small}
+            per_quad[quad] = {"small_scores": small}
+
+        def copy_small(quad):
+            small = stats.tile([P, QUAD, GROUP], F32, name="small_copy", tag="small_copy")
+            nc.scalar.copy(out=small[:], in_=per_quad[quad].pop("small_scores"))
+            per_quad[quad]["small"] = small
 
         def big_scores(n):
             b, s = divmod(n, SLOTS)
-            unit = {}
-            per_unit[n] = unit
-            cols = BLOCK if b > 0 else s * GROUP
-            if cols == 0:
-                return
             big = bigs.tile([P, BLOCK], F32, name="big", tag="big")
             q_ap = queries_t[b][:, s * P : (s + 1) * P]
+            slot = slice(s * GROUP, (s + 1) * GROUP)
+            if b == 0:
+                nc.tensor.matmul(big[:, : slot.stop], lhsT=q_ap, rhs=keys_t[:, : slot.stop], start=True, stop=False)
+                nc.tensor.matmul(big[:, slot], lhsT=ident_bf[:], rhs=own_masks[:, 0, :], start=False, stop=True)
+                per_unit[n] = {"big": big[:, : slot.stop]}
+                return
             if s > 0:
                 nc.tensor.matmul(
-                    big[:, : s * GROUP], lhsT=q_ap, rhs=keys_t[:, b * BLOCK : b * BLOCK + s * GROUP],
+                    big[:, : slot.start], lhsT=q_ap, rhs=keys_t[:, b * BLOCK : b * BLOCK + slot.start],
                     start=True, stop=True,
                 )
-            if b > 0:
-                nc.tensor.matmul(
-                    big[:, s * GROUP :], lhsT=q_ap, rhs=keys_t[:, (n - SLOTS) * GROUP : b * BLOCK],
-                    start=True, stop=False,
-                )
-                nc.tensor.matmul(
-                    big[:, s * GROUP : (s + 1) * GROUP], lhsT=ident_bf[:], rhs=far_mask[:], start=False, stop=True,
-                )
-            unit["big"] = big
-            unit["cols"] = cols
+            nc.tensor.matmul(
+                big[:, slot.start :], lhsT=q_ap, rhs=keys_t[:, (n - SLOTS) * GROUP : b * BLOCK], start=True, stop=False,
+            )
+            nc.tensor.matmul(big[:, slot], lhsT=ident_bf[:], rhs=far_mask[:], start=False, stop=True)
+            per_unit[n] = {"big": big[:]}
 
-        def scores(n):
-            if n % QUAD == 0:
-                small_scores(n // QUAD)
-            big_scores(n)
 
         def maxima(n):
-            if n % QUAD == 0:
+            if n % QUAD == 0 and n >= SLOTS:
                 quad = per_quad[n // QUAD]
                 quad["top_small"] = stats.tile([P, QUAD], F32, name="top_small", tag="top_small")
-                nc.vector.reduce_max(out=quad["top_small"][:], in_=quad["small"], axis=AX.X)
+                nc.vector.reduce_max(out=quad["top_small"][:], in_=quad["small"][:], axis=AX.X)
             unit = per_unit[n]
-            if "big" in unit:
-                unit["top_big"] = stats.tile([P, 1], F32, name="top_big", tag="top_big")
-                nc.vector.reduce_max(out=unit["top_big"][:], in_=unit["big"][:, : unit["cols"]], axis=AX.X)
+            unit["top_big"] = stats.tile([P, 1], F32, name="top_big", tag="top_big")
+            nc.vector.reduce_max(out=unit["top_big"][:], in_=unit["big"], axis=AX.X)
 
         def make_bias(n):
             unit = per_unit[n]
-            top_small = per_quad[n // QUAD]["top_small"][:, n % QUAD : n % QUAD + 1]
             bias = stats.tile([P, 1], F32, name="bias", tag="bias")
-            if "big" in unit:
+            if n >= SLOTS:
+                top_small = per_quad[n // QUAD]["top_small"][:, n % QUAD : n % QUAD + 1]
                 nc.gpsimd.tensor_scalar(
                     out=bias[:], in0=unit["top_big"][:], scalar1=top_small, scalar2=-scale,
                     op0=ALU.max, op1=ALU.mult,
                 )
             else:
-                nc.gpsimd.tensor_scalar_mul(out=bias[:], in0=top_small, scalar1=-scale)
+                nc.gpsimd.tensor_scalar_mul(out=bias[:], in0=unit["top_big"][:], scalar1=-scale)
             unit["bias"] = bias
 
         def exponentials(n):
             b, s = divmod(n, SLOTS)
             unit = per_unit.pop(n)
-            quad = per_quad[n // QUAD]
-            k = n % QUAD
             if s == 0:
                 sums[b] = [quad_stats.tile([P, SLOTS], F32, name="sum", tag="sum%d" % i) for i in range(4)]
                 if b == 0:
-                    nc.vector.memset(sums[b][0][:], 0.0)
-            if "big" in unit:
-                n_slots = SLOTS if b > 0 else s
-                nc.scalar.activation(
-                    out=run_of_columns(e_main[n % RING][:], 0, n_slots),
-                    in_=unit["big"][:, : n_slots * GROUP].rearrange("q (p u e) -> q u p e", u=2, e=2),
-                    func=ACT.Exp, bias=unit["bias"][:], scale=scale, accum_out=sums[b][0][:, s : s + 1],
-                )
+                    nc.vector.memset(sums[b][1][:], 0.0)
+            n_slots = SLOTS if b > 0 else s + 1
             nc.scalar.activation(
-                out=run_of_columns(e_shared[b % 2][:], s, 1),
-                in_=quad["small"][:, k, :].rearrange("q (p u e) -> q u p e", u=2, e=2),
-                func=ACT.Exp, bias=unit["bias"][:], scale=scale, accum_out=sums[b][1][:, s : s + 1],
+                out=run_of_columns(e_main[n % RING][:], 0, n_slots),
+                in_=unit["big"].rearrange("q (p u e) -> q u p e", u=2, e=2),
+                func=ACT.Exp, bias=unit["bias"][:], scale=scale, accum_out=sums[b][0][:, s : s + 1],
             )
+            if b > 0:
+                nc.scalar.activation(
+                    out=run_of_columns(e_shared[b % 2][:], s, 1),
+                    in_=per_quad[n // QUAD]["small"][:, n % QUAD, :].rearrange("q (p u e) -> q u p e", u=2, e=2),
+                    func=ACT.Exp, bias=unit["bias"][:], scale=scale, accum_out=sums[b][1][:, s : s + 1],
+                )
 
         def add_sums(b, units):
             sum_big, sum_small, total, inverse = [s[:, units] for s in sums[b]]
@@ -329,19 +327,19 @@ def tile_localgqattention_pb_t_kernel(tc, q_rot, k_rot, x, wv, out):
             for u in range(QUAD):
                 n = quad * QUAD + u
                 b, s = divmod(n, SLOTS)
-                products = []
-                if n > 0:
-                    codes, planes = packed[("main", n // 2)]
-                    g = n % 2 if n > 1 else 0
-                    main = (codes[:, g * P : (g + 1) * P], planes[:, g * P : (g + 1) * P])
+                codes, planes = packed[("main", n // 2)]
+                g = n % 2
+                main = (codes[:, g * P : (g + 1) * P], planes[:, g * P : (g + 1) * P])
+                if b == 0:
+                    products = [main + (v_codes[:, 0, :], v_scales[:, 0, :])]
+                else:
+                    products = [main + (v_codes[:, b - 1, :], part_planes[(b - 1) % 3][:, SLOTS + s, :].bitcast(U8))]
                     if s > 0:
                         products.append(main + (v_codes[:, b, :], part_planes[b % 3][:, s, :].bitcast(U8)))
-                    if b > 0:
-                        products.append(main + (v_codes[:, b - 1, :], part_planes[(b - 1) % 3][:, SLOTS + s, :].bitcast(U8)))
-                codes, planes = packed[("shared", flush_of(n))]
-                products.append((codes[:], planes[:], v_codes[:, b, :], diag_planes[b % 3][:, s, :].bitcast(U8)))
+                    codes, planes = packed[("shared", flush_of(n))]
+                    products.append((codes[:], planes[:], v_codes[:, b, :], diag_planes[b % 3][:, s, :].bitcast(U8)))
                 multiply(o_acc[:, u, :], products)
-            per_quad[quad]["o_acc"] = o_acc
+            per_quad.setdefault(quad, {})["o_acc"] = o_acc
 
         def divide_and_store(quad):
             result = results.tile([P, QUAD, D], F32, name="result", tag="result")
@@ -362,22 +360,22 @@ def tile_localgqattention_pb_t_kernel(tc, q_rot, k_rot, x, wv, out):
             return b * SLOTS + last
 
         flips = {}
-        flips[0] = (("wv",), hidden_passes(wv_in[:]), "wv", 1)
+        flips[-1] = (("wv",), hidden_passes(wv_in[:]), "wv", 1)
         for pair in range(N_UNITS // 2):
-            units = [n for n in (2 * pair, 2 * pair + 1) if n > 0]
-            flips[2 * pair + 2] = (("main", pair), [e_main[n % RING][:] for n in units], "main%d" % len(units), 16)
+            flips[2 * pair + 2] = (("main", pair), [e_main[n % RING][:] for n in (2 * pair, 2 * pair + 1)], "main", 16)
         for b in range(N_BLOCKS):
             for slot in range(4):
                 step = 2 * (4 * b + slot) + 1 if b < 2 else (b - 1) * SLOTS + (3, 5, 7, 11)[slot]
                 flips[step] = (("x", b, slot), hidden_passes(x_in[b][:, slot, :]), "x", 8)
-        for n in sorted(set([flush_of(n) for n in range(N_UNITS)])):
+        for n in sorted(set([flush_of(n) for n in range(SLOTS, N_UNITS)])):
             flips[n + 2] = (("shared", n), [e_shared[n // SLOTS % 2][:]], "shared", 3)
 
         product_quads = {}
         step = 0
         for quad in range(N_UNITS // QUAD):
             apart = QUAD if quad * QUAD < N_UNITS - 2 * SLOTS else 2
-            step = max(flush_of(quad * QUAD) + 5, step + apart)
+            ready = flush_of(quad * QUAD) + 5 if quad * QUAD >= SLOTS else SLOTS
+            step = max(ready, step + apart)
             product_quads[step] = quad
         last_step = step + 2
 
@@ -401,19 +399,22 @@ def tile_localgqattention_pb_t_kernel(tc, q_rot, k_rot, x, wv, out):
 
         with tc.manual_schedule():
             prepare_keys(0)()
-            prepare_queries(0, 0)()
+            copy_queries = prepare_queries(0, 0)
+            grouped = {-1: group_words(flip_rows(flips[-1][1]), HID_PASSES)}
+            copy_queries()
             for n in range(AHEAD):
-                scores(n)
+                big_scores(n)
             for n in range(2):
                 maxima(n)
                 make_bias(n)
             prepare_queries(0, 1)()
             flipped = {}
-            grouped = {}
             copies = []
             for n in range(last_step + 1):
                 if n < N_UNITS:
                     exponentials(n)
+                if SLOTS <= n + 3 < N_UNITS and (n + 3) % QUAD == 0:
+                    copy_small((n + 3) // QUAD)
                 if n in (2, 4):
                     clear_planes(nc.vector, n // 2)
                 if n + 2 < N_UNITS:
@@ -430,12 +431,14 @@ def tile_localgqattention_pb_t_kernel(tc, q_rot, k_rot, x, wv, out):
                     packed[key] = quantise(grouped.pop(n - 2), len(passes), kind, bufs)
                 if n - 1 in sum_spans:
                     invert_sums(*sum_spans[n - 1])
-                if n - 1 in flips:
+                if n - 1 in flipped:
                     grouped[n - 1] = group_words(flipped.pop(n - 1), len(flips[n - 1][1]))
                 if n in flips:
                     flipped[n] = flip_rows(flips[n][1])
+                if SLOTS <= n + 4 < N_UNITS and n % QUAD == 0:
+                    small_scores((n + 4) // QUAD)
                 if n + AHEAD < N_UNITS:
-                    scores(n + AHEAD)
+                    big_scores(n + AHEAD)
                 if n in product_quads:
                     multiply_values(product_quads[n])
                 for call in prepares.get(n - 2, []):

@@ -87,6 +87,8 @@ def tile_localgqattention_pb_t_kernel(tc, q_rot, k_rot, x, wv, out):
 
         ident_bf = keep.tile([P, P], BF16, name="ident_bf")
         make_identity(nc, ident_bf[:])
+        idle_rows = keep.tile([P, BLOCK], BF16, name="idle_rows")
+        nc.vector.memset(idle_rows[:].bitcast(I32), 0)
 
         own_f32 = keep.tile([P, GROUP], F32, name="own_f32")
         nc.gpsimd.memset(own_f32[:], 0.0)
@@ -156,6 +158,10 @@ def tile_localgqattention_pb_t_kernel(tc, q_rot, k_rot, x, wv, out):
                     start=(g == 0), stop=(g == len(products) - 1),
                 )
 
+        def keep_busy(columns):
+            idle = smalls.tile([P, BLOCK], F32, name="idle", tag="small")
+            nc.tensor.matmul(idle[:, :columns], lhsT=ident_bf[:], rhs=idle_rows[:, :columns], start=True, stop=True)
+
         queries_t = {}
         packed = {}
 
@@ -222,6 +228,7 @@ def tile_localgqattention_pb_t_kernel(tc, q_rot, k_rot, x, wv, out):
                     nc.sync.dma_start(out=diag_planes[b % 3][row : row + 1, s, :], in_=source[row : row + 1])
 
         per_quad = {}
+        products_done = {}
         per_unit = {}
         sums = {}
 
@@ -322,10 +329,9 @@ def tile_localgqattention_pb_t_kernel(tc, q_rot, k_rot, x, wv, out):
             sum_big, sum_small, total, inverse = [s[:, units] for s in sums[b]]
             nc.vector.reciprocal(out=inverse, in_=total)
 
-        def multiply_values(quad):
-            o_acc = work.tile([P, QUAD, D], F32, name="o_acc", tag="work")
-            for u in range(QUAD):
-                n = quad * QUAD + u
+        def multiply_values(units):
+            o_acc = work.tile([P, len(units), D], F32, name="o_acc", tag="work")
+            for u, n in enumerate(units):
                 b, s = divmod(n, SLOTS)
                 codes, planes = packed[("main", n // 2)]
                 g = n % 2
@@ -339,19 +345,17 @@ def tile_localgqattention_pb_t_kernel(tc, q_rot, k_rot, x, wv, out):
                     codes, planes = packed[("shared", flush_of(n))]
                     products.append((codes[:], planes[:], v_codes[:, b, :], diag_planes[b % 3][:, s, :].bitcast(U8)))
                 multiply(o_acc[:, u, :], products)
-            per_quad.setdefault(quad, {})["o_acc"] = o_acc
+            products_done[units.start] = o_acc
 
-        def divide_and_store(quad):
-            result = results.tile([P, QUAD, D], F32, name="result", tag="result")
-            o_acc = per_quad.pop(quad)["o_acc"]
-            b, s = divmod(quad * QUAD, SLOTS)
+        def divide_and_store(units):
+            result = results.tile([P, len(units), D], F32, name="result", tag="result")
+            b, s = divmod(units.start, SLOTS)
             nc.vector.tensor_tensor(
-                out=result[:], in0=o_acc[:],
-                in1=sums[b][3][:, s : s + QUAD].unsqueeze(2).to_broadcast([P, QUAD, D]), op=ALU.mult,
+                out=result[:], in0=products_done.pop(units.start)[:],
+                in1=sums[b][3][:, s : s + len(units)].unsqueeze(2).to_broadcast([P, len(units), D]), op=ALU.mult,
             )
-            rows = QUAD * P
             nc.sync.dma_start(
-                out=out_rows[quad * rows : (quad + 1) * rows, :].rearrange("(u p) d -> p u d", p=P), in_=result[:]
+                out=out_rows[units.start * P : units.stop * P, :].rearrange("(u p) d -> p u d", p=P), in_=result[:]
             )
 
         def flush_of(n):
@@ -360,23 +364,27 @@ def tile_localgqattention_pb_t_kernel(tc, q_rot, k_rot, x, wv, out):
             return b * SLOTS + last
 
         flips = {}
-        flips[-1] = (("wv",), hidden_passes(wv_in[:]), "wv", 1)
+        flips[-1] = [(("wv",), hidden_passes(wv_in[:]), "wv", 1)]
         for pair in range(N_UNITS // 2):
-            flips[2 * pair + 2] = (("main", pair), [e_main[n % RING][:] for n in (2 * pair, 2 * pair + 1)], "main", 16)
+            flips[2 * pair + 2] = [(("main", pair), [e_main[n % RING][:] for n in (2 * pair, 2 * pair + 1)], "main", 16)]
         for b in range(N_BLOCKS):
             for slot in range(4):
                 step = 2 * (4 * b + slot) + 1 if b < 2 else (b - 1) * SLOTS + (3, 5, 7, 11)[slot]
-                flips[step] = (("x", b, slot), hidden_passes(x_in[b][:, slot, :]), "x", 8)
+                flips[step] = [(("x", b, slot), hidden_passes(x_in[b][:, slot, :]), "x", 8)]
         for n in sorted(set([flush_of(n) for n in range(SLOTS, N_UNITS)])):
-            flips[n + 2] = (("shared", n), [e_shared[n // SLOTS % 2][:]], "shared", 3)
+            step = n + 2 if n + 1 < N_UNITS else n + 1
+            flips.setdefault(step, []).append((("shared", n), [e_shared[n // SLOTS % 2][:]], "shared", 3))
 
-        product_quads = {}
+        products = {}
         step = 0
-        for quad in range(N_UNITS // QUAD):
-            apart = QUAD if quad * QUAD < N_UNITS - 2 * SLOTS else 2
-            ready = flush_of(quad * QUAD) + 5 if quad * QUAD >= SLOTS else SLOTS
+        for first in range(0, N_UNITS, QUAD):
+            apart = QUAD if first < N_UNITS - 2 * SLOTS else 2
+            ready = flush_of(first) + 5 if first >= SLOTS else SLOTS
+            if first >= N_UNITS - SLOTS:
+                ready = N_UNITS + QUAD - (N_UNITS - QUAD - first) // 2
             step = max(ready, step + apart)
-            product_quads[step] = quad
+            products[step] = [range(first, first + QUAD)]
+        products[step] = [range(first, first + QUAD // 2), range(first + QUAD // 2, first + QUAD)]
         last_step = step + 2
 
         prepares = {10: [(project_values, 0)], SLOTS + 2: [(project_values, 1)]}
@@ -398,9 +406,14 @@ def tile_localgqattention_pb_t_kernel(tc, q_rot, k_rot, x, wv, out):
                 sum_spans[n + 1] = (b, slice(s + 1 - span, s + 1))
 
         with tc.manual_schedule():
-            prepare_keys(0)()
+            for i in range(4):
+                keep_busy(BLOCK)
+            copy_keys = prepare_keys(0)
+            for i in range(1):
+                keep_busy(BLOCK)
+            copy_keys()
             copy_queries = prepare_queries(0, 0)
-            grouped = {-1: group_words(flip_rows(flips[-1][1]), HID_PASSES)}
+            grouped = {-1: [group_words(flip_rows(hidden_passes(wv_in[:])), HID_PASSES)]}
             copy_queries()
             for n in range(AHEAD):
                 big_scores(n)
@@ -420,27 +433,28 @@ def tile_localgqattention_pb_t_kernel(tc, q_rot, k_rot, x, wv, out):
                 if n + 2 < N_UNITS:
                     maxima(n + 2)
                     make_bias(n + 2)
-                if n - 2 in product_quads:
-                    divide_and_store(product_quads[n - 2])
+                for units in products.get(n - 2, []):
+                    divide_and_store(units)
                 for copy in copies:
                     copy()
                 if n in sum_spans:
                     add_sums(*sum_spans[n])
-                if n - 2 in flips:
-                    key, passes, kind, bufs = flips[n - 2]
-                    packed[key] = quantise(grouped.pop(n - 2), len(passes), kind, bufs)
+                for key, passes, kind, bufs in flips.get(n - 2, []):
+                    packed[key] = quantise(grouped[n - 2].pop(0), len(passes), kind, bufs)
                 if n - 1 in sum_spans:
                     invert_sums(*sum_spans[n - 1])
                 if n - 1 in flipped:
-                    grouped[n - 1] = group_words(flipped.pop(n - 1), len(flips[n - 1][1]))
+                    grouped[n - 1] = [group_words(words, len(flips[n - 1][i][1])) for i, words in enumerate(flipped.pop(n - 1))]
                 if n in flips:
-                    flipped[n] = flip_rows(flips[n][1])
+                    flipped[n] = [flip_rows(passes) for key, passes, kind, bufs in flips[n]]
                 if SLOTS <= n + 4 < N_UNITS and n % QUAD == 0:
                     small_scores((n + 4) // QUAD)
                 if n + AHEAD < N_UNITS:
                     big_scores(n + AHEAD)
-                if n in product_quads:
-                    multiply_values(product_quads[n])
+                if n + AHEAD < SLOTS - 1:
+                    keep_busy(BLOCK - (n + AHEAD + 1) * GROUP)
+                for units in products.get(n, []):
+                    multiply_values(units)
                 for call in prepares.get(n - 2, []):
                     if call[0] is project_values:
                         quantise_values(call[1])

@@ -26,6 +26,7 @@ SLOTS = BLOCK // GROUP
 HALF = SLOTS // 2
 N_UNITS = T // GROUP
 QUAD = 4
+OCTET = 8
 HID_PASSES = HID // BLOCK
 AHEAD = 4
 RING = 6
@@ -87,8 +88,6 @@ def tile_localgqattention_pb_t_kernel(tc, q_rot, k_rot, x, wv, out):
 
         ident_bf = keep.tile([P, P], BF16, name="ident_bf")
         make_identity(nc, ident_bf[:])
-        idle_rows = keep.tile([P, BLOCK], BF16, name="idle_rows")
-        nc.vector.memset(idle_rows[:].bitcast(I32), 0)
 
         own_f32 = keep.tile([P, GROUP], F32, name="own_f32")
         nc.gpsimd.memset(own_f32[:], 0.0)
@@ -104,15 +103,15 @@ def tile_localgqattention_pb_t_kernel(tc, q_rot, k_rot, x, wv, out):
         )
         ident_f32 = keep.tile([P, P], F32, name="ident_f32")
         make_identity(nc, ident_f32[:])
-        own_masks = keep.tile([P, QUAD, GROUP], BF16, name="own_masks")
-        for u in range(QUAD):
+        own_masks = keep.tile([P, OCTET, GROUP], BF16, name="own_masks")
+        for u in range(OCTET):
             nc.vector.tensor_copy(out=own_masks[:, u, :], in_=own_f32[:])
         far_mask = keep.tile([P, GROUP], BF16, name="far_mask")
         nc.vector.tensor_copy(out=far_mask[:], in_=far_f32[:])
 
         e_main = [keep.tile([P, BLOCK], BF16, name="e_main%d" % i) for i in range(RING)]
         e_shared = [keep.tile([P, BLOCK], BF16, name="e_shared%d" % i) for i in range(2)]
-        for e_tile in e_main + e_shared:
+        for e_tile in e_main:
             nc.vector.memset(e_tile[:].bitcast(I32), 0)
 
         keys_t = keep.tile([P, T], BF16, name="keys_t")
@@ -157,10 +156,6 @@ def tile_localgqattention_pb_t_kernel(tc, q_rot, k_rot, x, wv, out):
                     rhs=r_codes.bitcast(FP8X4), rhs_scale=r_scales,
                     start=(g == 0), stop=(g == len(products) - 1),
                 )
-
-        def keep_busy(columns):
-            idle = smalls.tile([P, BLOCK], F32, name="idle", tag="small")
-            nc.tensor.matmul(idle[:, :columns], lhsT=ident_bf[:], rhs=idle_rows[:, :columns], start=True, stop=True)
 
         queries_t = {}
         packed = {}
@@ -227,7 +222,7 @@ def tile_localgqattention_pb_t_kernel(tc, q_rot, k_rot, x, wv, out):
                 if b > 0:
                     nc.sync.dma_start(out=diag_planes[b % 3][row : row + 1, s, :], in_=source[row : row + 1])
 
-        per_quad = {}
+        per_octet = {}
         products_done = {}
         per_unit = {}
         sums = {}
@@ -236,26 +231,25 @@ def tile_localgqattention_pb_t_kernel(tc, q_rot, k_rot, x, wv, out):
             halves = tile_ap.rearrange("q (u w) -> q u w", u=2)
             return halves[:, :, first * GROUP // 2 : (first + n_slots) * GROUP // 2].rearrange("q u (p e) -> q u p e", e=2)
 
-        def small_scores(quad):
-            b = quad * QUAD // SLOTS
-            small = smalls.tile([P, QUAD, GROUP], F32, name="small", tag="small")[:]
+        def small_scores(octet):
+            small = smalls.tile([P, OCTET, GROUP], F32, name="small", tag="small")
             nc.tensor.matmul(
-                small.rearrange("p u k -> p (u k)"), lhsT=ident_bf[:],
+                small[:].rearrange("p u k -> p (u k)"), lhsT=ident_bf[:],
                 rhs=own_masks[:].rearrange("p u k -> p (u k)"), start=True, stop=False,
             )
-            for u in range(QUAD):
-                n = quad * QUAD + u
-                s = n % SLOTS
+            for u in range(OCTET):
+                n = octet * OCTET + u
+                b, s = divmod(n, SLOTS)
                 nc.tensor.matmul(
                     small[:, u, :], lhsT=queries_t[b][:, s * P : (s + 1) * P],
-                    rhs=keys_t[:, n * GROUP : (n + 1) * GROUP], start=False, stop=(u == QUAD - 1),
+                    rhs=keys_t[:, n * GROUP : (n + 1) * GROUP], start=False, stop=(u == OCTET - 1),
                 )
-            per_quad[quad] = {"small_scores": small}
+            per_octet[octet] = {"scores": small}
 
-        def copy_small(quad):
-            small = stats.tile([P, QUAD, GROUP], F32, name="small_copy", tag="small_copy")
-            nc.scalar.copy(out=small[:], in_=per_quad[quad].pop("small_scores"))
-            per_quad[quad]["small"] = small
+        def copy_small(octet):
+            small = stats.tile([P, OCTET, GROUP], F32, name="small_copy", tag="small_copy", bufs=3)
+            nc.scalar.copy(out=small[:], in_=per_octet[octet].pop("scores")[:])
+            per_octet[octet]["small"] = small
 
         def big_scores(n):
             b, s = divmod(n, SLOTS)
@@ -280,10 +274,10 @@ def tile_localgqattention_pb_t_kernel(tc, q_rot, k_rot, x, wv, out):
 
 
         def maxima(n):
-            if n % QUAD == 0 and n >= SLOTS:
-                quad = per_quad[n // QUAD]
-                quad["top_small"] = stats.tile([P, QUAD], F32, name="top_small", tag="top_small")
-                nc.vector.reduce_max(out=quad["top_small"][:], in_=quad["small"][:], axis=AX.X)
+            if n % OCTET == 0 and n >= SLOTS:
+                octet = per_octet[n // OCTET]
+                octet["top_small"] = stats.tile([P, OCTET], F32, name="top_small", tag="top_small", bufs=3)
+                nc.vector.reduce_max(out=octet["top_small"][:], in_=octet["small"][:], axis=AX.X)
             unit = per_unit[n]
             unit["top_big"] = stats.tile([P, 1], F32, name="top_big", tag="top_big")
             nc.vector.reduce_max(out=unit["top_big"][:], in_=unit["big"], axis=AX.X)
@@ -292,7 +286,7 @@ def tile_localgqattention_pb_t_kernel(tc, q_rot, k_rot, x, wv, out):
             unit = per_unit[n]
             bias = stats.tile([P, 1], F32, name="bias", tag="bias")
             if n >= SLOTS:
-                top_small = per_quad[n // QUAD]["top_small"][:, n % QUAD : n % QUAD + 1]
+                top_small = per_octet[n // OCTET]["top_small"][:, n % OCTET : n % OCTET + 1]
                 nc.gpsimd.tensor_scalar(
                     out=bias[:], in0=unit["top_big"][:], scalar1=top_small, scalar2=-scale,
                     op0=ALU.max, op1=ALU.mult,
@@ -317,7 +311,7 @@ def tile_localgqattention_pb_t_kernel(tc, q_rot, k_rot, x, wv, out):
             if b > 0:
                 nc.scalar.activation(
                     out=run_of_columns(e_shared[b % 2][:], s, 1),
-                    in_=per_quad[n // QUAD]["small"][:, n % QUAD, :].rearrange("q (p u e) -> q u p e", u=2, e=2),
+                    in_=per_octet[n // OCTET]["small"][:, n % OCTET, :].rearrange("q (p u e) -> q u p e", u=2, e=2),
                     func=ACT.Exp, bias=unit["bias"][:], scale=scale, accum_out=sums[b][1][:, s : s + 1],
                 )
 
@@ -406,12 +400,7 @@ def tile_localgqattention_pb_t_kernel(tc, q_rot, k_rot, x, wv, out):
                 sum_spans[n + 1] = (b, slice(s + 1 - span, s + 1))
 
         with tc.manual_schedule():
-            for i in range(4):
-                keep_busy(BLOCK)
-            copy_keys = prepare_keys(0)
-            for i in range(1):
-                keep_busy(BLOCK)
-            copy_keys()
+            prepare_keys(0)()
             copy_queries = prepare_queries(0, 0)
             grouped = {-1: [group_words(flip_rows(hidden_passes(wv_in[:])), HID_PASSES)]}
             copy_queries()
@@ -426,8 +415,8 @@ def tile_localgqattention_pb_t_kernel(tc, q_rot, k_rot, x, wv, out):
             for n in range(last_step + 1):
                 if n < N_UNITS:
                     exponentials(n)
-                if SLOTS <= n + 3 < N_UNITS and (n + 3) % QUAD == 0:
-                    copy_small((n + 3) // QUAD)
+                if SLOTS <= n + 3 < N_UNITS and (n + 3) % OCTET == 0:
+                    copy_small((n + 3) // OCTET)
                 if n in (2, 4):
                     clear_planes(nc.vector, n // 2)
                 if n + 2 < N_UNITS:
@@ -447,12 +436,10 @@ def tile_localgqattention_pb_t_kernel(tc, q_rot, k_rot, x, wv, out):
                     grouped[n - 1] = [group_words(words, len(flips[n - 1][i][1])) for i, words in enumerate(flipped.pop(n - 1))]
                 if n in flips:
                     flipped[n] = [flip_rows(passes) for key, passes, kind, bufs in flips[n]]
-                if SLOTS <= n + 4 < N_UNITS and n % QUAD == 0:
-                    small_scores((n + 4) // QUAD)
+                if SLOTS <= n + 4 < N_UNITS and (n + 4) % OCTET == 0:
+                    small_scores((n + 4) // OCTET)
                 if n + AHEAD < N_UNITS:
                     big_scores(n + AHEAD)
-                if n + AHEAD < SLOTS - 1:
-                    keep_busy(BLOCK - (n + AHEAD + 1) * GROUP)
                 for units in products.get(n, []):
                     multiply_values(units)
                 for call in prepares.get(n - 2, []):

import math

import concourse.mybir as mybir
from concourse.masks import make_identity

F32 = mybir.dt.float32
BF16 = mybir.dt.bfloat16
I32 = mybir.dt.int32
U32 = mybir.dt.uint32
U8 = mybir.dt.uint8
FP8X4 = mybir.dt.float8_e4m3fn_x4
ALU = mybir.AluOpType
ACT = mybir.ActivationFunctionType
AX = mybir.AxisListType

P = 128
T = 4096
HID = 1024
HEADS = 4
D = 128
BLOCK = 512
TILES = BLOCK // P
N_BLOCKS = T // BLOCK
GROUP = 32
SLOTS = BLOCK // GROUP
HALF = SLOTS // 2
N_UNITS = T // GROUP
QUAD = 4
OCTET = 8
HID_PASSES = HID // BLOCK
AHEAD = 4
RING = 6
MASKED = -1.0e30

FLOPS = 2 * T * HID * D + 2 * 2 * HEADS * D * BLOCK * (2 * BLOCK * (N_BLOCKS - 1) + BLOCK)


def tile_localgqattention_pb_t_kernel(tc, q_rot, k_rot, x, wv, out):
    nc = tc.nc
    scale = 1.0 / math.sqrt(D)

    q_rows = q_rot.rearrange("b t h d -> (b t h) d")
    k_rows = k_rot.rearrange("b t h d -> (b t) (h d)")
    x_rows = x.flatten_outer_dims()
    out_rows = out.flatten_outer_dims().rearrange("t (h d) -> (t h) d", h=HEADS)

    with (
        tc.tile_pool(name="keep", bufs=1) as keep,
        tc.tile_pool(name="queries", bufs=3) as queries,
        tc.tile_pool(name="packs", bufs=3) as packs,
        tc.tile_pool(name="stats", bufs=6) as stats,
        tc.tile_pool(name="quad_stats", bufs=3) as quad_stats,
        tc.tile_pool(name="results", bufs=8) as results,
        tc.psum_pool(name="bigs", bufs=4) as bigs,
        tc.psum_pool(name="smalls", bufs=1) as smalls,
        tc.psum_pool(name="work", bufs=3) as work,
    ):
        k_in = [keep.tile([P, TILES, D], BF16, name="k_in%d" % b) for b in range(N_BLOCKS)]
        q_in = [keep.tile([P, SLOTS, D], BF16, name="q_in%d" % b) for b in range(N_BLOCKS)]
        x_in = [keep.tile([P, 4, HID], BF16, name="x_in%d" % b) for b in range(N_BLOCKS)]
        wv_in = keep.tile([P, HID], BF16, name="wv_in")

        def load_keys(b):
            rows = slice(b * BLOCK, (b + 1) * BLOCK)
            nc.sync.dma_start(out=k_in[b][:], in_=k_rows[rows, :].rearrange("(c p) d -> p c d", p=P))

        def load_queries(b, half):
            first = (b * SLOTS + half * HALF) * P
            nc.sync.dma_start(
                out=q_in[b][:, half * HALF : (half + 1) * HALF, :],
                in_=q_rows[first : first + HALF * P, :].rearrange("(u p) d -> p u d", p=P),
            )

        def load_hidden(b, first, last):
            rows = x_rows[b * BLOCK : (b + 1) * BLOCK, :].rearrange("(p j) f -> p j f", j=4)
            nc.sync.dma_start(out=x_in[b][:, first:last, :], in_=rows[:, first:last, :])

        load_keys(0)
        load_queries(0, 0)
        nc.sync.dma_start(out=wv_in[:], in_=wv)
        load_queries(0, 1)
        load_hidden(0, 0, 2)
        load_hidden(0, 2, 4)
        load_keys(1)
        load_hidden(1, 0, 4)
        load_queries(1, 0)
        load_queries(1, 1)

        ident_bf = keep.tile([P, P], BF16, name="ident_bf")
        make_identity(nc, ident_bf[:])

        own_f32 = keep.tile([P, GROUP], F32, name="own_f32")
        nc.gpsimd.memset(own_f32[:], 0.0)
        nc.gpsimd.affine_select(
            out=own_f32[:], in_=own_f32[:], compare_op=ALU.is_ge, fill=MASKED,
            base=0, pattern=[[-HEADS, GROUP]], channel_multiplier=1,
        )
        far_f32 = keep.tile([P, GROUP], F32, name="far_f32")
        nc.gpsimd.memset(far_f32[:], 0.0)
        nc.gpsimd.affine_select(
            out=far_f32[:], in_=far_f32[:], compare_op=ALU.is_ge, fill=MASKED,
            base=HEADS - 1, pattern=[[HEADS, GROUP]], channel_multiplier=-1,
        )
        ident_f32 = keep.tile([P, P], F32, name="ident_f32")
        make_identity(nc, ident_f32[:])
        own_masks = keep.tile([P, OCTET, GROUP], BF16, name="own_masks")
        for u in range(OCTET):
            nc.vector.tensor_copy(out=own_masks[:, u, :], in_=own_f32[:])
        far_mask = keep.tile([P, GROUP], BF16, name="far_mask")
        nc.vector.tensor_copy(out=far_mask[:], in_=far_f32[:])

        e_main = [keep.tile([P, BLOCK], BF16, name="e_main%d" % i) for i in range(RING)]
        e_shared = [keep.tile([P, BLOCK], BF16, name="e_shared%d" % i) for i in range(2)]
        for e_tile in e_main:
            nc.vector.memset(e_tile[:].bitcast(I32), 0)

        keys_t = keep.tile([P, T], BF16, name="keys_t")
        v_codes = keep.tile([P, N_BLOCKS, D], U32, name="v_codes", align_bytes=64)
        v_scales = keep.tile([P, N_BLOCKS, D], U8, name="v_scales", align_bytes=64)
        nc.gpsimd.memset(v_scales[:].bitcast(I32), 0)
        part_planes = [keep.tile([P, 2 * SLOTS, D // 4], I32, name="part_planes%d" % i, align_bytes=64) for i in range(3)]
        diag_planes = [keep.tile([P, SLOTS, D // 4], I32, name="diag_planes%d" % i, align_bytes=64) for i in range(3)]

        def clear_planes(engine, i):
            for planes in (part_planes[i], diag_planes[i]):
                engine.memset(planes[:].rearrange("p s w -> p (s w)"), 0)

        clear_planes(nc.gpsimd, 0)

        def flip_rows(passes):
            flipped = work.tile([P, 4, P], F32, name="flipped", tag="work")
            for g, rows_bf16 in enumerate(passes):
                words = rows_bf16.bitcast(F32)
                for u in range(2):
                    nc.tensor.transpose(flipped[:, 2 * g + u, :], words[:, u * P : (u + 1) * P], ident_f32[:])
            return flipped

        def group_words(flipped, n_pass):
            grouped = packs.tile([P, n_pass * BLOCK], BF16, name="grouped", tag="grouped%d" % n_pass, align_bytes=64)
            nc.scalar.copy(
                out=grouped[:].bitcast(F32).rearrange("p (g r u) -> p g r u", g=n_pass, u=2),
                in_=flipped[:, : 2 * n_pass, :].rearrange("p (g u) r -> p g r u", u=2),
            )
            return grouped

        def quantise(grouped, n_pass, kind, bufs):
            codes = packs.tile([P, n_pass * P], U32, name="codes", tag=kind + "_codes", bufs=bufs, align_bytes=64)
            planes = packs.tile([P, n_pass * P], U8, name="planes", tag=kind + "_scales", bufs=bufs, align_bytes=64)
            nc.vector.quantize_mx(out=codes[:].bitcast(FP8X4), scales=planes[:], in_=grouped[:])
            return codes, planes

        def multiply(acc, products):
            for g, (l_codes, l_scales, r_codes, r_scales) in enumerate(products):
                nc.tensor.matmul_mx(
                    out=acc, lhsT=l_codes.bitcast(FP8X4), lhsT_scale=l_scales,
                    rhs=r_codes.bitcast(FP8X4), rhs_scale=r_scales,
                    start=(g == 0), stop=(g == len(products) - 1),
                )

        queries_t = {}
        packed = {}

        def prepare_keys(b):
            k_flip = work.tile([P, TILES, P], BF16, name="k_flip", tag="work")
            for c in range(TILES):
                nc.tensor.transpose(k_flip[:, c, :], k_in[b][:, c, :], ident_bf[:])
            return lambda: nc.vector.tensor_copy(
                out=keys_t[:, b * BLOCK : (b + 1) * BLOCK], in_=k_flip[:].rearrange("p c r -> p (c r)")
            )

        def prepare_queries(b, half):
            if half == 0:
                queries_t[b] = queries.tile([P, BLOCK * HEADS], BF16, name="q_t", tag="q_t")
            q_flip = work.tile([P, HALF, P], BF16, name="q_flip", tag="work")
            for u in range(HALF):
                nc.tensor.transpose(q_flip[:, u, :], q_in[b][:, half * HALF + u, :], ident_bf[:])
            return lambda: nc.vector.tensor_copy(
                out=queries_t[b][:, half * HALF * P : (half + 1) * HALF * P],
                in_=q_flip[:].rearrange("p u r -> p (u r)"),
            )

        def hidden_passes(rows_bf16):
            return [rows_bf16[:, g * BLOCK : (g + 1) * BLOCK] for g in range(HID_PASSES)]

        stage = {}

        def project_values(b):
            v_acc = work.tile([P, 4, D], F32, name="v_acc", tag="work")
            wv_codes, wv_scales = packed[("wv",)]
            for slot in range(4):
                x_codes, x_scales = packed.pop(("x", b, slot))
                multiply(v_acc[:, slot, :], [
                    (x_codes[:, g * P : (g + 1) * P], x_scales[:, g * P : (g + 1) * P],
                     wv_codes[:, g * P : (g + 1) * P], wv_scales[:, g * P : (g + 1) * P])
                    for g in range(HID_PASSES)
                ])

            def copy_values():
                v_grouped = packs.tile([P, D, 4], BF16, name="v_grouped", tag="v_grouped", bufs=2, align_bytes=64)
                nc.vector.tensor_copy(out=v_grouped[:], in_=v_acc[:].rearrange("p s d -> p d s"))
                stage[b] = v_grouped

            return copy_values

        def quantise_values(b):
            nc.vector.quantize_mx(
                out=v_codes[:, b, :].bitcast(FP8X4), scales=v_scales[:, b, :],
                in_=stage.pop(b)[:].rearrange("p d s -> p (d s)"),
            )

        def spread_scales(b):
            source = v_scales[:, b, :].bitcast(I32)
            for s in range(SLOTS):
                row = 32 * (s // 4) + s % 4
                first = s + 1 if b > 0 else SLOTS
                last = s + 1 + SLOTS if b + 1 < N_BLOCKS else SLOTS
                if first < last:
                    nc.sync.dma_start(
                        out=part_planes[b % 3][row : row + 1, first:last, :],
                        in_=source[row : row + 1].unsqueeze(1).to_broadcast([1, last - first, D // 4]),
                    )
                if b > 0:
                    nc.sync.dma_start(out=diag_planes[b % 3][row : row + 1, s, :], in_=source[row : row + 1])

        per_octet = {}
        products_done = {}
        per_unit = {}
        sums = {}

        def run_of_columns(tile_ap, first, n_slots):
            halves = tile_ap.rearrange("q (u w) -> q u w", u=2)
            return halves[:, :, first * GROUP // 2 : (first + n_slots) * GROUP // 2].rearrange("q u (p e) -> q u p e", e=2)

        def small_scores(octet):
            small = smalls.tile([P, OCTET, GROUP], F32, name="small", tag="small")
            nc.tensor.matmul(
                small[:].rearrange("p u k -> p (u k)"), lhsT=ident_bf[:],
                rhs=own_masks[:].rearrange("p u k -> p (u k)"), start=True, stop=False,
            )
            for u in range(OCTET):
                n = octet * OCTET + u
                b, s = divmod(n, SLOTS)
                nc.tensor.matmul(
                    small[:, u, :], lhsT=queries_t[b][:, s * P : (s + 1) * P],
                    rhs=keys_t[:, n * GROUP : (n + 1) * GROUP], start=False, stop=(u == OCTET - 1),
                )
            per_octet[octet] = {"scores": small}

        def copy_small(octet):
            small = stats.tile([P, OCTET, GROUP], F32, name="small_copy", tag="small_copy", bufs=3)
            nc.scalar.copy(out=small[:], in_=per_octet[octet].pop("scores")[:])
            per_octet[octet]["small"] = small

        def big_scores(n):
            b, s = divmod(n, SLOTS)
            big = bigs.tile([P, BLOCK], F32, name="big", tag="big")
            q_ap = queries_t[b][:, s * P : (s + 1) * P]
            slot = slice(s * GROUP, (s + 1) * GROUP)
            if b == 0:
                nc.tensor.matmul(big[:, : slot.stop], lhsT=q_ap, rhs=keys_t[:, : slot.stop], start=True, stop=False)
                nc.tensor.matmul(big[:, slot], lhsT=ident_bf[:], rhs=own_masks[:, 0, :], start=False, stop=True)
                per_unit[n] = {"big": big[:, : slot.stop]}
                return
            if s > 0:
                nc.tensor.matmul(
                    big[:, : slot.start], lhsT=q_ap, rhs=keys_t[:, b * BLOCK : b * BLOCK + slot.start],
                    start=True, stop=True,
                )
            nc.tensor.matmul(
                big[:, slot.start :], lhsT=q_ap, rhs=keys_t[:, (n - SLOTS) * GROUP : b * BLOCK], start=True, stop=False,
            )
            nc.tensor.matmul(big[:, slot], lhsT=ident_bf[:], rhs=far_mask[:], start=False, stop=True)
            per_unit[n] = {"big": big[:]}


        def maxima(n):
            if n % OCTET == 0 and n >= SLOTS:
                octet = per_octet[n // OCTET]
                octet["top_small"] = stats.tile([P, OCTET], F32, name="top_small", tag="top_small", bufs=3)
                nc.vector.reduce_max(out=octet["top_small"][:], in_=octet["small"][:], axis=AX.X)
            unit = per_unit[n]
            unit["top_big"] = stats.tile([P, 1], F32, name="top_big", tag="top_big")
            nc.vector.reduce_max(out=unit["top_big"][:], in_=unit["big"], axis=AX.X)

        def make_bias(n):
            unit = per_unit[n]
            bias = stats.tile([P, 1], F32, name="bias", tag="bias")
            if n >= SLOTS:
                top_small = per_octet[n // OCTET]["top_small"][:, n % OCTET : n % OCTET + 1]
                nc.gpsimd.tensor_scalar(
                    out=bias[:], in0=unit["top_big"][:], scalar1=top_small, scalar2=-scale,
                    op0=ALU.max, op1=ALU.mult,
                )
            else:
                nc.gpsimd.tensor_scalar_mul(out=bias[:], in0=unit["top_big"][:], scalar1=-scale)
            unit["bias"] = bias

        def exponentials(n):
            b, s = divmod(n, SLOTS)
            unit = per_unit.pop(n)
            if s == 0:
                sums[b] = [quad_stats.tile([P, SLOTS], F32, name="sum", tag="sum%d" % i) for i in range(4)]
                if b == 0:
                    nc.vector.memset(sums[b][1][:], 0.0)
            n_slots = SLOTS if b > 0 else s + 1
            nc.scalar.activation(
                out=run_of_columns(e_main[n % RING][:], 0, n_slots),
                in_=unit["big"].rearrange("q (p u e) -> q u p e", u=2, e=2),
                func=ACT.Exp, bias=unit["bias"][:], scale=scale, accum_out=sums[b][0][:, s : s + 1],
            )
            if b > 0:
                nc.scalar.activation(
                    out=run_of_columns(e_shared[b % 2][:], s, 1),
                    in_=per_octet[n // OCTET]["small"][:, n % OCTET, :].rearrange("q (p u e) -> q u p e", u=2, e=2),
                    func=ACT.Exp, bias=unit["bias"][:], scale=scale, accum_out=sums[b][1][:, s : s + 1],
                )

        def add_sums(b, units):
            sum_big, sum_small, total, inverse = [s[:, units] for s in sums[b]]
            nc.gpsimd.tensor_tensor(out=total, in0=sum_big, in1=sum_small, op=ALU.add)

        def invert_sums(b, units):
            sum_big, sum_small, total, inverse = [s[:, units] for s in sums[b]]
            nc.vector.reciprocal(out=inverse, in_=total)

        def multiply_values(units):
            o_acc = work.tile([P, len(units), D], F32, name="o_acc", tag="work")
            for u, n in enumerate(units):
                b, s = divmod(n, SLOTS)
                codes, planes = packed[("main", n // 2)]
                g = n % 2
                main = (codes[:, g * P : (g + 1) * P], planes[:, g * P : (g + 1) * P])
                if b == 0:
                    products = [main + (v_codes[:, 0, :], v_scales[:, 0, :])]
                else:
                    products = [main + (v_codes[:, b - 1, :], part_planes[(b - 1) % 3][:, SLOTS + s, :].bitcast(U8))]
                    if s > 0:
                        products.append(main + (v_codes[:, b, :], part_planes[b % 3][:, s, :].bitcast(U8)))
                    codes, planes = packed[("shared", flush_of(n))]
                    products.append((codes[:], planes[:], v_codes[:, b, :], diag_planes[b % 3][:, s, :].bitcast(U8)))
                multiply(o_acc[:, u, :], products)
            products_done[units.start] = o_acc

        def divide_and_store(units):
            result = results.tile([P, len(units), D], F32, name="result", tag="result")
            b, s = divmod(units.start, SLOTS)
            nc.vector.tensor_tensor(
                out=result[:], in0=products_done.pop(units.start)[:],
                in1=sums[b][3][:, s : s + len(units)].unsqueeze(2).to_broadcast([P, len(units), D]), op=ALU.mult,
            )
            nc.sync.dma_start(
                out=out_rows[units.start * P : units.stop * P, :].rearrange("(u p) d -> p u d", p=P), in_=result[:]
            )

        def flush_of(n):
            b, s = divmod(n, SLOTS)
            last = SLOTS - 1 if b + 1 < N_BLOCKS else max(s // QUAD * QUAD + QUAD - 1, SLOTS // 2 - 1)
            return b * SLOTS + last

        flips = {}
        flips[-1] = [(("wv",), hidden_passes(wv_in[:]), "wv", 1)]
        for pair in range(N_UNITS // 2):
            flips[2 * pair + 2] = [(("main", pair), [e_main[n % RING][:] for n in (2 * pair, 2 * pair + 1)], "main", 16)]
        for b in range(N_BLOCKS):
            for slot in range(4):
                step = 2 * (4 * b + slot) + 1 if b < 2 else (b - 1) * SLOTS + (3, 5, 7, 11)[slot]
                flips[step] = [(("x", b, slot), hidden_passes(x_in[b][:, slot, :]), "x", 8)]
        for n in sorted(set([flush_of(n) for n in range(SLOTS, N_UNITS)])):
            step = n + 2 if n + 1 < N_UNITS else n + 1
            flips.setdefault(step, []).append((("shared", n), [e_shared[n // SLOTS % 2][:]], "shared", 3))

        products = {}
        step = 0
        for first in range(0, N_UNITS, QUAD):
            apart = QUAD if first < N_UNITS - 2 * SLOTS else 2
            ready = flush_of(first) + 5 if first >= SLOTS else SLOTS
            if first >= N_UNITS - SLOTS:
                ready = N_UNITS + QUAD - (N_UNITS - QUAD - first) // 2
            step = max(ready, step + apart)
            products[step] = [range(first, first + QUAD)]
        products[step] = [range(first, first + QUAD // 2), range(first + QUAD // 2, first + QUAD)]
        last_step = step + 2

        prepares = {10: [(project_values, 0)], SLOTS + 2: [(project_values, 1)]}
        for b in range(1, N_BLOCKS):
            before = (b - 1) * SLOTS
            prepares[before + 6] = [(prepare_keys, b)]
            prepares[before + (8 if b == 1 else 10)] = [(prepare_queries, b, 0)]
            if b == 1:
                prepares[before + 14] = [(prepare_queries, b, 1)]
            else:
                prepares[before + 14] = [(project_values, b)]
                prepares[before + SLOTS + 2] = [(prepare_queries, b, 1)]

        sum_spans = {}
        for n in range(N_UNITS):
            b, s = divmod(n, SLOTS)
            span = SLOTS if b + 1 < N_BLOCKS else QUAD
            if (s + 1) % span == 0:
                sum_spans[n + 1] = (b, slice(s + 1 - span, s + 1))

        with tc.manual_schedule():
            prepare_keys(0)()
            copy_queries = prepare_queries(0, 0)
            grouped = {-1: [group_words(flip_rows(hidden_passes(wv_in[:])), HID_PASSES)]}
            copy_queries()
            for n in range(AHEAD):
                big_scores(n)
            for n in range(2):
                maxima(n)
                make_bias(n)
            prepare_queries(0, 1)()
            flipped = {}
            copies = []
            for n in range(last_step + 1):
                if n < N_UNITS:
                    exponentials(n)
                if SLOTS <= n + 3 < N_UNITS and (n + 3) % OCTET == 0:
                    copy_small((n + 3) // OCTET)
                if n in (2, 4):
                    clear_planes(nc.vector, n // 2)
                if n + 2 < N_UNITS:
                    maxima(n + 2)
                    make_bias(n + 2)
                for units in products.get(n - 2, []):
                    divide_and_store(units)
                for copy in copies:
                    copy()
                if n in sum_spans:
                    add_sums(*sum_spans[n])
                for key, passes, kind, bufs in flips.get(n - 2, []):
                    packed[key] = quantise(grouped[n - 2].pop(0), len(passes), kind, bufs)
                if n - 1 in sum_spans:
                    invert_sums(*sum_spans[n - 1])
                if n - 1 in flipped:
                    grouped[n - 1] = [group_words(words, len(flips[n - 1][i][1])) for i, words in enumerate(flipped.pop(n - 1))]
                if n in flips:
                    flipped[n] = [flip_rows(passes) for key, passes, kind, bufs in flips[n]]
                if SLOTS <= n + 4 < N_UNITS and (n + 4) % OCTET == 0:
                    small_scores((n + 4) // OCTET)
                if n + AHEAD < N_UNITS:
                    big_scores(n + AHEAD)
                for units in products.get(n, []):
                    multiply_values(units)
                for call in prepares.get(n - 2, []):
                    if call[0] is project_values:
                        quantise_values(call[1])
                        spread_scales(call[1])
                copies = [call[0](*call[1:]) for call in prepares.get(n, [])]
                b, s = divmod(n, SLOTS)
                if b + 2 < N_BLOCKS and s == 0:
                    load_hidden(b + 2, 0, 4)
                    load_keys(b + 2)
                    load_queries(b + 2, 0)
                    load_queries(b + 2, 1)
